import numpy as np
import ml_dtypes


def mxq(x, axis, fmt="e4m3"):
    dtype, down = {"e4m3": (ml_dtypes.float8_e4m3fn, 7), "e5m2": (ml_dtypes.float8_e5m2, 14)}[fmt]
    v = np.moveaxis(np.asarray(x, np.float32).astype(ml_dtypes.bfloat16).astype(np.float64), axis, -1)
    blocks = v.reshape(v.shape[:-1] + (-1, 32))
    amax = np.abs(blocks).max(-1, keepdims=True)
    byte = np.maximum(np.where(amax > 0, np.frexp(amax)[1] - 1 + 127, 0) - down, 1)
    scale = np.exp2(byte - 127.0)
    codes = (blocks / scale).astype(np.float32).astype(dtype).astype(np.float64)
    return np.moveaxis((codes * scale).reshape(v.shape), -1, axis)


WIDE = False


def mx_kscale(k):
    if not WIDE:
        return np.ones(k)
    levels = np.array([10, -10, 5, -5, 0])
    a = np.random.permutation(np.resize(levels, k // 512 * 4)).reshape(k // 512, 4)
    idx = np.arange(k)
    return np.exp2(a[idx // 512, idx % 128 // 32])


BF16 = ml_dtypes.bfloat16


def bf(x):
    return np.asarray(x, np.float32).astype(BF16)


def f64(x):
    return np.asarray(x).astype(np.float64)


E2M1 = np.array([0.0, 0.5, 1.0, 1.5, 2.0, 3.0, 4.0, 6.0, -0.0, -0.5, -1.0, -1.5, -2.0, -3.0, -4.0, -6.0])


def pack_weight(w, fmt):
    k, n = w.shape
    w = f64(bf(w)).reshape(k // 32, 32, n)
    amax = np.abs(w).max(1)
    if fmt == "e4m3":
        byte = np.frexp(amax)[1] - 1 + 127 - 7
    else:
        mant, ex = np.frexp(amax / 6.0)
        byte = np.where(mant > 0.5, ex, ex - 1) + 127
    byte = np.clip(np.where(amax > 0, byte, 1), 1, 254)
    scaled = (w * np.exp2(127.0 - byte)[:, None, :]).reshape(k, n).astype(np.float32)
    by_word = np.ascontiguousarray(scaled.reshape(k // 512, 128, 4, n).transpose(0, 1, 3, 2))
    if fmt == "e4m3":
        words = by_word.astype(ml_dtypes.float8_e4m3fn).view(np.uint8)
    else:
        c = by_word.astype(ml_dtypes.float4_e2m1fn).view(np.uint8) & 0xF
        words = c[..., 0::2] | (c[..., 1::2] << 4)
    return np.ascontiguousarray(words), np.ascontiguousarray(byte.astype(np.uint8).reshape(k // 512, 16, n))


def unpack_weight(words, scales, fmt):
    g, p, n, _ = words.shape
    if fmt == "e4m3":
        vals = np.ascontiguousarray(words).view(ml_dtypes.float8_e4m3fn).astype(np.float64)
    else:
        nib = np.empty((g, p, n, 4), np.uint8)
        nib[..., 0::2] = words & 0xF
        nib[..., 1::2] = words >> 4
        vals = E2M1[nib]
    vals = vals * np.repeat(np.exp2(scales.astype(np.float64) - 127.0), 8, axis=1)[..., None]
    return vals.transpose(0, 1, 3, 2).reshape(g * 512, n)


B, S, D, F, R = 2, 128, 16384, 512, 128
SCALING = 2.0
FMT = "e4m3"


def silu(v):
    return v / (1.0 + np.exp(-v))


def setup_inputs():
    s = mx_kscale(D)
    x = bf(np.random.standard_normal((B, S, D)) * s)
    w1 = np.random.standard_normal((F, D)) / np.sqrt(D) / s
    w3 = np.random.standard_normal((F, D)) / np.sqrt(D) / s
    xa1 = bf(np.random.standard_normal((B, S, R)))
    xa3 = bf(np.random.standard_normal((B, S, R)))
    lora_B1 = bf(np.random.standard_normal((F, R)) * 0.25 / np.sqrt(R))
    lora_B3 = bf(np.random.standard_normal((F, R)) * 0.25 / np.sqrt(R))
    lora_A2 = np.random.standard_normal((R, F)) / np.sqrt(F)
    w1_words, w1_scales = pack_weight(np.ascontiguousarray(w1.T), FMT)
    w3_words, w3_scales = pack_weight(np.ascontiguousarray(w3.T), FMT)
    lora_A2_words, lora_A2_scales = pack_weight(np.ascontiguousarray(lora_A2.T), FMT)
    return {
        "x": x,
        "w1_words": w1_words,
        "w1_scales": w1_scales,
        "w3_words": w3_words,
        "w3_scales": w3_scales,
        "xa1": xa1,
        "xa3": xa3,
        "lora_B1": lora_B1,
        "lora_B3": lora_B3,
        "lora_A2_words": lora_A2_words,
        "lora_A2_scales": lora_A2_scales,
    }


def reference(x, w1_words, w1_scales, w3_words, w3_scales, xa1, xa3, lora_B1, lora_B3, lora_A2_words, lora_A2_scales):
    xq = mxq(f64(x), 2, "e4m3")
    h1 = (xq @ unpack_weight(w1_words, w1_scales, FMT)) + (f64(xa1) @ f64(lora_B1).T) * SCALING
    h3 = (xq @ unpack_weight(w3_words, w3_scales, FMT)) + (f64(xa3) @ f64(lora_B3).T) * SCALING
    g = silu(h1) * h3
    ga2 = mxq(g, 2, "e4m3") @ unpack_weight(lora_A2_words, lora_A2_scales, FMT)
    return g, ga2

@@ -1,0 +1,359 @@
+from contextlib import ExitStack
+
+import concourse.mybir as mybir
+from concourse.masks import make_identity
+
+F32 = mybir.dt.float32
+BF16 = mybir.dt.bfloat16
+I32 = mybir.dt.int32
+U32 = mybir.dt.uint32
+U8 = mybir.dt.uint8
+FP8X4 = mybir.dt.float8_e4m3fn_x4
+SILU = mybir.ActivationFunctionType.Silu
+
+P = 128
+TOKEN_TILES = 2
+D = 16384
+F = 512
+R = 128
+PACK = 4
+K_PASS = P * PACK
+GROUPS = D // K_PASS
+ROUND_GROUPS = 4
+ROUNDS = GROUPS // ROUND_GROUPS
+ROUND_COLS = K_PASS * ROUND_GROUPS
+PIECE_GROUPS = 2
+PIECES = ROUND_GROUPS // PIECE_GROUPS
+BANK_GROUPS = 2
+PLANE_GROUPS = 8
+LORA_STEP = 3
+LORA_BLOCKS = TOKEN_TILES + F // P
+LORA_SCALING = 2.0
+
+FLOPS = 2 * TOKEN_TILES * P * (2 * D * F + 2 * R * F + F * R)
+
+
+def tile_feedforward_pa_k_kernel(
+    tc,
+    x,
+    w1_words,
+    w1_scales,
+    w3_words,
+    w3_scales,
+    xa1,
+    xa3,
+    lora_B1,
+    lora_B3,
+    lora_A2_words,
+    lora_A2_scales,
+    out_0,
+    out_1,
+):
+    nc = tc.nc
+    branches = ("w1", "w3")
+    words_of = {"w1": w1_words, "w3": w3_words}
+    scales_of = {"w1": w1_scales, "w3": w3_scales}
+    lora_inputs = {"w1": (xa1, lora_B1), "w3": (xa3, lora_B3)}
+
+    with ExitStack() as ctx:
+        keep = ctx.enter_context(tc.tile_pool(name="keep", bufs=1))
+        x_pool = ctx.enter_context(tc.tile_pool(name="x_pool", bufs=4 * TOKEN_TILES))
+        sorted_pool = ctx.enter_context(tc.tile_pool(name="sorted_pool", bufs=3))
+        grouped_pool = ctx.enter_context(tc.tile_pool(name="grouped_pool", bufs=3))
+        codes_pool = ctx.enter_context(tc.tile_pool(name="codes_pool", bufs=6))
+        w_pool = ctx.enter_context(tc.tile_pool(name="w_pool", bufs=4 * 2 * PIECES))
+        turn_psum = ctx.enter_context(tc.psum_pool(name="turn_psum", bufs=4))
+        acc_psum = ctx.enter_context(tc.psum_pool(name="acc_psum", bufs=1))
+        ctx.enter_context(tc.manual_schedule())
+
+        x_raw = {}
+        x_sorted = {}
+        x_grouped = {}
+        x_codes = {}
+        x_scales = {}
+        w_pieces = {}
+        planes = {}
+        lora_in = {}
+        lora_turned = {}
+        lora_term = {}
+        acc = {}
+        gate = {}
+
+        def load_x(unit):
+            rnd, tt = divmod(unit, TOKEN_TILES)
+            raw = x_pool.tile([P, ROUND_COLS], BF16, name="x_raw", tag="x_raw")
+            nc.sync.dma_start(out=raw[:], in_=x[tt, :, rnd * ROUND_COLS : (rnd + 1) * ROUND_COLS])
+            x_raw[unit] = raw
+
+        def load_w(rnd, branch):
+            last = rnd == ROUNDS - 1 and branch == branches[-1]
+            split = PIECE_GROUPS if last else 1
+            for piece in range(PIECES):
+                first = rnd * ROUND_GROUPS + piece * PIECE_GROUPS
+                w_piece = w_pool.tile(
+                    [P, PIECE_GROUPS, F], U32, name="w_piece", tag="w_piece", align_bytes=64
+                )
+                count = PIECE_GROUPS // split
+                for i in range(split):
+                    nc.sync.dma_start(
+                        out=w_piece[:, i * count : (i + 1) * count, :].bitcast(I32),
+                        in_=words_of[branch][first + i * count : first + (i + 1) * count]
+                        .rearrange("g p n t -> p g (n t)")
+                        .bitcast(I32),
+                    )
+                w_pieces[(rnd, branch, piece)] = w_piece
+
+        def load_scale_rows(branch, chunk):
+            source = scales_of[branch].bitcast(F32)[
+                chunk * PLANE_GROUPS : (chunk + 1) * PLANE_GROUPS
+            ]
+            for r in range(4):
+                nc.gpsimd.dma_start(
+                    out=planes[(branch, chunk)][4 * chunk + r : P : 32, :, :].bitcast(F32),
+                    in_=source[:, r : 16 : 4, :].rearrange("g q n -> q g n"),
+                )
+
+        def zero_planes(chunk):
+            for branch in branches:
+                planes[(branch, chunk)] = keep.tile(
+                    [P, PLANE_GROUPS, F], U8, name="planes_%s_%d" % (branch, chunk), align_bytes=64
+                )
+                nc.vector.memset(planes[(branch, chunk)][:].bitcast(I32), 0)
+
+        def load_lora():
+            for branch in branches:
+                xa, lora_b = lora_inputs[branch]
+                lora_in[branch] = keep.tile([P, LORA_BLOCKS, R], BF16, name="lora_in_" + branch)
+                nc.sync.dma_start(
+                    out=lora_in[branch][:, 0:TOKEN_TILES, :], in_=xa.rearrange("b s r -> s b r")
+                )
+                nc.sync.dma_start(
+                    out=lora_in[branch][:, TOKEN_TILES:, :],
+                    in_=lora_b.rearrange("(p t) r -> p t r", t=PACK),
+                )
+
+        def sort_x(unit):
+            x_sorted[unit] = sorted_pool.tile(
+                [P, ROUND_GROUPS, 2, P], F32, name="sorted_words", tag="sorted_words"
+            )
+            nc.vector.tensor_copy(
+                out=x_sorted[unit][:],
+                in_=x_raw[unit][:].bitcast(F32).rearrange("s (g p u) -> s g u p", g=ROUND_GROUPS, u=2),
+            )
+
+        def turn_x(unit):
+            grouped = grouped_pool.tile(
+                [P, ROUND_GROUPS, P, PACK], BF16, name="grouped", tag="grouped", align_bytes=64
+            )
+            grouped_words = grouped[:].bitcast(F32)
+            for bank in range(ROUND_GROUPS // BANK_GROUPS):
+                turned = turn_psum.tile([P, BANK_GROUPS, 2, P], F32, name="turned", tag="turn")
+                for i in range(BANK_GROUPS):
+                    for u in range(2):
+                        nc.tensor.transpose(
+                            turned[:, i, u, :],
+                            x_sorted[unit][:, bank * BANK_GROUPS + i, u, :],
+                            identity_f32[:],
+                        )
+                copy_out = nc.scalar.copy if bank % 2 == 0 else nc.vector.tensor_copy
+                copy_out(
+                    out=grouped_words[:, bank * BANK_GROUPS : (bank + 1) * BANK_GROUPS, :, :],
+                    in_=turned[:].rearrange("p g u t -> p g t u"),
+                )
+            x_grouped[unit] = grouped
+
+        def quantise_x(unit):
+            codes = codes_pool.tile(
+                [P, ROUND_GROUPS, P], U32, name="x_codes", tag="x_codes", align_bytes=64
+            )
+            scales = codes_pool.tile(
+                [P, ROUND_GROUPS, P], U8, name="x_scales", tag="x_scales", align_bytes=64
+            )
+            nc.vector.quantize_mx(
+                out=codes[:].rearrange("p g t -> p (g t)").bitcast(FP8X4),
+                scales=scales[:].rearrange("p g t -> p (g t)"),
+                in_=x_grouped[unit][:].rearrange("p g t j -> p (g t j)"),
+            )
+            x_codes[unit] = codes
+            x_scales[unit] = scales
+
+        def multiply(rnd, branch):
+            for piece in range(PIECES):
+                for tt in range(TOKEN_TILES):
+                    for i in range(PIECE_GROUPS):
+                        local = piece * PIECE_GROUPS + i
+                        group = rnd * ROUND_GROUPS + local
+                        chunk, in_plane = divmod(group, PLANE_GROUPS)
+                        nc.tensor.matmul_mx(
+                            out=acc[(branch, tt)][:],
+                            lhsT=x_codes[TOKEN_TILES * rnd + tt][:, local, :].bitcast(FP8X4),
+                            lhsT_scale=x_scales[TOKEN_TILES * rnd + tt][:, local, :],
+                            rhs=w_pieces[(rnd, branch, piece)][:, i, :].bitcast(FP8X4),
+                            rhs_scale=planes[(branch, chunk)][4 * chunk : P, in_plane, :],
+                            start=(group == 0),
+                            stop=(group == GROUPS - 1),
+                        )
+
+        def transpose_lora():
+            for branch in branches:
+                turned = turn_psum.tile([P, LORA_BLOCKS, P], BF16, name="lora_ps", tag="turn")
+                for i in range(LORA_BLOCKS):
+                    nc.tensor.transpose(turned[:, i, :], lora_in[branch][:, i, :], identity_bf16[:])
+                lora_turned[branch] = keep.tile(
+                    [P, LORA_BLOCKS, P], BF16, name="lora_turned_" + branch
+                )
+                nc.scalar.copy(out=lora_turned[branch][:], in_=turned[:])
+
+        def multiply_lora():
+            for branch in branches:
+                for tt in range(TOKEN_TILES):
+                    product = turn_psum.tile([P, PACK, P], F32, name="product", tag="turn")
+                    nc.tensor.matmul(
+                        out=product[:].rearrange("s t p -> s (t p)"),
+                        lhsT=lora_turned[branch][:, tt, :],
+                        rhs=lora_turned[branch][:, TOKEN_TILES:, :].rearrange("r t p -> r (t p)"),
+                        start=True,
+                        stop=True,
+                    )
+                    lora_term[(branch, tt)] = keep.tile(
+                        [P, PACK, P], F32, name="lora_term_%s_%d" % (branch, tt)
+                    )
+                    nc.scalar.mul(
+                        out=lora_term[(branch, tt)][:],
+                        in_=product[:],
+                        mul=LORA_SCALING,
+                    )
+
+        zero_planes(0)
+        identity_f32 = keep.tile([P, P], F32, name="identity_f32")
+        make_identity(nc, identity_f32[:])
+        for branch in branches:
+            load_scale_rows(branch, 0)
+        identity_bf16 = keep.tile([P, P], BF16, name="identity_bf16")
+        make_identity(nc, identity_bf16[:])
+        table_in = keep.tile([P, 1], F32, name="table_in")
+        table_out = keep.tile([P, 1], F32, name="table_out")
+        nc.vector.memset(table_in[:], 0.0)
+        nc.scalar.activation(out=table_out[:], in_=table_in[:], func=SILU)
+        for branch in branches:
+            for tt in range(TOKEN_TILES):
+                acc[(branch, tt)] = acc_psum.tile([P, F], F32, name="acc_%s_%d" % (branch, tt))
+
+        for unit in range(TOKEN_TILES):
+            load_x(unit)
+        zero_planes(1)
+        for branch in branches:
+            load_scale_rows(branch, 1)
+        load_x(2)
+        load_w(0, "w1")
+        load_x(3)
+        load_x(4)
+        load_w(0, "w3")
+        sort_x(0)
+        for unit in range(TOKEN_TILES):
+            sort_x(unit + 1)
+            turn_x(unit)
+            quantise_x(unit)
+
+        a2_words = keep.tile([P, R], U32, name="a2_words", align_bytes=64)
+        a2_plane = keep.tile([P, R], U8, name="a2_plane", align_bytes=64)
+
+        for step in range(2 * ROUNDS):
+            rnd, odd = divmod(step, 2)
+            if step + 5 < 2 * ROUNDS:
+                load_x(step + 5)
+            if rnd + 1 < ROUNDS:
+                load_w(rnd + 1, branches[odd])
+            if step == 0:
+                load_lora()
+            if step == LORA_STEP:
+                transpose_lora()
+            if step + 3 < 2 * ROUNDS:
+                sort_x(step + 3)
+            if step + 2 < 2 * ROUNDS:
+                turn_x(step + 2)
+                quantise_x(step + 2)
+            if step == 1:
+                for chunk in range(2, GROUPS // PLANE_GROUPS):
+                    zero_planes(chunk)
+                    for branch in branches:
+                        load_scale_rows(branch, chunk)
+                nc.vector.memset(a2_plane[:].bitcast(I32), 0)
+                nc.gpsimd.dma_start(
+                    out=a2_words[:].bitcast(F32),
+                    in_=lora_A2_words[0].rearrange("p n t -> p (n t)").bitcast(F32),
+                )
+                for r in range(4):
+                    nc.gpsimd.dma_start(
+                        out=a2_plane[r : P : 32, :].bitcast(F32),
+                        in_=lora_A2_scales[0].bitcast(F32)[r : 16 : 4, :],
+                    )
+            if step == LORA_STEP:
+                multiply_lora()
+            multiply(rnd, branches[odd])
+            if step == 2 * ROUNDS - 2:
+                for tt in range(TOKEN_TILES):
+                    h1 = keep.tile([P, PACK, P], F32, name="h1_%d" % tt)
+                    nc.vector.tensor_add(
+                        out=h1[:],
+                        in0=acc[("w1", tt)][:].rearrange("s (p t) -> s t p", t=PACK),
+                        in1=lora_term[("w1", tt)][:],
+                    )
+                    gate[tt] = keep.tile([P, PACK, P], F32, name="gate_%d" % tt)
+                    nc.scalar.activation(out=gate[tt][:], in_=h1[:], func=SILU)
+
+        h3 = {}
+        g_sorted = {}
+        for tt in range(TOKEN_TILES):
+            h3[tt] = keep.tile([P, PACK, P], F32, name="h3_%d" % tt)
+            nc.vector.tensor_add(
+                out=h3[tt][:],
+                in0=acc[("w3", tt)][:].rearrange("s (p t) -> s t p", t=PACK),
+                in1=lora_term[("w3", tt)][:],
+            )
+        for tt in range(TOKEN_TILES):
+            g_sorted[tt] = keep.tile([P, PACK, P], BF16, name="g_sorted_%d" % tt)
+            nc.vector.tensor_mul(out=g_sorted[tt][:], in0=h3[tt][:], in1=gate[tt][:])
+        g_grouped = {}
+        for tt in range(TOKEN_TILES):
+            g_turned = turn_psum.tile([P, PACK, P], BF16, name="g_turned", tag="turn")
+            for t in range(PACK):
+                nc.tensor.transpose(g_turned[:, t, :], g_sorted[tt][:, t, :], identity_bf16[:])
+            g_grouped[tt] = keep.tile([P, P, PACK], BF16, name="g_grouped_%d" % tt, align_bytes=64)
+            nc.scalar.copy(out=g_grouped[tt][:], in_=g_turned[:].rearrange("p t s -> p s t"))
+
+        def store_g(tt):
+            g = keep.tile([P, F], F32, name="g_%d" % tt)
+            nc.vector.tensor_mul(
+                out=g[:].rearrange("s (p t) -> s p t", t=PACK),
+                in0=h3[tt][:].rearrange("s t p -> s p t"),
+                in1=gate[tt][:].rearrange("s t p -> s p t"),
+            )
+            nc.sync.dma_start(out=out_0[tt], in_=g[:])
+
+        def project_g(tt):
+            g_codes = keep.tile([P, P], U32, name="g_codes_%d" % tt, align_bytes=64)
+            g_scales = keep.tile([P, P], U8, name="g_scales_%d" % tt, align_bytes=64)
+            nc.vector.quantize_mx(
+                out=g_codes[:].bitcast(FP8X4),
+                scales=g_scales[:],
+                in_=g_grouped[tt][:].rearrange("p s t -> p (s t)"),
+            )
+            ga2_psum = turn_psum.tile([P, R], F32, name="ga2_psum", tag="turn")
+            nc.tensor.matmul_mx(
+                out=ga2_psum[:],
+                lhsT=g_codes[:].bitcast(FP8X4),
+                lhsT_scale=g_scales[:],
+                rhs=a2_words[:].bitcast(FP8X4),
+                rhs_scale=a2_plane[:],
+                start=True,
+                stop=True,
+            )
+            ga2 = keep.tile([P, R], F32, name="ga2_%d" % tt)
+            nc.scalar.copy(out=ga2[:], in_=ga2_psum[:])
+            nc.scalar.dma_start(out=out_1[tt], in_=ga2[:])
+
+        store_g(0)
+        project_g(0)
+        project_g(1)
+        store_g(1)

@@ -25,7 +25,11 @@ ROUND_COLS = K_PASS * ROUND_GROUPS
 PIECE_GROUPS = 2
 PIECES = ROUND_GROUPS // PIECE_GROUPS
 BANK_GROUPS = 2
-PLANE_GROUPS = 8
+OFFSETS = 4
+SCALE_ROWS = 16
+LAG = 2
+LEAD = LAG + 2
+WOVEN = 2
 LORA_STEP = 3
 LORA_BLOCKS = TOKEN_TILES + F // P
 LORA_SCALING = 2.0
@@ -60,7 +64,7 @@ def tile_feedforward_pa_k_kernel(
         x_pool = ctx.enter_context(tc.tile_pool(name="x_pool", bufs=4 * TOKEN_TILES))
         sorted_pool = ctx.enter_context(tc.tile_pool(name="sorted_pool", bufs=3))
         grouped_pool = ctx.enter_context(tc.tile_pool(name="grouped_pool", bufs=3))
-        codes_pool = ctx.enter_context(tc.tile_pool(name="codes_pool", bufs=6))
+        codes_pool = ctx.enter_context(tc.tile_pool(name="codes_pool", bufs=2 * ROUNDS))
         w_pool = ctx.enter_context(tc.tile_pool(name="w_pool", bufs=4 * 2 * PIECES))
         turn_psum = ctx.enter_context(tc.psum_pool(name="turn_psum", bufs=4))
         acc_psum = ctx.enter_context(tc.psum_pool(name="acc_psum", bufs=1))
@@ -84,6 +88,7 @@ def tile_feedforward_pa_k_kernel(
             raw = x_pool.tile([P, ROUND_COLS], BF16, name="x_raw", tag="x_raw")
             nc.sync.dma_start(out=raw[:], in_=x[tt, :, rnd * ROUND_COLS : (rnd + 1) * ROUND_COLS])
             x_raw[unit] = raw
+            weave_scale_rows()
 
         def load_w(rnd, branch):
             last = rnd == ROUNDS - 1 and branch == branches[-1]
@@ -102,23 +107,28 @@ def tile_feedforward_pa_k_kernel(
                         .bitcast(I32),
                     )
                 w_pieces[(rnd, branch, piece)] = w_piece
+                weave_scale_rows()
 
-        def load_scale_rows(branch, chunk):
-            source = scales_of[branch].bitcast(F32)[
-                chunk * PLANE_GROUPS : (chunk + 1) * PLANE_GROUPS
-            ]
-            for r in range(4):
-                nc.gpsimd.dma_start(
-                    out=planes[(branch, chunk)][4 * chunk + r : P : 32, :, :].bitcast(F32),
-                    in_=source[:, r : 16 : 4, :].rearrange("g q n -> q g n"),
-                )
+        def load_scale_row(branch, q):
+            first = 32 * (q // 4) + q % 4
+            nc.sync.dma_start(
+                out=planes[branch][first : first + 4 * OFFSETS : 4, :, :].bitcast(I32),
+                in_=scales_of[branch].bitcast(I32)[:, q, :].rearrange("(a j) n -> j a n", j=OFFSETS),
+            )
 
-        def zero_planes(chunk):
+        waiting_rows = [(branch, q) for branch in branches for q in range(SCALE_ROWS)]
+
+        def weave_scale_rows():
+            for branch, q in waiting_rows[:WOVEN]:
+                load_scale_row(branch, q)
+                waiting_rows.remove((branch, q))
+
+        def zero_planes():
             for branch in branches:
-                planes[(branch, chunk)] = keep.tile(
-                    [P, PLANE_GROUPS, F], U8, name="planes_%s_%d" % (branch, chunk), align_bytes=64
+                planes[branch] = keep.tile(
+                    [P, GROUPS // OFFSETS, F], U8, name="planes_" + branch, align_bytes=64
                 )
-                nc.vector.memset(planes[(branch, chunk)][:].bitcast(I32), 0)
+                nc.vector.memset(planes[branch][:].bitcast(I32), 0)
 
         def load_lora():
             for branch in branches:
@@ -183,13 +193,13 @@ def tile_feedforward_pa_k_kernel(
                     for i in range(PIECE_GROUPS):
                         local = piece * PIECE_GROUPS + i
                         group = rnd * ROUND_GROUPS + local
-                        chunk, in_plane = divmod(group, PLANE_GROUPS)
+                        in_plane, offset = divmod(group, OFFSETS)
                         nc.tensor.matmul_mx(
                             out=acc[(branch, tt)][:],
                             lhsT=x_codes[TOKEN_TILES * rnd + tt][:, local, :].bitcast(FP8X4),
                             lhsT_scale=x_scales[TOKEN_TILES * rnd + tt][:, local, :],
                             rhs=w_pieces[(rnd, branch, piece)][:, i, :].bitcast(FP8X4),
-                            rhs_scale=planes[(branch, chunk)][4 * chunk : P, in_plane, :],
+                            rhs_scale=planes[branch][4 * offset : P, in_plane, :],
                             start=(group == 0),
                             stop=(group == GROUPS - 1),
                         )
@@ -224,11 +234,9 @@ def tile_feedforward_pa_k_kernel(
                         mul=LORA_SCALING,
                     )
 
-        zero_planes(0)
+        zero_planes()
         identity_f32 = keep.tile([P, P], F32, name="identity_f32")
         make_identity(nc, identity_f32[:])
-        for branch in branches:
-            load_scale_rows(branch, 0)
         identity_bf16 = keep.tile([P, P], BF16, name="identity_bf16")
         make_identity(nc, identity_bf16[:])
         table_in = keep.tile([P, 1], F32, name="table_in")
@@ -239,59 +247,57 @@ def tile_feedforward_pa_k_kernel(
             for tt in range(TOKEN_TILES):
                 acc[(branch, tt)] = acc_psum.tile([P, F], F32, name="acc_%s_%d" % (branch, tt))
 
-        for unit in range(TOKEN_TILES):
+        a2_words = keep.tile([P, R], U32, name="a2_words", align_bytes=64)
+        a2_plane = keep.tile([P, R], U8, name="a2_plane", align_bytes=64)
+        nc.vector.memset(a2_plane[:].bitcast(I32), 0)
+        nc.gpsimd.dma_start(
+            out=a2_words[:].bitcast(I32),
+            in_=lora_A2_words[0].rearrange("p n t -> p (n t)").bitcast(I32),
+        )
+        for r in range(4):
+            nc.gpsimd.dma_start(
+                out=a2_plane[r : P : 32, :].bitcast(I32),
+                in_=lora_A2_scales[0].bitcast(I32)[r : 16 : 4, :],
+            )
+
+        steps = []
+        for i in range(ROUNDS + LAG):
+            if i < ROUNDS:
+                steps.append((i, "w1"))
+            if i >= LAG:
+                steps.append((i - LAG, "w3"))
+
+        def load_step(step):
+            if step + LEAD < 2 * ROUNDS:
+                load_x(step + LEAD)
+            load_w(*steps[step])
+            if step == 1:
+                load_lora()
+
+        for unit in range(LEAD):
             load_x(unit)
-        zero_planes(1)
-        for branch in branches:
-            load_scale_rows(branch, 1)
-        load_x(2)
-        load_w(0, "w1")
-        load_x(3)
-        load_x(4)
-        load_w(0, "w3")
+        load_step(0)
         sort_x(0)
-        for unit in range(TOKEN_TILES):
-            sort_x(unit + 1)
+        for unit in range(LEAD):
+            if unit + 1 < LEAD:
+                sort_x(unit + 1)
             turn_x(unit)
             quantise_x(unit)
 
-        a2_words = keep.tile([P, R], U32, name="a2_words", align_bytes=64)
-        a2_plane = keep.tile([P, R], U8, name="a2_plane", align_bytes=64)
-
-        for step in range(2 * ROUNDS):
-            rnd, odd = divmod(step, 2)
-            if step + 5 < 2 * ROUNDS:
-                load_x(step + 5)
-            if rnd + 1 < ROUNDS:
-                load_w(rnd + 1, branches[odd])
-            if step == 0:
-                load_lora()
+        for step, (rnd, branch) in enumerate(steps):
+            unit = step + LEAD
+            if step + 1 < len(steps):
+                load_step(step + 1)
             if step == LORA_STEP:
                 transpose_lora()
-            if step + 3 < 2 * ROUNDS:
-                sort_x(step + 3)
-            if step + 2 < 2 * ROUNDS:
-                turn_x(step + 2)
-                quantise_x(step + 2)
-            if step == 1:
-                for chunk in range(2, GROUPS // PLANE_GROUPS):
-                    zero_planes(chunk)
-                    for branch in branches:
-                        load_scale_rows(branch, chunk)
-                nc.vector.memset(a2_plane[:].bitcast(I32), 0)
-                nc.gpsimd.dma_start(
-                    out=a2_words[:].bitcast(F32),
-                    in_=lora_A2_words[0].rearrange("p n t -> p (n t)").bitcast(F32),
-                )
-                for r in range(4):
-                    nc.gpsimd.dma_start(
-                        out=a2_plane[r : P : 32, :].bitcast(F32),
-                        in_=lora_A2_scales[0].bitcast(F32)[r : 16 : 4, :],
-                    )
+            if unit < 2 * ROUNDS:
+                sort_x(unit)
+                turn_x(unit)
+                quantise_x(unit)
             if step == LORA_STEP:
                 multiply_lora()
-            multiply(rnd, branches[odd])
-            if step == 2 * ROUNDS - 2:
+            multiply(rnd, branch)
+            if (rnd, branch) == (ROUNDS - 1, "w1"):
                 for tt in range(TOKEN_TILES):
                     h1 = keep.tile([P, PACK, P], F32, name="h1_%d" % tt)
                     nc.vector.tensor_add(

@@ -22,15 +22,14 @@ GROUPS = D // K_PASS
 ROUND_GROUPS = 4
 ROUNDS = GROUPS // ROUND_GROUPS
 ROUND_COLS = K_PASS * ROUND_GROUPS
-PIECE_GROUPS = 2
-PIECES = ROUND_GROUPS // PIECE_GROUPS
+UNITS = TOKEN_TILES * ROUNDS
 BANK_GROUPS = 2
 OFFSETS = 4
 SCALE_ROWS = 16
-LAG = 2
-LEAD = LAG + 2
+LAG = 1
+LEAD = 3
+AHEAD = 1
 WOVEN = 2
-LORA_STEP = 3
 LORA_BLOCKS = TOKEN_TILES + F // P
 LORA_SCALING = 2.0
 
@@ -61,11 +60,11 @@ def tile_feedforward_pa_k_kernel(
 
     with ExitStack() as ctx:
         keep = ctx.enter_context(tc.tile_pool(name="keep", bufs=1))
-        x_pool = ctx.enter_context(tc.tile_pool(name="x_pool", bufs=4 * TOKEN_TILES))
+        x_pool = ctx.enter_context(tc.tile_pool(name="x_pool", bufs=8))
         sorted_pool = ctx.enter_context(tc.tile_pool(name="sorted_pool", bufs=3))
         grouped_pool = ctx.enter_context(tc.tile_pool(name="grouped_pool", bufs=3))
-        codes_pool = ctx.enter_context(tc.tile_pool(name="codes_pool", bufs=2 * ROUNDS))
-        w_pool = ctx.enter_context(tc.tile_pool(name="w_pool", bufs=4 * 2 * PIECES))
+        codes_pool = ctx.enter_context(tc.tile_pool(name="codes_pool", bufs=UNITS))
+        w_pool = ctx.enter_context(tc.tile_pool(name="w_pool", bufs=8))
         turn_psum = ctx.enter_context(tc.psum_pool(name="turn_psum", bufs=4))
         acc_psum = ctx.enter_context(tc.psum_pool(name="acc_psum", bufs=1))
         ctx.enter_context(tc.manual_schedule())
@@ -75,7 +74,7 @@ def tile_feedforward_pa_k_kernel(
         x_grouped = {}
         x_codes = {}
         x_scales = {}
-        w_pieces = {}
+        w_round = {}
         planes = {}
         lora_in = {}
         lora_turned = {}
@@ -83,52 +82,44 @@ def tile_feedforward_pa_k_kernel(
         acc = {}
         gate = {}
 
-        def load_x(unit):
-            rnd, tt = divmod(unit, TOKEN_TILES)
-            raw = x_pool.tile([P, ROUND_COLS], BF16, name="x_raw", tag="x_raw")
-            nc.sync.dma_start(out=raw[:], in_=x[tt, :, rnd * ROUND_COLS : (rnd + 1) * ROUND_COLS])
-            x_raw[unit] = raw
-            weave_scale_rows()
-
-        def load_w(rnd, branch):
-            last = rnd == ROUNDS - 1 and branch == branches[-1]
-            split = PIECE_GROUPS if last else 1
-            for piece in range(PIECES):
-                first = rnd * ROUND_GROUPS + piece * PIECE_GROUPS
-                w_piece = w_pool.tile(
-                    [P, PIECE_GROUPS, F], U32, name="w_piece", tag="w_piece", align_bytes=64
-                )
-                count = PIECE_GROUPS // split
-                for i in range(split):
-                    nc.sync.dma_start(
-                        out=w_piece[:, i * count : (i + 1) * count, :].bitcast(I32),
-                        in_=words_of[branch][first + i * count : first + (i + 1) * count]
-                        .rearrange("g p n t -> p g (n t)")
-                        .bitcast(I32),
-                    )
-                w_pieces[(rnd, branch, piece)] = w_piece
-                weave_scale_rows()
-
-        def load_scale_row(branch, q):
+        def load_scale_row(queue, branch, q):
             first = 32 * (q // 4) + q % 4
-            nc.sync.dma_start(
+            queue.dma_start(
                 out=planes[branch][first : first + 4 * OFFSETS : 4, :, :].bitcast(I32),
                 in_=scales_of[branch].bitcast(I32)[:, q, :].rearrange("(a j) n -> j a n", j=OFFSETS),
             )
 
-        waiting_rows = [(branch, q) for branch in branches for q in range(SCALE_ROWS)]
+        all_rows = [(branch, q) for branch in branches for q in range(SCALE_ROWS)]
+        gpsimd_rows = [(branch, q) for branch, q in all_rows if q >= 8]
+        sync_rows = [row for row in all_rows if row not in gpsimd_rows]
 
         def weave_scale_rows():
-            for branch, q in waiting_rows[:WOVEN]:
-                load_scale_row(branch, q)
-                waiting_rows.remove((branch, q))
+            for branch, q in sync_rows[:WOVEN]:
+                load_scale_row(nc.sync, branch, q)
+                sync_rows.remove((branch, q))
 
-        def zero_planes():
-            for branch in branches:
-                planes[branch] = keep.tile(
-                    [P, GROUPS // OFFSETS, F], U8, name="planes_" + branch, align_bytes=64
+        def load_x(unit):
+            rnd, tt = divmod(unit, TOKEN_TILES)
+            x_raw[unit] = x_pool.tile([P, ROUND_COLS], BF16, name="x_raw", tag="x_raw")
+            nc.sync.dma_start(
+                out=x_raw[unit][:], in_=x[tt, :, rnd * ROUND_COLS : (rnd + 1) * ROUND_COLS]
+            )
+            weave_scale_rows()
+
+        def load_w(rnd, branch, count):
+            words = w_pool.tile(
+                [P, ROUND_GROUPS, F], U32, name="w_words", tag="w_words", align_bytes=64
+            )
+            for i in range(0, ROUND_GROUPS, count):
+                first = rnd * ROUND_GROUPS + i
+                nc.sync.dma_start(
+                    out=words[:, i : i + count, :].bitcast(I32),
+                    in_=words_of[branch][first : first + count]
+                    .rearrange("g p n t -> p g (n t)")
+                    .bitcast(I32),
                 )
-                nc.vector.memset(planes[branch][:].bitcast(I32), 0)
+                weave_scale_rows()
+            w_round[(rnd, branch)] = words
 
         def load_lora():
             for branch in branches:
@@ -188,18 +179,17 @@ def tile_feedforward_pa_k_kernel(
             x_scales[unit] = scales
 
         def multiply(rnd, branch):
-            for piece in range(PIECES):
+            for pair in range(0, ROUND_GROUPS, 2):
                 for tt in range(TOKEN_TILES):
-                    for i in range(PIECE_GROUPS):
-                        local = piece * PIECE_GROUPS + i
+                    for local in range(pair, pair + 2):
                         group = rnd * ROUND_GROUPS + local
-                        in_plane, offset = divmod(group, OFFSETS)
+                        column, offset = divmod(group, OFFSETS)
                         nc.tensor.matmul_mx(
                             out=acc[(branch, tt)][:],
                             lhsT=x_codes[TOKEN_TILES * rnd + tt][:, local, :].bitcast(FP8X4),
                             lhsT_scale=x_scales[TOKEN_TILES * rnd + tt][:, local, :],
-                            rhs=w_pieces[(rnd, branch, piece)][:, i, :].bitcast(FP8X4),
-                            rhs_scale=planes[branch][4 * offset : P, in_plane, :],
+                            rhs=w_round[(rnd, branch)][:, local, :].bitcast(FP8X4),
+                            rhs_scale=planes[branch][4 * offset : P, column, :],
                             start=(group == 0),
                             stop=(group == GROUPS - 1),
                         )
@@ -234,11 +224,17 @@ def tile_feedforward_pa_k_kernel(
                         mul=LORA_SCALING,
                     )
 
-        zero_planes()
+        for branch in branches:
+            planes[branch] = keep.tile(
+                [P, GROUPS // OFFSETS, F], U8, name="planes_" + branch, align_bytes=64
+            )
+            nc.vector.memset(planes[branch][:].bitcast(I32), 0)
         identity_f32 = keep.tile([P, P], F32, name="identity_f32")
         make_identity(nc, identity_f32[:])
         identity_bf16 = keep.tile([P, P], BF16, name="identity_bf16")
         make_identity(nc, identity_bf16[:])
+        for branch, q in gpsimd_rows:
+            load_scale_row(nc.gpsimd, branch, q)
         table_in = keep.tile([P, 1], F32, name="table_in")
         table_out = keep.tile([P, 1], F32, name="table_out")
         nc.vector.memset(table_in[:], 0.0)
@@ -246,19 +242,9 @@ def tile_feedforward_pa_k_kernel(
         for branch in branches:
             for tt in range(TOKEN_TILES):
                 acc[(branch, tt)] = acc_psum.tile([P, F], F32, name="acc_%s_%d" % (branch, tt))
-
         a2_words = keep.tile([P, R], U32, name="a2_words", align_bytes=64)
         a2_plane = keep.tile([P, R], U8, name="a2_plane", align_bytes=64)
         nc.vector.memset(a2_plane[:].bitcast(I32), 0)
-        nc.gpsimd.dma_start(
-            out=a2_words[:].bitcast(I32),
-            in_=lora_A2_words[0].rearrange("p n t -> p (n t)").bitcast(I32),
-        )
-        for r in range(4):
-            nc.gpsimd.dma_start(
-                out=a2_plane[r : P : 32, :].bitcast(I32),
-                in_=lora_A2_scales[0].bitcast(I32)[r : 16 : 4, :],
-            )
 
         steps = []
         for i in range(ROUNDS + LAG):
@@ -268,34 +254,45 @@ def tile_feedforward_pa_k_kernel(
                 steps.append((i - LAG, "w3"))
 
         def load_step(step):
-            if step + LEAD < 2 * ROUNDS:
-                load_x(step + LEAD)
-            load_w(*steps[step])
-            if step == 1:
-                load_lora()
+            if step + LEAD + AHEAD < UNITS:
+                load_x(step + LEAD + AHEAD)
+            left = len(steps) - step
+            load_w(*steps[step], 1 if left <= 1 else 2 if left <= 16 else ROUND_GROUPS)
+            if left == 1:
+                nc.sync.dma_start(
+                    out=a2_words[:].bitcast(I32),
+                    in_=lora_A2_words[0].rearrange("p n t -> p (n t)").bitcast(I32),
+                )
+                for r in range(4):
+                    nc.sync.dma_start(
+                        out=a2_plane[r : P : 32, :].bitcast(I32),
+                        in_=lora_A2_scales[0].bitcast(I32)[r : 16 : 4, :],
+                    )
 
-        for unit in range(LEAD):
+        for unit in range(LEAD + AHEAD):
             load_x(unit)
+            if unit == 1:
+                load_lora()
         load_step(0)
+        load_step(1)
         sort_x(0)
         for unit in range(LEAD):
-            if unit + 1 < LEAD:
+            if unit + 1 < LEAD + AHEAD:
                 sort_x(unit + 1)
             turn_x(unit)
             quantise_x(unit)
+            if unit == 2:
+                transpose_lora()
+                multiply_lora()
 
         for step, (rnd, branch) in enumerate(steps):
-            unit = step + LEAD
-            if step + 1 < len(steps):
-                load_step(step + 1)
-            if step == LORA_STEP:
-                transpose_lora()
-            if unit < 2 * ROUNDS:
-                sort_x(unit)
-                turn_x(unit)
-                quantise_x(unit)
-            if step == LORA_STEP:
-                multiply_lora()
+            if step + 2 < len(steps):
+                load_step(step + 2)
+            if step + LEAD + AHEAD < UNITS:
+                sort_x(step + LEAD + AHEAD)
+            if step + LEAD < UNITS:
+                turn_x(step + LEAD)
+                quantise_x(step + LEAD)
             multiply(rnd, branch)
             if (rnd, branch) == (ROUNDS - 1, "w1"):
                 for tt in range(TOKEN_TILES):

@@ -26,8 +26,8 @@ UNITS = TOKEN_TILES * ROUNDS
 BANK_GROUPS = 2
 OFFSETS = 4
 SCALE_ROWS = 16
-LAG = 1
-LEAD = 3
+LAG = 3
+LEAD = 5
 AHEAD = 1
 WOVEN = 2
 LORA_BLOCKS = TOKEN_TILES + F // P

@@ -26,9 +26,10 @@ UNITS = TOKEN_TILES * ROUNDS
 BANK_GROUPS = 2
 OFFSETS = 4
 SCALE_ROWS = 16
-LAG = 3
-LEAD = 5
-AHEAD = 1
+LAG = 2
+LEAD = 4
+AHEAD = 0
+HEAD = 7
 WOVEN = 2
 LORA_BLOCKS = TOKEN_TILES + F // P
 LORA_SCALING = 2.0
@@ -216,11 +217,11 @@ def tile_feedforward_pa_k_kernel(
                         stop=True,
                     )
                     lora_term[(branch, tt)] = keep.tile(
-                        [P, PACK, P], F32, name="lora_term_%s_%d" % (branch, tt)
+                        [P, 2, P, 2], F32, name="lora_term_%s_%d" % (branch, tt)
                     )
                     nc.scalar.mul(
                         out=lora_term[(branch, tt)][:],
-                        in_=product[:],
+                        in_=product[:].rearrange("s (u e) p -> s u p e", u=2),
                         mul=LORA_SCALING,
                     )
 
@@ -254,10 +255,10 @@ def tile_feedforward_pa_k_kernel(
                 steps.append((i - LAG, "w3"))
 
         def load_step(step):
-            if step + LEAD + AHEAD < UNITS:
+            if HEAD <= step + LEAD + AHEAD < UNITS:
                 load_x(step + LEAD + AHEAD)
             left = len(steps) - step
-            load_w(*steps[step], 1 if left <= 1 else 2 if left <= 16 else ROUND_GROUPS)
+            load_w(*steps[step], 1 if left <= 1 else 2 if left <= 5 else ROUND_GROUPS)
             if left == 1:
                 nc.sync.dma_start(
                     out=a2_words[:].bitcast(I32),
@@ -269,68 +270,71 @@ def tile_feedforward_pa_k_kernel(
                         in_=lora_A2_scales[0].bitcast(I32)[r : 16 : 4, :],
                     )
 
-        for unit in range(LEAD + AHEAD):
+        for unit in range(HEAD):
             load_x(unit)
-            if unit == 1:
+            if unit == 5:
                 load_lora()
         load_step(0)
         load_step(1)
         sort_x(0)
-        for unit in range(LEAD):
-            if unit + 1 < LEAD + AHEAD:
+        for unit in range(HEAD):
+            if unit + 1 < HEAD:
                 sort_x(unit + 1)
             turn_x(unit)
             quantise_x(unit)
-            if unit == 2:
+            if unit == 5:
                 transpose_lora()
                 multiply_lora()
 
         for step, (rnd, branch) in enumerate(steps):
             if step + 2 < len(steps):
                 load_step(step + 2)
-            if step + LEAD + AHEAD < UNITS:
+            if HEAD <= step + LEAD + AHEAD < UNITS:
                 sort_x(step + LEAD + AHEAD)
-            if step + LEAD < UNITS:
+            if HEAD <= step + LEAD < UNITS:
                 turn_x(step + LEAD)
                 quantise_x(step + LEAD)
             multiply(rnd, branch)
             if (rnd, branch) == (ROUNDS - 1, "w1"):
                 for tt in range(TOKEN_TILES):
-                    h1 = keep.tile([P, PACK, P], F32, name="h1_%d" % tt)
+                    h1 = keep.tile([P, 2, P, 2], F32, name="h1_%d" % tt)
                     nc.vector.tensor_add(
                         out=h1[:],
-                        in0=acc[("w1", tt)][:].rearrange("s (p t) -> s t p", t=PACK),
+                        in0=acc[("w1", tt)][:].rearrange("s (p u e) -> s u p e", u=2, e=2),
                         in1=lora_term[("w1", tt)][:],
                     )
-                    gate[tt] = keep.tile([P, PACK, P], F32, name="gate_%d" % tt)
+                    gate[tt] = keep.tile([P, 2, P, 2], F32, name="gate_%d" % tt)
                     nc.scalar.activation(out=gate[tt][:], in_=h1[:], func=SILU)
 
         h3 = {}
         g_sorted = {}
         for tt in range(TOKEN_TILES):
-            h3[tt] = keep.tile([P, PACK, P], F32, name="h3_%d" % tt)
+            h3[tt] = keep.tile([P, 2, P, 2], F32, name="h3_%d" % tt)
             nc.vector.tensor_add(
                 out=h3[tt][:],
-                in0=acc[("w3", tt)][:].rearrange("s (p t) -> s t p", t=PACK),
+                in0=acc[("w3", tt)][:].rearrange("s (p u e) -> s u p e", u=2, e=2),
                 in1=lora_term[("w3", tt)][:],
             )
         for tt in range(TOKEN_TILES):
-            g_sorted[tt] = keep.tile([P, PACK, P], BF16, name="g_sorted_%d" % tt)
+            g_sorted[tt] = keep.tile([P, 2, P, 2], BF16, name="g_sorted_%d" % tt)
             nc.vector.tensor_mul(out=g_sorted[tt][:], in0=h3[tt][:], in1=gate[tt][:])
         g_grouped = {}
         for tt in range(TOKEN_TILES):
-            g_turned = turn_psum.tile([P, PACK, P], BF16, name="g_turned", tag="turn")
-            for t in range(PACK):
-                nc.tensor.transpose(g_turned[:, t, :], g_sorted[tt][:, t, :], identity_bf16[:])
+            g_turned = turn_psum.tile([P, 2, P], F32, name="g_turned", tag="turn")
+            g_words = g_sorted[tt][:].rearrange("s u p e -> s u (p e)").bitcast(F32)
+            for u in range(2):
+                nc.tensor.transpose(g_turned[:, u, :], g_words[:, u, :], identity_f32[:])
             g_grouped[tt] = keep.tile([P, P, PACK], BF16, name="g_grouped_%d" % tt, align_bytes=64)
-            nc.scalar.copy(out=g_grouped[tt][:], in_=g_turned[:].rearrange("p t s -> p s t"))
+            nc.scalar.copy(
+                out=g_grouped[tt][:].bitcast(F32), in_=g_turned[:].rearrange("p u s -> p s u")
+            )
 
         def store_g(tt):
             g = keep.tile([P, F], F32, name="g_%d" % tt)
             nc.vector.tensor_mul(
-                out=g[:].rearrange("s (p t) -> s p t", t=PACK),
-                in0=h3[tt][:].rearrange("s t p -> s p t"),
-                in1=gate[tt][:].rearrange("s t p -> s p t"),
+                out=g[:].rearrange("s (p u e) -> s p u e", u=2, e=2),
+                in0=h3[tt][:].rearrange("s u p e -> s p u e"),
+                in1=gate[tt][:].rearrange("s u p e -> s p u e"),
             )
             nc.sync.dma_start(out=out_0[tt], in_=g[:])
 
@@ -357,6 +361,6 @@ def tile_feedforward_pa_k_kernel(
             nc.scalar.dma_start(out=out_1[tt], in_=ga2[:])
 
         store_g(0)
+        store_g(1)
         project_g(0)
         project_g(1)
-        store_g(1)

@@ -26,10 +26,10 @@ UNITS = TOKEN_TILES * ROUNDS
 BANK_GROUPS = 2
 OFFSETS = 4
 SCALE_ROWS = 16
-LAG = 2
-LEAD = 4
+LAG = 1
+LEAD = 3
 AHEAD = 0
-HEAD = 7
+HEAD = 4
 WOVEN = 2
 LORA_BLOCKS = TOKEN_TILES + F // P
 LORA_SCALING = 2.0
@@ -91,11 +91,12 @@ def tile_feedforward_pa_k_kernel(
             )
 
         all_rows = [(branch, q) for branch in branches for q in range(SCALE_ROWS)]
-        gpsimd_rows = [(branch, q) for branch, q in all_rows if q >= 8]
+        gpsimd_rows = [(branch, q) for branch, q in all_rows if False]
         sync_rows = [row for row in all_rows if row not in gpsimd_rows]
+        sync_rows.sort(key=lambda row: row[1] < SCALE_ROWS // 2)
 
-        def weave_scale_rows():
-            for branch, q in sync_rows[:WOVEN]:
+        def weave_scale_rows(count=WOVEN):
+            for branch, q in sync_rows[:count]:
                 load_scale_row(nc.sync, branch, q)
                 sync_rows.remove((branch, q))
 
@@ -272,7 +273,9 @@ def tile_feedforward_pa_k_kernel(
 
         for unit in range(HEAD):
             load_x(unit)
-            if unit == 5:
+            if unit == 0:
+                weave_scale_rows(22)
+            if unit == 1:
                 load_lora()
         load_step(0)
         load_step(1)
@@ -282,7 +285,7 @@ def tile_feedforward_pa_k_kernel(
                 sort_x(unit + 1)
             turn_x(unit)
             quantise_x(unit)
-            if unit == 5:
+            if unit == 1:
                 transpose_lora()
                 multiply_lora()
 

@@ -29,8 +29,8 @@ SCALE_ROWS = 16
 LAG = 1
 LEAD = 3
 AHEAD = 0
-HEAD = 4
-WOVEN = 2
+HEAD = 5
+WOVEN = 4
 LORA_BLOCKS = TOKEN_TILES + F // P
 LORA_SCALING = 2.0
 
@@ -61,11 +61,11 @@ def tile_feedforward_pa_k_kernel(
 
     with ExitStack() as ctx:
         keep = ctx.enter_context(tc.tile_pool(name="keep", bufs=1))
-        x_pool = ctx.enter_context(tc.tile_pool(name="x_pool", bufs=8))
+        x_pool = ctx.enter_context(tc.tile_pool(name="x_pool", bufs=6))
         sorted_pool = ctx.enter_context(tc.tile_pool(name="sorted_pool", bufs=3))
         grouped_pool = ctx.enter_context(tc.tile_pool(name="grouped_pool", bufs=3))
         codes_pool = ctx.enter_context(tc.tile_pool(name="codes_pool", bufs=UNITS))
-        w_pool = ctx.enter_context(tc.tile_pool(name="w_pool", bufs=8))
+        w_pool = ctx.enter_context(tc.tile_pool(name="w_pool", bufs=6))
         turn_psum = ctx.enter_context(tc.psum_pool(name="turn_psum", bufs=4))
         acc_psum = ctx.enter_context(tc.psum_pool(name="acc_psum", bufs=1))
         ctx.enter_context(tc.manual_schedule())
@@ -83,22 +83,30 @@ def tile_feedforward_pa_k_kernel(
         acc = {}
         gate = {}
 
-        def load_scale_row(queue, branch, q):
-            first = 32 * (q // 4) + q % 4
+        def stage_scale_rows():
+            for w, branch in enumerate(branches):
+                nc.sync.dma_start(
+                    out=staged[32 + w : 96 : 4, :, :, :].rearrange("i a r n -> i a (r n)"),
+                    in_=scales_of[branch]
+                    .bitcast(I32)
+                    .rearrange("(a j) (c r) n -> (j c) a (r n)", j=OFFSETS, r=4),
+                )
+
+        def spread_scale_rows(queue, branch, quadrant):
+            first = 32 + 4 * quadrant + branches.index(branch)
             queue.dma_start(
-                out=planes[branch][first : first + 4 * OFFSETS : 4, :, :].bitcast(I32),
-                in_=scales_of[branch].bitcast(I32)[:, q, :].rearrange("(a j) n -> j a n", j=OFFSETS),
+                out=planes[branch][32 * quadrant : 32 * quadrant + 16, :, :]
+                .rearrange("p a n -> p (a n)")
+                .bitcast(I32),
+                in_=regrouped[first:96:16, :, :, :].rearrange("j r a n -> j r (a n)"),
             )
 
-        all_rows = [(branch, q) for branch in branches for q in range(SCALE_ROWS)]
-        gpsimd_rows = [(branch, q) for branch, q in all_rows if False]
-        sync_rows = [row for row in all_rows if row not in gpsimd_rows]
-        sync_rows.sort(key=lambda row: row[1] < SCALE_ROWS // 2)
+        waiting = []
 
         def weave_scale_rows(count=WOVEN):
-            for branch, q in sync_rows[:count]:
-                load_scale_row(nc.sync, branch, q)
-                sync_rows.remove((branch, q))
+            for branch, quadrant in waiting[:count]:
+                spread_scale_rows(nc.sync, branch, quadrant)
+                waiting.remove((branch, quadrant))
 
         def load_x(unit):
             rnd, tt = divmod(unit, TOKEN_TILES)
@@ -226,6 +234,9 @@ def tile_feedforward_pa_k_kernel(
                         mul=LORA_SCALING,
                     )
 
+        staged = keep.tile([P, GROUPS // OFFSETS, 4, F // 4], I32, name="staged")
+        regrouped = keep.tile([P, 4, GROUPS // OFFSETS, F // 4], I32, name="regrouped")
+        nc.vector.memset(staged[:], 0)
         for branch in branches:
             planes[branch] = keep.tile(
                 [P, GROUPS // OFFSETS, F], U8, name="planes_" + branch, align_bytes=64
@@ -235,8 +246,6 @@ def tile_feedforward_pa_k_kernel(
         make_identity(nc, identity_f32[:])
         identity_bf16 = keep.tile([P, P], BF16, name="identity_bf16")
         make_identity(nc, identity_bf16[:])
-        for branch, q in gpsimd_rows:
-            load_scale_row(nc.gpsimd, branch, q)
         table_in = keep.tile([P, 1], F32, name="table_in")
         table_out = keep.tile([P, 1], F32, name="table_out")
         nc.vector.memset(table_in[:], 0.0)
@@ -273,15 +282,23 @@ def tile_feedforward_pa_k_kernel(
 
         for unit in range(HEAD):
             load_x(unit)
-            if unit == 0:
-                weave_scale_rows(22)
+            if unit == 2:
+                stage_scale_rows()
+            if unit == 4:
+                for early in range(3):
+                    sort_x(early)
+                nc.vector.tensor_copy(out=regrouped[:], in_=staged[:].rearrange("p a r n -> p r a n"))
+                waiting.extend((b, c) for b in branches for c in range(4) if not (False))
+                for branch in branches:
+                    for c in range(4):
+                        if False:
+                            spread_scale_rows(nc.gpsimd, branch, c)
             if unit == 1:
                 load_lora()
         load_step(0)
         load_step(1)
-        sort_x(0)
         for unit in range(HEAD):
-            if unit + 1 < HEAD:
+            if 3 <= unit + 1 < HEAD:
                 sort_x(unit + 1)
             turn_x(unit)
             quantise_x(unit)

@@ -29,7 +29,7 @@ SCALE_ROWS = 16
 LAG = 1
 LEAD = 3
 AHEAD = 0
-HEAD = 5
+HEAD = 6
 WOVEN = 4
 LORA_BLOCKS = TOKEN_TILES + F // P
 LORA_SCALING = 2.0
@@ -61,11 +61,11 @@ def tile_feedforward_pa_k_kernel(
 
     with ExitStack() as ctx:
         keep = ctx.enter_context(tc.tile_pool(name="keep", bufs=1))
-        x_pool = ctx.enter_context(tc.tile_pool(name="x_pool", bufs=6))
+        x_pool = ctx.enter_context(tc.tile_pool(name="x_pool", bufs=7))
         sorted_pool = ctx.enter_context(tc.tile_pool(name="sorted_pool", bufs=3))
         grouped_pool = ctx.enter_context(tc.tile_pool(name="grouped_pool", bufs=3))
         codes_pool = ctx.enter_context(tc.tile_pool(name="codes_pool", bufs=UNITS))
-        w_pool = ctx.enter_context(tc.tile_pool(name="w_pool", bufs=6))
+        w_pool = ctx.enter_context(tc.tile_pool(name="w_pool", bufs=5))
         turn_psum = ctx.enter_context(tc.psum_pool(name="turn_psum", bufs=4))
         acc_psum = ctx.enter_context(tc.psum_pool(name="acc_psum", bufs=1))
         ctx.enter_context(tc.manual_schedule())
@@ -166,8 +166,7 @@ def tile_feedforward_pa_k_kernel(
                             x_sorted[unit][:, bank * BANK_GROUPS + i, u, :],
                             identity_f32[:],
                         )
-                copy_out = nc.scalar.copy if bank % 2 == 0 else nc.vector.tensor_copy
-                copy_out(
+                nc.scalar.copy(
                     out=grouped_words[:, bank * BANK_GROUPS : (bank + 1) * BANK_GROUPS, :, :],
                     in_=turned[:].rearrange("p g u t -> p g t u"),
                 )
@@ -282,10 +281,10 @@ def tile_feedforward_pa_k_kernel(
 
         for unit in range(HEAD):
             load_x(unit)
-            if unit == 2:
+            if unit == 1:
                 stage_scale_rows()
-            if unit == 4:
-                for early in range(3):
+            if unit == 5:
+                for early in range(2):
                     sort_x(early)
                 nc.vector.tensor_copy(out=regrouped[:], in_=staged[:].rearrange("p a r n -> p r a n"))
                 waiting.extend((b, c) for b in branches for c in range(4) if not (False))
@@ -298,7 +297,7 @@ def tile_feedforward_pa_k_kernel(
         load_step(0)
         load_step(1)
         for unit in range(HEAD):
-            if 3 <= unit + 1 < HEAD:
+            if 2 <= unit + 1 < HEAD:
                 sort_x(unit + 1)
             turn_x(unit)
             quantise_x(unit)
@@ -311,9 +310,10 @@ def tile_feedforward_pa_k_kernel(
                 load_step(step + 2)
             if HEAD <= step + LEAD + AHEAD < UNITS:
                 sort_x(step + LEAD + AHEAD)
+            if HEAD < step + LEAD <= UNITS:
+                quantise_x(step + LEAD - 1)
             if HEAD <= step + LEAD < UNITS:
                 turn_x(step + LEAD)
-                quantise_x(step + LEAD)
             multiply(rnd, branch)
             if (rnd, branch) == (ROUNDS - 1, "w1"):
                 for tt in range(TOKEN_TILES):

@@ -29,10 +29,11 @@ SCALE_ROWS = 16
 LAG = 1
 LEAD = 3
 AHEAD = 0
-HEAD = 6
-WOVEN = 4
+HEAD = 5
+WOVEN = 2
 LORA_BLOCKS = TOKEN_TILES + F // P
 LORA_SCALING = 2.0
+HALF = F // 2
 
 FLOPS = 2 * TOKEN_TILES * P * (2 * D * F + 2 * R * F + F * R)
 
@@ -61,7 +62,7 @@ def tile_feedforward_pa_k_kernel(
 
     with ExitStack() as ctx:
         keep = ctx.enter_context(tc.tile_pool(name="keep", bufs=1))
-        x_pool = ctx.enter_context(tc.tile_pool(name="x_pool", bufs=7))
+        x_pool = ctx.enter_context(tc.tile_pool(name="x_pool", bufs=6))
         sorted_pool = ctx.enter_context(tc.tile_pool(name="sorted_pool", bufs=3))
         grouped_pool = ctx.enter_context(tc.tile_pool(name="grouped_pool", bufs=3))
         codes_pool = ctx.enter_context(tc.tile_pool(name="codes_pool", bufs=UNITS))
@@ -92,29 +93,25 @@ def tile_feedforward_pa_k_kernel(
                     .rearrange("(a j) (c r) n -> (j c) a (r n)", j=OFFSETS, r=4),
                 )
 
-        def spread_scale_rows(queue, branch, quadrant):
+        def spread_scale_rows(branch, quadrant):
             first = 32 + 4 * quadrant + branches.index(branch)
-            queue.dma_start(
+            nc.sync.dma_start(
                 out=planes[branch][32 * quadrant : 32 * quadrant + 16, :, :]
                 .rearrange("p a n -> p (a n)")
                 .bitcast(I32),
                 in_=regrouped[first:96:16, :, :, :].rearrange("j r a n -> j r (a n)"),
             )
 
-        waiting = []
-
-        def weave_scale_rows(count=WOVEN):
-            for branch, quadrant in waiting[:count]:
-                spread_scale_rows(nc.sync, branch, quadrant)
-                waiting.remove((branch, quadrant))
+        def unit_piece(unit):
+            return 4 if unit == UNITS - 1 else ROUND_GROUPS
 
         def load_x(unit):
             rnd, tt = divmod(unit, TOKEN_TILES)
             x_raw[unit] = x_pool.tile([P, ROUND_COLS], BF16, name="x_raw", tag="x_raw")
-            nc.sync.dma_start(
-                out=x_raw[unit][:], in_=x[tt, :, rnd * ROUND_COLS : (rnd + 1) * ROUND_COLS]
-            )
-            weave_scale_rows()
+            width = K_PASS * unit_piece(unit)
+            for i in range(0, ROUND_COLS, width):
+                first = rnd * ROUND_COLS + i
+                nc.sync.dma_start(out=x_raw[unit][:, i : i + width], in_=x[tt, :, first : first + width])
 
         def load_w(rnd, branch, count):
             words = w_pool.tile(
@@ -128,7 +125,6 @@ def tile_feedforward_pa_k_kernel(
                     .rearrange("g p n t -> p g (n t)")
                     .bitcast(I32),
                 )
-                weave_scale_rows()
             w_round[(rnd, branch)] = words
 
         def load_lora():
@@ -136,7 +132,8 @@ def tile_feedforward_pa_k_kernel(
                 xa, lora_b = lora_inputs[branch]
                 lora_in[branch] = keep.tile([P, LORA_BLOCKS, R], BF16, name="lora_in_" + branch)
                 nc.sync.dma_start(
-                    out=lora_in[branch][:, 0:TOKEN_TILES, :], in_=xa.rearrange("b s r -> s b r")
+                    out=lora_in[branch][:, 0:TOKEN_TILES, :],
+                    in_=xa.rearrange("b (q i) r -> (b q) i r", i=TOKEN_TILES),
                 )
                 nc.sync.dma_start(
                     out=lora_in[branch][:, TOKEN_TILES:, :],
@@ -147,10 +144,12 @@ def tile_feedforward_pa_k_kernel(
             x_sorted[unit] = sorted_pool.tile(
                 [P, ROUND_GROUPS, 2, P], F32, name="sorted_words", tag="sorted_words"
             )
-            nc.vector.tensor_copy(
-                out=x_sorted[unit][:],
-                in_=x_raw[unit][:].bitcast(F32).rearrange("s (g p u) -> s g u p", g=ROUND_GROUPS, u=2),
-            )
+            words = x_raw[unit][:].bitcast(F32).rearrange("s (g p u) -> s g u p", g=ROUND_GROUPS, u=2)
+            count = unit_piece(unit)
+            for i in range(0, ROUND_GROUPS, count):
+                nc.vector.tensor_copy(
+                    out=x_sorted[unit][:, i : i + count, :, :], in_=words[:, i : i + count, :, :]
+                )
 
         def turn_x(unit):
             grouped = grouped_pool.tile(
@@ -166,7 +165,8 @@ def tile_feedforward_pa_k_kernel(
                             x_sorted[unit][:, bank * BANK_GROUPS + i, u, :],
                             identity_f32[:],
                         )
-                nc.scalar.copy(
+                copy_out = nc.scalar.copy if bank % 2 == 0 or unit < HEAD else nc.vector.tensor_copy
+                copy_out(
                     out=grouped_words[:, bank * BANK_GROUPS : (bank + 1) * BANK_GROUPS, :, :],
                     in_=turned[:].rearrange("p g u t -> p g t u"),
                 )
@@ -187,6 +187,8 @@ def tile_feedforward_pa_k_kernel(
             x_codes[unit] = codes
             x_scales[unit] = scales
 
+        closing = {"w1": GROUPS - 1, "w3": GROUPS - ROUND_GROUPS - 1}
+
         def multiply(rnd, branch):
             for pair in range(0, ROUND_GROUPS, 2):
                 for tt in range(TOKEN_TILES):
@@ -200,7 +202,7 @@ def tile_feedforward_pa_k_kernel(
                             rhs=w_round[(rnd, branch)][:, local, :].bitcast(FP8X4),
                             rhs_scale=planes[branch][4 * offset : P, column, :],
                             start=(group == 0),
-                            stop=(group == GROUPS - 1),
+                            stop=(group == closing[branch]),
                         )
 
         def transpose_lora():
@@ -211,7 +213,15 @@ def tile_feedforward_pa_k_kernel(
                 lora_turned[branch] = keep.tile(
                     [P, LORA_BLOCKS, P], BF16, name="lora_turned_" + branch
                 )
-                nc.scalar.copy(out=lora_turned[branch][:], in_=turned[:])
+                nc.scalar.copy(
+                    out=lora_turned[branch][:, 0:TOKEN_TILES, :].rearrange(
+                        "r b (q i) -> r (b q) i", i=TOKEN_TILES
+                    ),
+                    in_=turned[:, 0:TOKEN_TILES, :].rearrange("r i p -> r p i"),
+                )
+                nc.scalar.copy(
+                    out=lora_turned[branch][:, TOKEN_TILES:, :], in_=turned[:, TOKEN_TILES:, :]
+                )
 
         def multiply_lora():
             for branch in branches:
@@ -233,6 +243,10 @@ def tile_feedforward_pa_k_kernel(
                         mul=LORA_SCALING,
                     )
 
+        table_in = keep.tile([P, 1], F32, name="table_in")
+        table_out = keep.tile([P, 1], F32, name="table_out")
+        nc.vector.memset(table_in[:], 0.0)
+        nc.scalar.activation(out=table_out[:], in_=table_in[:], func=SILU)
         staged = keep.tile([P, GROUPS // OFFSETS, 4, F // 4], I32, name="staged")
         regrouped = keep.tile([P, 4, GROUPS // OFFSETS, F // 4], I32, name="regrouped")
         nc.vector.memset(staged[:], 0)
@@ -245,10 +259,6 @@ def tile_feedforward_pa_k_kernel(
         make_identity(nc, identity_f32[:])
         identity_bf16 = keep.tile([P, P], BF16, name="identity_bf16")
         make_identity(nc, identity_bf16[:])
-        table_in = keep.tile([P, 1], F32, name="table_in")
-        table_out = keep.tile([P, 1], F32, name="table_out")
-        nc.vector.memset(table_in[:], 0.0)
-        nc.scalar.activation(out=table_out[:], in_=table_in[:], func=SILU)
         for branch in branches:
             for tt in range(TOKEN_TILES):
                 acc[(branch, tt)] = acc_psum.tile([P, F], F32, name="acc_%s_%d" % (branch, tt))
@@ -267,7 +277,7 @@ def tile_feedforward_pa_k_kernel(
             if HEAD <= step + LEAD + AHEAD < UNITS:
                 load_x(step + LEAD + AHEAD)
             left = len(steps) - step
-            load_w(*steps[step], 1 if left <= 1 else 2 if left <= 5 else ROUND_GROUPS)
+            load_w(*steps[step], 1 if left <= 1 else 2 if left <= 7 else ROUND_GROUPS)
             if left == 1:
                 nc.sync.dma_start(
                     out=a2_words[:].bitcast(I32),
@@ -283,18 +293,15 @@ def tile_feedforward_pa_k_kernel(
             load_x(unit)
             if unit == 1:
                 stage_scale_rows()
-            if unit == 5:
-                for early in range(2):
-                    sort_x(early)
-                nc.vector.tensor_copy(out=regrouped[:], in_=staged[:].rearrange("p a r n -> p r a n"))
-                waiting.extend((b, c) for b in branches for c in range(4) if not (False))
-                for branch in branches:
-                    for c in range(4):
-                        if False:
-                            spread_scale_rows(nc.gpsimd, branch, c)
-            if unit == 1:
                 load_lora()
         load_step(0)
+        for unit in range(2):
+            sort_x(unit)
+        nc.vector.tensor_copy(out=regrouped[:], in_=staged[:].rearrange("p a r n -> p r a n"))
+        for quadrants in ((2, 3), (0, 1)):
+            for branch in branches:
+                for quadrant in quadrants:
+                    spread_scale_rows(branch, quadrant)
         load_step(1)
         for unit in range(HEAD):
             if 2 <= unit + 1 < HEAD:
@@ -305,7 +312,7 @@ def tile_feedforward_pa_k_kernel(
                 transpose_lora()
                 multiply_lora()
 
-        for step, (rnd, branch) in enumerate(steps):
+        for step, (rnd, branch) in enumerate(steps[:-1]):
             if step + 2 < len(steps):
                 load_step(step + 2)
             if HEAD <= step + LEAD + AHEAD < UNITS:
@@ -327,17 +334,51 @@ def tile_feedforward_pa_k_kernel(
                     nc.scalar.activation(out=gate[tt][:], in_=h1[:], func=SILU)
 
         h3 = {}
+        h3_part = {}
         g_sorted = {}
         for tt in range(TOKEN_TILES):
-            h3[tt] = keep.tile([P, 2, P, 2], F32, name="h3_%d" % tt)
+            h3_part[tt] = keep.tile([P, 2, P, 2], F32, name="h3_part_%d" % tt)
             nc.vector.tensor_add(
-                out=h3[tt][:],
+                out=h3_part[tt][:],
                 in0=acc[("w3", tt)][:].rearrange("s (p u e) -> s u p e", u=2, e=2),
                 in1=lora_term[("w3", tt)][:],
             )
-        for tt in range(TOKEN_TILES):
+            h3[tt] = keep.tile([P, 2, P, 2], F32, name="h3_%d" % tt)
             g_sorted[tt] = keep.tile([P, 2, P, 2], BF16, name="g_sorted_%d" % tt)
-            nc.vector.tensor_mul(out=g_sorted[tt][:], in0=h3[tt][:], in1=gate[tt][:])
+        for half in range(2):
+            rest = {}
+            for tt in range(TOKEN_TILES):
+                rest[tt] = turn_psum.tile([P, HALF], F32, name="rest", tag="turn")
+            for locals_ in ((0, 1, 2), (3,)):
+                for tt in range(TOKEN_TILES):
+                    for local in locals_:
+                        column, offset = divmod(GROUPS - ROUND_GROUPS + local, OFFSETS)
+                        nc.tensor.matmul_mx(
+                            out=rest[tt][:],
+                            lhsT=x_codes[UNITS - TOKEN_TILES + tt][:, local, :].bitcast(FP8X4),
+                            lhsT_scale=x_scales[UNITS - TOKEN_TILES + tt][:, local, :],
+                            rhs=w_round[steps[-1]][
+                                :, local, half * HALF : (half + 1) * HALF
+                            ].bitcast(FP8X4),
+                            rhs_scale=planes["w3"][
+                                4 * offset : P, column, half * HALF : (half + 1) * HALF
+                            ],
+                            start=(local == 0),
+                            stop=(local == ROUND_GROUPS - 1),
+                        )
+            part = slice(half * P // 2, (half + 1) * P // 2)
+            for tt in range(TOKEN_TILES):
+                nc.vector.tensor_add(
+                    out=h3[tt][:, :, part, :],
+                    in0=rest[tt][:].rearrange("s (p u e) -> s u p e", u=2, e=2),
+                    in1=h3_part[tt][:, :, part, :],
+                )
+            for tt in range(TOKEN_TILES):
+                nc.vector.tensor_mul(
+                    out=g_sorted[tt][:, :, part, :],
+                    in0=h3[tt][:, :, part, :],
+                    in1=gate[tt][:, :, part, :],
+                )
         g_grouped = {}
         for tt in range(TOKEN_TILES):
             g_turned = turn_psum.tile([P, 2, P], F32, name="g_turned", tag="turn")

@@ -29,7 +29,7 @@ SCALE_ROWS = 16
 LAG = 1
 LEAD = 3
 AHEAD = 0
-HEAD = 5
+HEAD = 4
 WOVEN = 2
 LORA_BLOCKS = TOKEN_TILES + F // P
 LORA_SCALING = 2.0
@@ -66,7 +66,7 @@ def tile_feedforward_pa_k_kernel(
         sorted_pool = ctx.enter_context(tc.tile_pool(name="sorted_pool", bufs=3))
         grouped_pool = ctx.enter_context(tc.tile_pool(name="grouped_pool", bufs=3))
         codes_pool = ctx.enter_context(tc.tile_pool(name="codes_pool", bufs=UNITS))
-        w_pool = ctx.enter_context(tc.tile_pool(name="w_pool", bufs=5))
+        w_pool = ctx.enter_context(tc.tile_pool(name="w_pool", bufs=7))
         turn_psum = ctx.enter_context(tc.psum_pool(name="turn_psum", bufs=4))
         acc_psum = ctx.enter_context(tc.psum_pool(name="acc_psum", bufs=1))
         ctx.enter_context(tc.manual_schedule())
@@ -84,19 +84,19 @@ def tile_feedforward_pa_k_kernel(
         acc = {}
         gate = {}
 
-        def stage_scale_rows():
-            for w, branch in enumerate(branches):
-                nc.sync.dma_start(
-                    out=staged[32 + w : 96 : 4, :, :, :].rearrange("i a r n -> i a (r n)"),
-                    in_=scales_of[branch]
-                    .bitcast(I32)
-                    .rearrange("(a j) (c r) n -> (j c) a (r n)", j=OFFSETS, r=4),
-                )
-
-        def spread_scale_rows(branch, quadrant):
-            first = 32 + 4 * quadrant + branches.index(branch)
+        def stage_scale_rows(branch, half):
+            first = 32 + 2 * branches.index(branch) + half
             nc.sync.dma_start(
-                out=planes[branch][32 * quadrant : 32 * quadrant + 16, :, :]
+                out=staged[first:96:4, :, :, :].rearrange("i a r n -> i a (r n)"),
+                in_=scales_of[branch]
+                .bitcast(I32)[half * GROUPS // 2 : (half + 1) * GROUPS // 2]
+                .rearrange("(a j) (c r) n -> (j c) a (r n)", j=OFFSETS, r=4),
+            )
+
+        def spread_scale_rows(branch, half, quadrant):
+            first = 32 + 4 * quadrant + 2 * branches.index(branch) + half
+            nc.sync.dma_start(
+                out=planes[branch][32 * quadrant : 32 * quadrant + 16, 4 * half : 4 * half + 4, :]
                 .rearrange("p a n -> p (a n)")
                 .bitcast(I32),
                 in_=regrouped[first:96:16, :, :, :].rearrange("j r a n -> j r (a n)"),
@@ -147,7 +147,8 @@ def tile_feedforward_pa_k_kernel(
             words = x_raw[unit][:].bitcast(F32).rearrange("s (g p u) -> s g u p", g=ROUND_GROUPS, u=2)
             count = unit_piece(unit)
             for i in range(0, ROUND_GROUPS, count):
-                nc.vector.tensor_copy(
+                sort = nc.scalar.copy if unit < 3 else nc.vector.tensor_copy
+                sort(
                     out=x_sorted[unit][:, i : i + count, :, :], in_=words[:, i : i + count, :, :]
                 )
 
@@ -247,9 +248,8 @@ def tile_feedforward_pa_k_kernel(
         table_out = keep.tile([P, 1], F32, name="table_out")
         nc.vector.memset(table_in[:], 0.0)
         nc.scalar.activation(out=table_out[:], in_=table_in[:], func=SILU)
-        staged = keep.tile([P, GROUPS // OFFSETS, 4, F // 4], I32, name="staged")
-        regrouped = keep.tile([P, 4, GROUPS // OFFSETS, F // 4], I32, name="regrouped")
-        nc.vector.memset(staged[:], 0)
+        staged = keep.tile([P, 4, 4, F // 4], I32, name="staged")
+        regrouped = keep.tile([P, 4, 4, F // 4], I32, name="regrouped")
         for branch in branches:
             planes[branch] = keep.tile(
                 [P, GROUPS // OFFSETS, F], U8, name="planes_" + branch, align_bytes=64
@@ -290,21 +290,34 @@ def tile_feedforward_pa_k_kernel(
                     )
 
         for unit in range(HEAD):
+            if unit == 1:
+                for branch in branches:
+                    for half in range(2):
+                        stage_scale_rows(branch, half)
             load_x(unit)
             if unit == 1:
-                stage_scale_rows()
                 load_lora()
         load_step(0)
-        for unit in range(2):
+        for unit in range(0):
             sort_x(unit)
-        nc.vector.tensor_copy(out=regrouped[:], in_=staged[:].rearrange("p a r n -> p r a n"))
-        for quadrants in ((2, 3), (0, 1)):
-            for branch in branches:
-                for quadrant in quadrants:
-                    spread_scale_rows(branch, quadrant)
+        for rows in (slice(32, 64), slice(64, 96)):
+            nc.vector.tensor_copy(
+                out=regrouped[rows, :, :, :], in_=staged[rows, :, :, :].rearrange("p a r n -> p r a n")
+            )
+        spreads = [
+            (branch, half, quadrant)
+            for half, quadrants, these in ((0, (2, 3), branches), (0, (0, 1), branches[:1]), (1, (2, 3), branches), (0, (0, 1), branches[1:]), (1, (0, 1), branches))
+            for branch in these
+            for quadrant in quadrants
+        ]
+        for spread in spreads[:11]:
+            spread_scale_rows(*spread)
         load_step(1)
+        for spread in spreads[11:]:
+            spread_scale_rows(*spread)
+        sort_x(0)
         for unit in range(HEAD):
-            if 2 <= unit + 1 < HEAD:
+            if 1 <= unit + 1 < HEAD:
                 sort_x(unit + 1)
             turn_x(unit)
             quantise_x(unit)

@@ -306,14 +306,14 @@ def tile_feedforward_pa_k_kernel(
             )
         spreads = [
             (branch, half, quadrant)
-            for half, quadrants, these in ((0, (2, 3), branches), (0, (0, 1), branches[:1]), (1, (2, 3), branches), (0, (0, 1), branches[1:]), (1, (0, 1), branches))
+            for half, quadrants, these in ((0, (2, 3), branches), (1, (2, 3), branches), (0, (0, 1), branches), (1, (0, 1), branches))
             for branch in these
             for quadrant in quadrants
         ]
-        for spread in spreads[:11]:
+        for spread in spreads[:13]:
             spread_scale_rows(*spread)
         load_step(1)
-        for spread in spreads[11:]:
+        for spread in spreads[13:]:
             spread_scale_rows(*spread)
         sort_x(0)
         for unit in range(HEAD):

@@ -30,7 +30,7 @@ LAG = 1
 LEAD = 3
 AHEAD = 0
 HEAD = 4
-WOVEN = 2
+WOVEN = 1
 LORA_BLOCKS = TOKEN_TILES + F // P
 LORA_SCALING = 2.0
 HALF = F // 2
@@ -102,6 +102,13 @@ def tile_feedforward_pa_k_kernel(
                 in_=regrouped[first:96:16, :, :, :].rearrange("j r a n -> j r (a n)"),
             )
 
+        waiting = []
+
+        def weave_spreads(count=WOVEN):
+            for spread in waiting[:count]:
+                spread_scale_rows(*spread)
+                waiting.remove(spread)
+
         def unit_piece(unit):
             return 4 if unit == UNITS - 1 else ROUND_GROUPS
 
@@ -112,6 +119,7 @@ def tile_feedforward_pa_k_kernel(
             for i in range(0, ROUND_COLS, width):
                 first = rnd * ROUND_COLS + i
                 nc.sync.dma_start(out=x_raw[unit][:, i : i + width], in_=x[tt, :, first : first + width])
+            weave_spreads()
 
         def load_w(rnd, branch, count):
             words = w_pool.tile(
@@ -125,6 +133,7 @@ def tile_feedforward_pa_k_kernel(
                     .rearrange("g p n t -> p g (n t)")
                     .bitcast(I32),
                 )
+                weave_spreads()
             w_round[(rnd, branch)] = words
 
         def load_lora():
@@ -310,11 +319,9 @@ def tile_feedforward_pa_k_kernel(
             for branch in these
             for quadrant in quadrants
         ]
-        for spread in spreads[:13]:
-            spread_scale_rows(*spread)
+        waiting.extend(spreads)
+        weave_spreads(10)
         load_step(1)
-        for spread in spreads[13:]:
-            spread_scale_rows(*spread)
         sort_x(0)
         for unit in range(HEAD):
             if 1 <= unit + 1 < HEAD:

@@ -110,7 +110,7 @@ def tile_feedforward_pa_k_kernel(
                 waiting.remove(spread)
 
         def unit_piece(unit):
-            return 4 if unit == UNITS - 1 else ROUND_GROUPS
+            return 2 if unit == UNITS - 1 else ROUND_GROUPS
 
         def load_x(unit):
             rnd, tt = divmod(unit, TOKEN_TILES)
@@ -282,9 +282,16 @@ def tile_feedforward_pa_k_kernel(
             if i >= LAG:
                 steps.append((i - LAG, "w3"))
 
+        def units_of(step):
+            if step >= 99:
+                return range(step + 3, min(step + 4, UNITS))
+            if step % 2 or step == 0:
+                return range(0)
+            return range(step + 2, min(step + 4, UNITS))
+
         def load_step(step):
-            if HEAD <= step + LEAD + AHEAD < UNITS:
-                load_x(step + LEAD + AHEAD)
+            for unit in units_of(step):
+                load_x(unit)
             left = len(steps) - step
             load_w(*steps[step], 1 if left <= 1 else 2 if left <= 7 else ROUND_GROUPS)
             if left == 1:
@@ -332,15 +339,21 @@ def tile_feedforward_pa_k_kernel(
                 transpose_lora()
                 multiply_lora()
 
+        late = []
         for step, (rnd, branch) in enumerate(steps[:-1]):
             if step + 2 < len(steps):
                 load_step(step + 2)
-            if HEAD <= step + LEAD + AHEAD < UNITS:
-                sort_x(step + LEAD + AHEAD)
-            if HEAD < step + LEAD <= UNITS:
-                quantise_x(step + LEAD - 1)
-            if HEAD <= step + LEAD < UNITS:
-                turn_x(step + LEAD)
+            for unit in units_of(step):
+                sort_x(unit)
+            for unit in late:
+                quantise_x(unit)
+            late.clear()
+            for unit in units_of(step):
+                turn_x(unit)
+                if unit + 1 in units_of(step):
+                    quantise_x(unit)
+                else:
+                    late.append(unit)
             multiply(rnd, branch)
             if (rnd, branch) == (ROUNDS - 1, "w1"):
                 for tt in range(TOKEN_TILES):

@@ -83,6 +83,7 @@ def tile_feedforward_pa_k_kernel(
         lora_term = {}
         acc = {}
         gate = {}
+        gated_lora = {}
 
         def stage_scale_rows(branch, half):
             first = 32 + 2 * branches.index(branch) + half
@@ -197,7 +198,7 @@ def tile_feedforward_pa_k_kernel(
             x_codes[unit] = codes
             x_scales[unit] = scales
 
-        closing = {"w1": GROUPS - 1, "w3": GROUPS - ROUND_GROUPS - 1}
+        closing = {"w1": GROUPS - 1, "w3": GROUPS - 1}
 
         def multiply(rnd, branch):
             for pair in range(0, ROUND_GROUPS, 2):
@@ -245,11 +246,11 @@ def tile_feedforward_pa_k_kernel(
                         stop=True,
                     )
                     lora_term[(branch, tt)] = keep.tile(
-                        [P, 2, P, 2], F32, name="lora_term_%s_%d" % (branch, tt)
+                        [P, PACK, P], F32, name="lora_term_%s_%d" % (branch, tt)
                     )
                     nc.scalar.mul(
                         out=lora_term[(branch, tt)][:],
-                        in_=product[:].rearrange("s (u e) p -> s u p e", u=2),
+                        in_=product[:],
                         mul=LORA_SCALING,
                     )
 
@@ -340,7 +341,7 @@ def tile_feedforward_pa_k_kernel(
                 multiply_lora()
 
         late = []
-        for step, (rnd, branch) in enumerate(steps[:-1]):
+        for step, (rnd, branch) in enumerate(steps):
             if step + 2 < len(steps):
                 load_step(step + 2)
             for unit in units_of(step):
@@ -357,78 +358,55 @@ def tile_feedforward_pa_k_kernel(
             multiply(rnd, branch)
             if (rnd, branch) == (ROUNDS - 1, "w1"):
                 for tt in range(TOKEN_TILES):
-                    h1 = keep.tile([P, 2, P, 2], F32, name="h1_%d" % tt)
+                    h1 = keep.tile([P, PACK, P], F32, name="h1_%d" % tt)
                     nc.vector.tensor_add(
                         out=h1[:],
-                        in0=acc[("w1", tt)][:].rearrange("s (p u e) -> s u p e", u=2, e=2),
+                        in0=acc[("w1", tt)][:].rearrange("s (p t) -> s t p", t=PACK),
                         in1=lora_term[("w1", tt)][:],
                     )
-                    gate[tt] = keep.tile([P, 2, P, 2], F32, name="gate_%d" % tt)
+                    gate[tt] = keep.tile([P, PACK, P], F32, name="gate_%d" % tt)
                     nc.scalar.activation(out=gate[tt][:], in_=h1[:], func=SILU)
-
-        h3 = {}
-        h3_part = {}
-        g_sorted = {}
-        for tt in range(TOKEN_TILES):
-            h3_part[tt] = keep.tile([P, 2, P, 2], F32, name="h3_part_%d" % tt)
-            nc.vector.tensor_add(
-                out=h3_part[tt][:],
-                in0=acc[("w3", tt)][:].rearrange("s (p u e) -> s u p e", u=2, e=2),
-                in1=lora_term[("w3", tt)][:],
-            )
-            h3[tt] = keep.tile([P, 2, P, 2], F32, name="h3_%d" % tt)
-            g_sorted[tt] = keep.tile([P, 2, P, 2], BF16, name="g_sorted_%d" % tt)
-        for half in range(2):
-            rest = {}
-            for tt in range(TOKEN_TILES):
-                rest[tt] = turn_psum.tile([P, HALF], F32, name="rest", tag="turn")
-            for locals_ in ((0, 1, 2), (3,)):
                 for tt in range(TOKEN_TILES):
-                    for local in locals_:
-                        column, offset = divmod(GROUPS - ROUND_GROUPS + local, OFFSETS)
-                        nc.tensor.matmul_mx(
-                            out=rest[tt][:],
-                            lhsT=x_codes[UNITS - TOKEN_TILES + tt][:, local, :].bitcast(FP8X4),
-                            lhsT_scale=x_scales[UNITS - TOKEN_TILES + tt][:, local, :],
-                            rhs=w_round[steps[-1]][
-                                :, local, half * HALF : (half + 1) * HALF
-                            ].bitcast(FP8X4),
-                            rhs_scale=planes["w3"][
-                                4 * offset : P, column, half * HALF : (half + 1) * HALF
-                            ],
-                            start=(local == 0),
-                            stop=(local == ROUND_GROUPS - 1),
-                        )
-            part = slice(half * P // 2, (half + 1) * P // 2)
-            for tt in range(TOKEN_TILES):
-                nc.vector.tensor_add(
-                    out=h3[tt][:, :, part, :],
-                    in0=rest[tt][:].rearrange("s (p u e) -> s u p e", u=2, e=2),
-                    in1=h3_part[tt][:, :, part, :],
-                )
-            for tt in range(TOKEN_TILES):
-                nc.vector.tensor_mul(
-                    out=g_sorted[tt][:, :, part, :],
-                    in0=h3[tt][:, :, part, :],
-                    in1=gate[tt][:, :, part, :],
-                )
+                    gated_lora[tt] = keep.tile([P, PACK, P], F32, name="gated_lora_%d" % tt)
+                    nc.vector.tensor_mul(
+                        out=gated_lora[tt][:], in0=gate[tt][:], in1=lora_term[("w3", tt)][:]
+                    )
+
+        gated_sum = {}
+        g_turned = {}
         g_grouped = {}
+
+        def turn_term(tt, term, first):
+            for t in range(PACK):
+                nc.tensor.matmul(
+                    out=g_turned[tt][:, t, :],
+                    lhsT=term[:, t, :],
+                    rhs=identity_f32[:],
+                    start=(first and t == 0),
+                    stop=(not first and t == PACK - 1),
+                    is_transpose=True,
+                )
+
         for tt in range(TOKEN_TILES):
-            g_turned = turn_psum.tile([P, 2, P], F32, name="g_turned", tag="turn")
-            g_words = g_sorted[tt][:].rearrange("s u p e -> s u (p e)").bitcast(F32)
-            for u in range(2):
-                nc.tensor.transpose(g_turned[:, u, :], g_words[:, u, :], identity_f32[:])
-            g_grouped[tt] = keep.tile([P, P, PACK], BF16, name="g_grouped_%d" % tt, align_bytes=64)
-            nc.scalar.copy(
-                out=g_grouped[tt][:].bitcast(F32), in_=g_turned[:].rearrange("p u s -> p s u")
+            gated_sum[tt] = keep.tile([P, PACK, P], F32, name="gated_sum_%d" % tt)
+            nc.vector.tensor_mul(
+                out=gated_sum[tt][:],
+                in0=acc[("w3", tt)][:].rearrange("s (p t) -> s t p", t=PACK),
+                in1=gate[tt][:],
             )
+            g_turned[tt] = turn_psum.tile([P, PACK, P], F32, name="g_turned", tag="turn")
+            turn_term(tt, gated_lora[tt], True)
+        for tt in range(TOKEN_TILES):
+            turn_term(tt, gated_sum[tt], False)
+            g_grouped[tt] = keep.tile([P, P, PACK], BF16, name="g_grouped_%d" % tt, align_bytes=64)
+            nc.scalar.copy(out=g_grouped[tt][:], in_=g_turned[tt][:].rearrange("p t s -> p s t"))
 
         def store_g(tt):
             g = keep.tile([P, F], F32, name="g_%d" % tt)
-            nc.vector.tensor_mul(
-                out=g[:].rearrange("s (p u e) -> s p u e", u=2, e=2),
-                in0=h3[tt][:].rearrange("s u p e -> s p u e"),
-                in1=gate[tt][:].rearrange("s u p e -> s p u e"),
+            nc.vector.tensor_add(
+                out=g[:].rearrange("s (p t) -> s p t", t=PACK),
+                in0=gated_sum[tt][:].rearrange("s t p -> s p t"),
+                in1=gated_lora[tt][:].rearrange("s t p -> s p t"),
             )
             nc.sync.dma_start(out=out_0[tt], in_=g[:])
 

@@ -77,7 +77,6 @@ def tile_feedforward_pa_k_kernel(
         x_codes = {}
         x_scales = {}
         w_round = {}
-        planes = {}
         lora_in = {}
         lora_turned = {}
         lora_term = {}
@@ -85,30 +84,28 @@ def tile_feedforward_pa_k_kernel(
         gate = {}
         gated_lora = {}
 
-        def stage_scale_rows(branch, half):
-            first = 32 + 2 * branches.index(branch) + half
+        def stage_scale_rows(branch, parity, quadrant):
             nc.sync.dma_start(
-                out=staged[first:96:4, :, :, :].rearrange("i a r n -> i a (r n)"),
-                in_=scales_of[branch]
-                .bitcast(I32)[half * GROUPS // 2 : (half + 1) * GROUPS // 2]
-                .rearrange("(a j) (c r) n -> (j c) a (r n)", j=OFFSETS, r=4),
+                out=staged[32:96, quadrant, 2 * branches.index(branch) + parity, :],
+                in_=scales_of[branch].bitcast(I32)[parity:GROUPS:2, 4 * quadrant : 4 * quadrant + 4, :],
             )
 
-        def spread_scale_rows(branch, half, quadrant):
-            first = 32 + 4 * quadrant + 2 * branches.index(branch) + half
+        def spread_scale_rows(span, quadrant):
             nc.sync.dma_start(
-                out=planes[branch][32 * quadrant : 32 * quadrant + 16, 4 * half : 4 * half + 4, :]
-                .rearrange("p a n -> p (a n)")
+                out=planes[32 * quadrant : 32 * quadrant + 16, span, :, :]
+                .rearrange("p c n -> p (c n)")
                 .bitcast(I32),
-                in_=regrouped[first:96:16, :, :, :].rearrange("j r a n -> j r (a n)"),
+                in_=staged[32 + 16 * span : 48 + 16 * span, quadrant, :, :].rearrange("p c n -> p (c n)"),
             )
 
-        waiting = []
+        def stage_quadrant(quadrant):
+            for branch in branches:
+                for parity in range(2):
+                    stage_scale_rows(branch, parity, quadrant)
 
-        def weave_spreads(count=WOVEN):
-            for spread in waiting[:count]:
-                spread_scale_rows(*spread)
-                waiting.remove(spread)
+        def spread_span(span):
+            for quadrant in (0, 2, 1, 3):
+                spread_scale_rows(span, quadrant)
 
         def unit_piece(unit):
             return 2 if unit == UNITS - 1 else ROUND_GROUPS
@@ -120,7 +117,6 @@ def tile_feedforward_pa_k_kernel(
             for i in range(0, ROUND_COLS, width):
                 first = rnd * ROUND_COLS + i
                 nc.sync.dma_start(out=x_raw[unit][:, i : i + width], in_=x[tt, :, first : first + width])
-            weave_spreads()
 
         def load_w(rnd, branch, count):
             words = w_pool.tile(
@@ -134,7 +130,6 @@ def tile_feedforward_pa_k_kernel(
                     .rearrange("g p n t -> p g (n t)")
                     .bitcast(I32),
                 )
-                weave_spreads()
             w_round[(rnd, branch)] = words
 
         def load_lora():
@@ -157,8 +152,7 @@ def tile_feedforward_pa_k_kernel(
             words = x_raw[unit][:].bitcast(F32).rearrange("s (g p u) -> s g u p", g=ROUND_GROUPS, u=2)
             count = unit_piece(unit)
             for i in range(0, ROUND_GROUPS, count):
-                sort = nc.scalar.copy if unit < 3 else nc.vector.tensor_copy
-                sort(
+                nc.vector.tensor_copy(
                     out=x_sorted[unit][:, i : i + count, :, :], in_=words[:, i : i + count, :, :]
                 )
 
@@ -176,7 +170,7 @@ def tile_feedforward_pa_k_kernel(
                             x_sorted[unit][:, bank * BANK_GROUPS + i, u, :],
                             identity_f32[:],
                         )
-                copy_out = nc.scalar.copy if bank % 2 == 0 or unit < HEAD else nc.vector.tensor_copy
+                copy_out = nc.scalar.copy if bank % 2 == 0 else nc.vector.tensor_copy
                 copy_out(
                     out=grouped_words[:, bank * BANK_GROUPS : (bank + 1) * BANK_GROUPS, :, :],
                     in_=turned[:].rearrange("p g u t -> p g t u"),
@@ -205,13 +199,14 @@ def tile_feedforward_pa_k_kernel(
                 for tt in range(TOKEN_TILES):
                     for local in range(pair, pair + 2):
                         group = rnd * ROUND_GROUPS + local
-                        column, offset = divmod(group, OFFSETS)
+                        span, rest = divmod(group, 2 * OFFSETS)
+                        offset, parity = divmod(rest, 2)
                         nc.tensor.matmul_mx(
                             out=acc[(branch, tt)][:],
                             lhsT=x_codes[TOKEN_TILES * rnd + tt][:, local, :].bitcast(FP8X4),
                             lhsT_scale=x_scales[TOKEN_TILES * rnd + tt][:, local, :],
                             rhs=w_round[(rnd, branch)][:, local, :].bitcast(FP8X4),
-                            rhs_scale=planes[branch][4 * offset : P, column, :],
+                            rhs_scale=planes[4 * offset : P, span, 2 * branches.index(branch) + parity, :],
                             start=(group == 0),
                             stop=(group == closing[branch]),
                         )
@@ -259,12 +254,8 @@ def tile_feedforward_pa_k_kernel(
         nc.vector.memset(table_in[:], 0.0)
         nc.scalar.activation(out=table_out[:], in_=table_in[:], func=SILU)
         staged = keep.tile([P, 4, 4, F // 4], I32, name="staged")
-        regrouped = keep.tile([P, 4, 4, F // 4], I32, name="regrouped")
-        for branch in branches:
-            planes[branch] = keep.tile(
-                [P, GROUPS // OFFSETS, F], U8, name="planes_" + branch, align_bytes=64
-            )
-            nc.vector.memset(planes[branch][:].bitcast(I32), 0)
+        planes = keep.tile([P, 4, 4, F], U8, name="planes", align_bytes=64)
+        nc.vector.memset(planes[:].rearrange("p y c n -> p (y c n)").bitcast(I32), 0)
         identity_f32 = keep.tile([P, P], F32, name="identity_f32")
         make_identity(nc, identity_f32[:])
         identity_bf16 = keep.tile([P, P], BF16, name="identity_bf16")
@@ -306,29 +297,14 @@ def tile_feedforward_pa_k_kernel(
                         in_=lora_A2_scales[0].bitcast(I32)[r : 16 : 4, :],
                     )
 
-        for unit in range(HEAD):
-            if unit == 1:
-                for branch in branches:
-                    for half in range(2):
-                        stage_scale_rows(branch, half)
+        load_x(0)
+        for unit in range(1, HEAD):
             load_x(unit)
-            if unit == 1:
-                load_lora()
+            stage_quadrant(unit - 1)
+        load_lora()
+        stage_quadrant(3)
         load_step(0)
-        for unit in range(0):
-            sort_x(unit)
-        for rows in (slice(32, 64), slice(64, 96)):
-            nc.vector.tensor_copy(
-                out=regrouped[rows, :, :, :], in_=staged[rows, :, :, :].rearrange("p a r n -> p r a n")
-            )
-        spreads = [
-            (branch, half, quadrant)
-            for half, quadrants, these in ((0, (2, 3), branches), (1, (2, 3), branches), (0, (0, 1), branches), (1, (0, 1), branches))
-            for branch in these
-            for quadrant in quadrants
-        ]
-        waiting.extend(spreads)
-        weave_spreads(10)
+        spread_span(0)
         load_step(1)
         sort_x(0)
         for unit in range(HEAD):
@@ -342,6 +318,8 @@ def tile_feedforward_pa_k_kernel(
 
         late = []
         for step, (rnd, branch) in enumerate(steps):
+            if step in (0, 4, 8):
+                spread_span(step // 4 + 1)
             if step + 2 < len(steps):
                 load_step(step + 2)
             for unit in units_of(step):

@@ -16,24 +16,24 @@ TOKEN_TILES = 2
 D = 16384
 F = 512
 R = 128
+LORA_SCALING = 2.0
 PACK = 4
 K_PASS = P * PACK
 GROUPS = D // K_PASS
+QUADRANT = 32
+QUADRANTS = P // QUADRANT
+QUADRANT_ROWS = 4
 ROUND_GROUPS = 4
 ROUNDS = GROUPS // ROUND_GROUPS
-ROUND_COLS = K_PASS * ROUND_GROUPS
 UNITS = TOKEN_TILES * ROUNDS
 BANK_GROUPS = 2
-OFFSETS = 4
-SCALE_ROWS = 16
-LAG = 1
-LEAD = 3
-AHEAD = 0
-HEAD = 4
-WOVEN = 1
+HEAD_UNITS = 2 * TOKEN_TILES
+SET_STEPS = 4
+SETS = 2 * ROUNDS // SET_STEPS
+STAGE_FIRST = 32
+STAGE_END = 96
+LOAD_GROUPS = (4, 4, 2, 1)
 LORA_BLOCKS = TOKEN_TILES + F // P
-LORA_SCALING = 2.0
-HALF = F // 2
 
 FLOPS = 2 * TOKEN_TILES * P * (2 * D * F + 2 * R * F + F * R)
 
@@ -60,6 +60,18 @@ def tile_feedforward_pa_k_kernel(
     scales_of = {"w1": w1_scales, "w3": w3_scales}
     lora_inputs = {"w1": (xa1, lora_B1), "w3": (xa3, lora_B3)}
 
+    steps = [("w1", 0)]
+    for rnd in range(1, ROUNDS):
+        steps.extend([("w1", rnd), ("w3", rnd - 1)])
+    steps.append(("w3", ROUNDS - 1))
+    sets = [sorted(steps[i : i + SET_STEPS]) for i in range(0, len(steps), SET_STEPS)]
+    plane_column = {step: i for i, step in enumerate(sum(sets, []))}
+
+    def units_before(index):
+        if steps[index][0] == "w1":
+            return range(0)
+        return range(index + TOKEN_TILES, min(index + 2 * TOKEN_TILES, UNITS))
+
     with ExitStack() as ctx:
         keep = ctx.enter_context(tc.tile_pool(name="keep", bufs=1))
         x_pool = ctx.enter_context(tc.tile_pool(name="x_pool", bufs=6))
@@ -71,66 +83,81 @@ def tile_feedforward_pa_k_kernel(
         acc_psum = ctx.enter_context(tc.psum_pool(name="acc_psum", bufs=1))
         ctx.enter_context(tc.manual_schedule())
 
-        x_raw = {}
-        x_sorted = {}
-        x_grouped = {}
-        x_codes = {}
-        x_scales = {}
-        w_round = {}
-        lora_in = {}
-        lora_turned = {}
-        lora_term = {}
+        x_raw, x_sorted, x_grouped, x_codes, x_scales = {}, {}, {}, {}, {}
+        w_words = {}
+        lora_in, lora_turned, lora_term = {}, {}, {}
+        gate, gated_lora, gated_sum, g_turned, g_grouped = {}, {}, {}, {}, {}
+
+        table_in = keep.tile([P, 1], F32, name="table_in")
+        table_out = keep.tile([P, 1], F32, name="table_out")
+        nc.vector.memset(table_in[:], 0.0)
+        nc.scalar.activation(out=table_out[:], in_=table_in[:], func=SILU)
+        staged = keep.tile([P, SET_STEPS, QUADRANT_ROWS, F // 4], I32, name="staged")
+        regrouped = keep.tile([P, QUADRANT_ROWS, SET_STEPS, F // 4], I32, name="regrouped")
+        planes = keep.tile([P, len(steps), F], U8, name="planes", align_bytes=64)
+        nc.vector.memset(planes[:].rearrange("p c n -> p (c n)").bitcast(I32), 0)
+        a2_words = keep.tile([P, R], U32, name="a2_words", align_bytes=64)
+        a2_plane = keep.tile([P, R], U8, name="a2_plane", align_bytes=64)
+        nc.vector.memset(a2_plane[:].bitcast(I32), 0)
+        identity_f32 = keep.tile([P, P], F32, name="identity_f32")
+        make_identity(nc, identity_f32[:])
+        identity_bf16 = keep.tile([P, P], BF16, name="identity_bf16")
+        make_identity(nc, identity_bf16[:])
         acc = {}
-        gate = {}
-        gated_lora = {}
+        for branch in branches:
+            for tt in range(TOKEN_TILES):
+                acc[(branch, tt)] = acc_psum.tile([P, F], F32, name="acc_%s_%d" % (branch, tt))
 
-        def stage_scale_rows(branch, parity, quadrant):
+        def stage_scales(which, branch):
+            rounds = [rnd for name, rnd in sets[which] if name == branch]
+            first = sets[which].index((branch, rounds[0]))
             nc.sync.dma_start(
-                out=staged[32:96, quadrant, 2 * branches.index(branch) + parity, :],
-                in_=scales_of[branch].bitcast(I32)[parity:GROUPS:2, 4 * quadrant : 4 * quadrant + 4, :],
+                out=staged[STAGE_FIRST + which : STAGE_END : SETS, first : first + len(rounds), :, :]
+                .rearrange("i c r n -> i c (r n)"),
+                in_=scales_of[branch]
+                .bitcast(I32)[rounds[0] * ROUND_GROUPS : (rounds[-1] + 1) * ROUND_GROUPS]
+                .rearrange("(c j) (q r) n -> (j q) c (r n)", j=ROUND_GROUPS, r=QUADRANT_ROWS),
             )
 
-        def spread_scale_rows(span, quadrant):
-            nc.sync.dma_start(
-                out=planes[32 * quadrant : 32 * quadrant + 16, span, :, :]
-                .rearrange("p c n -> p (c n)")
-                .bitcast(I32),
-                in_=staged[32 + 16 * span : 48 + 16 * span, quadrant, :, :].rearrange("p c n -> p (c n)"),
-            )
+        def regroup_scales():
+            for first in range(STAGE_FIRST, STAGE_END, QUADRANT):
+                rows = slice(first, first + QUADRANT)
+                nc.vector.tensor_copy(
+                    out=regrouped[rows, :, :, :],
+                    in_=staged[rows, :, :, :].rearrange("p c r n -> p r c n"),
+                )
 
-        def stage_quadrant(quadrant):
-            for branch in branches:
-                for parity in range(2):
-                    stage_scale_rows(branch, parity, quadrant)
+        def spread_scales(which, quadrants):
+            for quadrant in quadrants:
+                first = STAGE_FIRST + SETS * quadrant + which
+                live = slice(QUADRANT * quadrant, QUADRANT * quadrant + ROUND_GROUPS * QUADRANT_ROWS)
+                nc.sync.dma_start(
+                    out=planes[live, SET_STEPS * which : SET_STEPS * (which + 1), :]
+                    .rearrange("p c n -> p (c n)")
+                    .bitcast(I32),
+                    in_=regrouped[first : STAGE_END : SETS * QUADRANTS, :, :, :].rearrange(
+                        "j r c n -> j r (c n)"
+                    ),
+                )
 
-        def spread_span(span):
-            for quadrant in (0, 2, 1, 3):
-                spread_scale_rows(span, quadrant)
+        lower_quadrants = range(QUADRANTS // 2)
+        upper_quadrants = range(QUADRANTS // 2, QUADRANTS)
 
-        def unit_piece(unit):
-            return 2 if unit == UNITS - 1 else ROUND_GROUPS
+        def pieces_of(unit):
+            count = BANK_GROUPS if unit == UNITS - 1 else ROUND_GROUPS
+            return [slice(i, i + count) for i in range(0, ROUND_GROUPS, count)]
 
         def load_x(unit):
             rnd, tt = divmod(unit, TOKEN_TILES)
-            x_raw[unit] = x_pool.tile([P, ROUND_COLS], BF16, name="x_raw", tag="x_raw")
-            width = K_PASS * unit_piece(unit)
-            for i in range(0, ROUND_COLS, width):
-                first = rnd * ROUND_COLS + i
-                nc.sync.dma_start(out=x_raw[unit][:, i : i + width], in_=x[tt, :, first : first + width])
-
-        def load_w(rnd, branch, count):
-            words = w_pool.tile(
-                [P, ROUND_GROUPS, F], U32, name="w_words", tag="w_words", align_bytes=64
-            )
-            for i in range(0, ROUND_GROUPS, count):
-                first = rnd * ROUND_GROUPS + i
+            x_raw[unit] = x_pool.tile([P, ROUND_GROUPS, K_PASS], BF16, name="x_raw", tag="x_raw")
+            source = x[tt].rearrange("s (g k) -> s g k", k=K_PASS)[
+                :, rnd * ROUND_GROUPS : (rnd + 1) * ROUND_GROUPS, :
+            ]
+            for piece in pieces_of(unit):
                 nc.sync.dma_start(
-                    out=words[:, i : i + count, :].bitcast(I32),
-                    in_=words_of[branch][first : first + count]
-                    .rearrange("g p n t -> p g (n t)")
-                    .bitcast(I32),
+                    out=x_raw[unit][:, piece, :].rearrange("s g k -> s (g k)"),
+                    in_=source[:, piece, :].rearrange("s g k -> s (g k)"),
                 )
-            w_round[(rnd, branch)] = words
 
         def load_lora():
             for branch in branches:
@@ -145,75 +172,97 @@ def tile_feedforward_pa_k_kernel(
                     in_=lora_b.rearrange("(p t) r -> p t r", t=PACK),
                 )
 
-        def sort_x(unit):
-            x_sorted[unit] = sorted_pool.tile(
-                [P, ROUND_GROUPS, 2, P], F32, name="sorted_words", tag="sorted_words"
+        def load_step(index):
+            for unit in units_before(index):
+                load_x(unit)
+            which, place = divmod(index, SET_STEPS)
+            if which > 0 and place == 0:
+                spread_scales(which, lower_quadrants)
+            branch, rnd = steps[index]
+            words = w_pool.tile(
+                [P, ROUND_GROUPS, F], U32, name="w_words", tag="w_words", align_bytes=64
             )
-            words = x_raw[unit][:].bitcast(F32).rearrange("s (g p u) -> s g u p", g=ROUND_GROUPS, u=2)
-            count = unit_piece(unit)
+            count = LOAD_GROUPS[which]
             for i in range(0, ROUND_GROUPS, count):
-                nc.vector.tensor_copy(
-                    out=x_sorted[unit][:, i : i + count, :, :], in_=words[:, i : i + count, :, :]
+                first = rnd * ROUND_GROUPS + i
+                nc.sync.dma_start(
+                    out=words[:, i : i + count, :].bitcast(I32),
+                    in_=words_of[branch][first : first + count]
+                    .rearrange("g p n t -> p g (n t)")
+                    .bitcast(I32),
+                )
+            w_words[steps[index]] = words
+
+        def load_a2():
+            nc.sync.dma_start(
+                out=a2_words[:].bitcast(I32),
+                in_=lora_A2_words[0].rearrange("p n t -> p (n t)").bitcast(I32),
+            )
+            for r in range(QUADRANT_ROWS):
+                nc.sync.dma_start(
+                    out=a2_plane[r:P:QUADRANT, :].bitcast(I32),
+                    in_=lora_A2_scales[0].bitcast(I32)[r :: QUADRANT_ROWS, :],
                 )
 
-        def turn_x(unit):
-            grouped = grouped_pool.tile(
-                [P, ROUND_GROUPS, P, PACK], BF16, name="grouped", tag="grouped", align_bytes=64
+        def sort_x(unit, copy):
+            x_sorted[unit] = sorted_pool.tile(
+                [P, ROUND_GROUPS, 2, P], F32, name="x_sorted", tag="x_sorted"
             )
-            grouped_words = grouped[:].bitcast(F32)
-            for bank in range(ROUND_GROUPS // BANK_GROUPS):
-                turned = turn_psum.tile([P, BANK_GROUPS, 2, P], F32, name="turned", tag="turn")
+            pairs = x_raw[unit][:].bitcast(F32).rearrange("s g (p u) -> s g u p", u=2)
+            for piece in pieces_of(unit):
+                copy(out=x_sorted[unit][:, piece, :, :], in_=pairs[:, piece, :, :])
+
+        def turn_x(unit, copies):
+            grouped = grouped_pool.tile(
+                [P, ROUND_GROUPS, P, PACK], BF16, name="x_grouped", tag="x_grouped", align_bytes=64
+            )
+            for bank, copy in enumerate(copies):
+                first = bank * BANK_GROUPS
+                turned = turn_psum.tile([P, BANK_GROUPS, 2, P], F32, name="x_turned", tag="turn")
                 for i in range(BANK_GROUPS):
                     for u in range(2):
                         nc.tensor.transpose(
-                            turned[:, i, u, :],
-                            x_sorted[unit][:, bank * BANK_GROUPS + i, u, :],
-                            identity_f32[:],
+                            turned[:, i, u, :], x_sorted[unit][:, first + i, u, :], identity_f32[:]
                         )
-                copy_out = nc.scalar.copy if bank % 2 == 0 else nc.vector.tensor_copy
-                copy_out(
-                    out=grouped_words[:, bank * BANK_GROUPS : (bank + 1) * BANK_GROUPS, :, :],
-                    in_=turned[:].rearrange("p g u t -> p g t u"),
+                copy(
+                    out=grouped[:].bitcast(F32)[:, first : first + BANK_GROUPS, :, :],
+                    in_=turned[:].rearrange("p g u s -> p g s u"),
                 )
             x_grouped[unit] = grouped
 
         def quantise_x(unit):
-            codes = codes_pool.tile(
+            x_codes[unit] = codes_pool.tile(
                 [P, ROUND_GROUPS, P], U32, name="x_codes", tag="x_codes", align_bytes=64
             )
-            scales = codes_pool.tile(
+            x_scales[unit] = codes_pool.tile(
                 [P, ROUND_GROUPS, P], U8, name="x_scales", tag="x_scales", align_bytes=64
             )
             nc.vector.quantize_mx(
-                out=codes[:].rearrange("p g t -> p (g t)").bitcast(FP8X4),
-                scales=scales[:].rearrange("p g t -> p (g t)"),
-                in_=x_grouped[unit][:].rearrange("p g t j -> p (g t j)"),
+                out=x_codes[unit][:].rearrange("p g s -> p (g s)").bitcast(FP8X4),
+                scales=x_scales[unit][:].rearrange("p g s -> p (g s)"),
+                in_=x_grouped[unit][:].rearrange("p g s t -> p (g s t)"),
             )
-            x_codes[unit] = codes
-            x_scales[unit] = scales
 
-        closing = {"w1": GROUPS - 1, "w3": GROUPS - 1}
-
-        def multiply(rnd, branch):
+        def multiply(branch, rnd):
+            column = plane_column[(branch, rnd)]
             for pair in range(0, ROUND_GROUPS, 2):
                 for tt in range(TOKEN_TILES):
+                    unit = TOKEN_TILES * rnd + tt
                     for local in range(pair, pair + 2):
                         group = rnd * ROUND_GROUPS + local
-                        span, rest = divmod(group, 2 * OFFSETS)
-                        offset, parity = divmod(rest, 2)
                         nc.tensor.matmul_mx(
                             out=acc[(branch, tt)][:],
-                            lhsT=x_codes[TOKEN_TILES * rnd + tt][:, local, :].bitcast(FP8X4),
-                            lhsT_scale=x_scales[TOKEN_TILES * rnd + tt][:, local, :],
-                            rhs=w_round[(rnd, branch)][:, local, :].bitcast(FP8X4),
-                            rhs_scale=planes[4 * offset : P, span, 2 * branches.index(branch) + parity, :],
+                            lhsT=x_codes[unit][:, local, :].bitcast(FP8X4),
+                            lhsT_scale=x_scales[unit][:, local, :],
+                            rhs=w_words[(branch, rnd)][:, local, :].bitcast(FP8X4),
+                            rhs_scale=planes[QUADRANT_ROWS * local : P, column, :],
                             start=(group == 0),
-                            stop=(group == closing[branch]),
+                            stop=(group == GROUPS - 1),
                         )
 
-        def transpose_lora():
+        def turn_lora():
             for branch in branches:
-                turned = turn_psum.tile([P, LORA_BLOCKS, P], BF16, name="lora_ps", tag="turn")
+                turned = turn_psum.tile([P, LORA_BLOCKS, P], BF16, name="lora_psum", tag="turn")
                 for i in range(LORA_BLOCKS):
                     nc.tensor.transpose(turned[:, i, :], lora_in[branch][:, i, :], identity_bf16[:])
                 lora_turned[branch] = keep.tile(
@@ -232,7 +281,7 @@ def tile_feedforward_pa_k_kernel(
         def multiply_lora():
             for branch in branches:
                 for tt in range(TOKEN_TILES):
-                    product = turn_psum.tile([P, PACK, P], F32, name="product", tag="turn")
+                    product = turn_psum.tile([P, PACK, P], F32, name="lora_product", tag="turn")
                     nc.tensor.matmul(
                         out=product[:].rearrange("s t p -> s (t p)"),
                         lhsT=lora_turned[branch][:, tt, :],
@@ -243,127 +292,69 @@ def tile_feedforward_pa_k_kernel(
                     lora_term[(branch, tt)] = keep.tile(
                         [P, PACK, P], F32, name="lora_term_%s_%d" % (branch, tt)
                     )
-                    nc.scalar.mul(
-                        out=lora_term[(branch, tt)][:],
-                        in_=product[:],
-                        mul=LORA_SCALING,
-                    )
+                    nc.scalar.mul(out=lora_term[(branch, tt)][:], in_=product[:], mul=LORA_SCALING)
 
-        table_in = keep.tile([P, 1], F32, name="table_in")
-        table_out = keep.tile([P, 1], F32, name="table_out")
-        nc.vector.memset(table_in[:], 0.0)
-        nc.scalar.activation(out=table_out[:], in_=table_in[:], func=SILU)
-        staged = keep.tile([P, 4, 4, F // 4], I32, name="staged")
-        planes = keep.tile([P, 4, 4, F], U8, name="planes", align_bytes=64)
-        nc.vector.memset(planes[:].rearrange("p y c n -> p (y c n)").bitcast(I32), 0)
-        identity_f32 = keep.tile([P, P], F32, name="identity_f32")
-        make_identity(nc, identity_f32[:])
-        identity_bf16 = keep.tile([P, P], BF16, name="identity_bf16")
-        make_identity(nc, identity_bf16[:])
-        for branch in branches:
+        def make_gate():
             for tt in range(TOKEN_TILES):
-                acc[(branch, tt)] = acc_psum.tile([P, F], F32, name="acc_%s_%d" % (branch, tt))
-        a2_words = keep.tile([P, R], U32, name="a2_words", align_bytes=64)
-        a2_plane = keep.tile([P, R], U8, name="a2_plane", align_bytes=64)
-        nc.vector.memset(a2_plane[:].bitcast(I32), 0)
-
-        steps = []
-        for i in range(ROUNDS + LAG):
-            if i < ROUNDS:
-                steps.append((i, "w1"))
-            if i >= LAG:
-                steps.append((i - LAG, "w3"))
-
-        def units_of(step):
-            if step >= 99:
-                return range(step + 3, min(step + 4, UNITS))
-            if step % 2 or step == 0:
-                return range(0)
-            return range(step + 2, min(step + 4, UNITS))
-
-        def load_step(step):
-            for unit in units_of(step):
-                load_x(unit)
-            left = len(steps) - step
-            load_w(*steps[step], 1 if left <= 1 else 2 if left <= 7 else ROUND_GROUPS)
-            if left == 1:
-                nc.sync.dma_start(
-                    out=a2_words[:].bitcast(I32),
-                    in_=lora_A2_words[0].rearrange("p n t -> p (n t)").bitcast(I32),
+                h1 = keep.tile([P, PACK, P], F32, name="h1_%d" % tt)
+                nc.vector.tensor_add(
+                    out=h1[:],
+                    in0=acc[("w1", tt)][:].rearrange("s (p t) -> s t p", t=PACK),
+                    in1=lora_term[("w1", tt)][:],
                 )
-                for r in range(4):
-                    nc.sync.dma_start(
-                        out=a2_plane[r : P : 32, :].bitcast(I32),
-                        in_=lora_A2_scales[0].bitcast(I32)[r : 16 : 4, :],
-                    )
+                gate[tt] = keep.tile([P, PACK, P], F32, name="gate_%d" % tt)
+                nc.scalar.activation(out=gate[tt][:], in_=h1[:], func=SILU)
+            for tt in range(TOKEN_TILES):
+                gated_lora[tt] = keep.tile([P, PACK, P], F32, name="gated_lora_%d" % tt)
+                nc.vector.tensor_mul(
+                    out=gated_lora[tt][:], in0=gate[tt][:], in1=lora_term[("w3", tt)][:]
+                )
 
-        load_x(0)
-        for unit in range(1, HEAD):
-            load_x(unit)
-            stage_quadrant(unit - 1)
+        on_scalar, on_vector = nc.scalar.copy, nc.vector.tensor_copy
+        for which in range(SETS):
+            if which == SETS - 1:
+                load_x(0)
+            for branch in branches:
+                stage_scales(which, branch)
+        load_x(1)
         load_lora()
-        stage_quadrant(3)
+        load_x(2)
+        load_x(3)
         load_step(0)
-        spread_span(0)
+        regroup_scales()
+        for which in range(SETS):
+            spread_scales(which, upper_quadrants)
+        spread_scales(0, lower_quadrants)
         load_step(1)
-        sort_x(0)
-        for unit in range(HEAD):
-            if 1 <= unit + 1 < HEAD:
-                sort_x(unit + 1)
-            turn_x(unit)
-            quantise_x(unit)
-            if unit == 1:
-                transpose_lora()
-                multiply_lora()
 
-        late = []
-        for step, (rnd, branch) in enumerate(steps):
-            if step in (0, 4, 8):
-                spread_span(step // 4 + 1)
-            if step + 2 < len(steps):
-                load_step(step + 2)
-            for unit in units_of(step):
-                sort_x(unit)
-            for unit in late:
+        sort_x(0, on_scalar)
+        sort_x(1, on_scalar)
+        turn_x(0, (on_scalar, on_scalar))
+        sort_x(2, on_scalar)
+        turn_x(1, (on_scalar, on_scalar))
+        turn_lora()
+        sort_x(3, on_vector)
+        quantise_x(0)
+        quantise_x(1)
+        turn_x(2, (on_scalar, on_vector))
+        turn_x(3, (on_scalar, on_vector))
+        multiply_lora()
+        quantise_x(2)
+        quantise_x(3)
+
+        for index, (branch, rnd) in enumerate(steps):
+            if index + 2 < len(steps):
+                load_step(index + 2)
+            elif index + 2 == len(steps):
+                load_a2()
+            for unit in units_before(index):
+                sort_x(unit, on_vector)
+            for unit in units_before(index):
+                turn_x(unit, (on_scalar, on_vector))
                 quantise_x(unit)
-            late.clear()
-            for unit in units_of(step):
-                turn_x(unit)
-                if unit + 1 in units_of(step):
-                    quantise_x(unit)
-                else:
-                    late.append(unit)
-            multiply(rnd, branch)
-            if (rnd, branch) == (ROUNDS - 1, "w1"):
-                for tt in range(TOKEN_TILES):
-                    h1 = keep.tile([P, PACK, P], F32, name="h1_%d" % tt)
-                    nc.vector.tensor_add(
-                        out=h1[:],
-                        in0=acc[("w1", tt)][:].rearrange("s (p t) -> s t p", t=PACK),
-                        in1=lora_term[("w1", tt)][:],
-                    )
-                    gate[tt] = keep.tile([P, PACK, P], F32, name="gate_%d" % tt)
-                    nc.scalar.activation(out=gate[tt][:], in_=h1[:], func=SILU)
-                for tt in range(TOKEN_TILES):
-                    gated_lora[tt] = keep.tile([P, PACK, P], F32, name="gated_lora_%d" % tt)
-                    nc.vector.tensor_mul(
-                        out=gated_lora[tt][:], in0=gate[tt][:], in1=lora_term[("w3", tt)][:]
-                    )
-
-        gated_sum = {}
-        g_turned = {}
-        g_grouped = {}
-
-        def turn_term(tt, term, first):
-            for t in range(PACK):
-                nc.tensor.matmul(
-                    out=g_turned[tt][:, t, :],
-                    lhsT=term[:, t, :],
-                    rhs=identity_f32[:],
-                    start=(first and t == 0),
-                    stop=(not first and t == PACK - 1),
-                    is_transpose=True,
-                )
+            multiply(branch, rnd)
+            if (branch, rnd) == ("w1", ROUNDS - 1):
+                make_gate()
 
         for tt in range(TOKEN_TILES):
             gated_sum[tt] = keep.tile([P, PACK, P], F32, name="gated_sum_%d" % tt)
@@ -372,14 +363,22 @@ def tile_feedforward_pa_k_kernel(
                 in0=acc[("w3", tt)][:].rearrange("s (p t) -> s t p", t=PACK),
                 in1=gate[tt][:],
             )
-            g_turned[tt] = turn_psum.tile([P, PACK, P], F32, name="g_turned", tag="turn")
-            turn_term(tt, gated_lora[tt], True)
         for tt in range(TOKEN_TILES):
-            turn_term(tt, gated_sum[tt], False)
+            g_turned[tt] = turn_psum.tile([P, PACK, P], F32, name="g_turned", tag="turn")
+            terms = (gated_lora[tt], gated_sum[tt])
+            for i, term in enumerate(terms):
+                for t in range(PACK):
+                    nc.tensor.matmul(
+                        out=g_turned[tt][:, t, :],
+                        lhsT=term[:, t, :],
+                        rhs=identity_f32[:],
+                        start=(i == 0 and t == 0),
+                        stop=(i == len(terms) - 1 and t == PACK - 1),
+                        is_transpose=True,
+                    )
             g_grouped[tt] = keep.tile([P, P, PACK], BF16, name="g_grouped_%d" % tt, align_bytes=64)
             nc.scalar.copy(out=g_grouped[tt][:], in_=g_turned[tt][:].rearrange("p t s -> p s t"))
-
-        def store_g(tt):
+        for tt in range(TOKEN_TILES):
             g = keep.tile([P, F], F32, name="g_%d" % tt)
             nc.vector.tensor_add(
                 out=g[:].rearrange("s (p t) -> s p t", t=PACK),
@@ -387,8 +386,7 @@ def tile_feedforward_pa_k_kernel(
                 in1=gated_lora[tt][:].rearrange("s t p -> s p t"),
             )
             nc.sync.dma_start(out=out_0[tt], in_=g[:])
-
-        def project_g(tt):
+        for tt in range(TOKEN_TILES):
             g_codes = keep.tile([P, P], U32, name="g_codes_%d" % tt, align_bytes=64)
             g_scales = keep.tile([P, P], U8, name="g_scales_%d" % tt, align_bytes=64)
             nc.vector.quantize_mx(
@@ -409,8 +407,3 @@ def tile_feedforward_pa_k_kernel(
             ga2 = keep.tile([P, R], F32, name="ga2_%d" % tt)
             nc.scalar.copy(out=ga2[:], in_=ga2_psum[:])
             nc.scalar.dma_start(out=out_1[tt], in_=ga2[:])
-
-        store_g(0)
-        store_g(1)
-        project_g(0)
-        project_g(1)

@@ -27,12 +27,12 @@ ROUND_GROUPS = 4
 ROUNDS = GROUPS // ROUND_GROUPS
 UNITS = TOKEN_TILES * ROUNDS
 BANK_GROUPS = 2
-HEAD_UNITS = 2 * TOKEN_TILES
-SET_STEPS = 4
-SETS = 2 * ROUNDS // SET_STEPS
+LAG = 2
+HEAD_ROUNDS = 2
+SETS = 4
+SET_ROUNDS = ROUNDS // 2
 STAGE_FIRST = 32
 STAGE_END = 96
-LOAD_GROUPS = (4, 4, 2, 1)
 LORA_BLOCKS = TOKEN_TILES + F // P
 
 FLOPS = 2 * TOKEN_TILES * P * (2 * D * F + 2 * R * F + F * R)
@@ -60,17 +60,22 @@ def tile_feedforward_pa_k_kernel(
     scales_of = {"w1": w1_scales, "w3": w3_scales}
     lora_inputs = {"w1": (xa1, lora_B1), "w3": (xa3, lora_B3)}
 
-    steps = [("w1", 0)]
-    for rnd in range(1, ROUNDS):
-        steps.extend([("w1", rnd), ("w3", rnd - 1)])
-    steps.append(("w3", ROUNDS - 1))
-    sets = [sorted(steps[i : i + SET_STEPS]) for i in range(0, len(steps), SET_STEPS)]
-    plane_column = {step: i for i, step in enumerate(sum(sets, []))}
+    steps = []
+    for rnd in range(ROUNDS + LAG):
+        if rnd < ROUNDS:
+            steps.append(("w1", rnd))
+        if rnd >= LAG:
+            steps.append(("w3", rnd - LAG))
+    sets = [(branch, half) for branch in branches for half in range(2)]
 
     def units_before(index):
-        if steps[index][0] == "w1":
-            return range(0)
-        return range(index + TOKEN_TILES, min(index + 2 * TOKEN_TILES, UNITS))
+        following = steps[index + 1 : index + 2]
+        rounds = [rnd for branch, rnd in following if branch == "w1" and rnd >= HEAD_ROUNDS]
+        return [TOKEN_TILES * rnd + tt for rnd in rounds for tt in range(TOKEN_TILES)]
+
+    def sets_before(index):
+        ahead = steps[index : index + 2] if units_before(index) else []
+        return [(branch, rnd // SET_ROUNDS) for branch, rnd in ahead if rnd % SET_ROUNDS == 0]
 
     with ExitStack() as ctx:
         keep = ctx.enter_context(tc.tile_pool(name="keep", bufs=1))
@@ -92,10 +97,12 @@ def tile_feedforward_pa_k_kernel(
         table_out = keep.tile([P, 1], F32, name="table_out")
         nc.vector.memset(table_in[:], 0.0)
         nc.scalar.activation(out=table_out[:], in_=table_in[:], func=SILU)
-        staged = keep.tile([P, SET_STEPS, QUADRANT_ROWS, F // 4], I32, name="staged")
-        regrouped = keep.tile([P, QUADRANT_ROWS, SET_STEPS, F // 4], I32, name="regrouped")
-        planes = keep.tile([P, len(steps), F], U8, name="planes", align_bytes=64)
-        nc.vector.memset(planes[:].rearrange("p c n -> p (c n)").bitcast(I32), 0)
+        staged = keep.tile([P, SET_ROUNDS, QUADRANT_ROWS, F // 4], I32, name="staged")
+        regrouped = keep.tile([P, QUADRANT_ROWS, SET_ROUNDS, F // 4], I32, name="regrouped")
+        planes = {}
+        for branch in branches:
+            planes[branch] = keep.tile([P, ROUNDS, F], U8, name="planes_" + branch, align_bytes=64)
+            nc.vector.memset(planes[branch][:].bitcast(I32), 0)
         a2_words = keep.tile([P, R], U32, name="a2_words", align_bytes=64)
         a2_plane = keep.tile([P, R], U8, name="a2_plane", align_bytes=64)
         nc.vector.memset(a2_plane[:].bitcast(I32), 0)
@@ -108,14 +115,12 @@ def tile_feedforward_pa_k_kernel(
             for tt in range(TOKEN_TILES):
                 acc[(branch, tt)] = acc_psum.tile([P, F], F32, name="acc_%s_%d" % (branch, tt))
 
-        def stage_scales(which, branch):
-            rounds = [rnd for name, rnd in sets[which] if name == branch]
-            first = sets[which].index((branch, rounds[0]))
+        def stage_scales(branch, half):
+            first = STAGE_FIRST + sets.index((branch, half))
             nc.sync.dma_start(
-                out=staged[STAGE_FIRST + which : STAGE_END : SETS, first : first + len(rounds), :, :]
-                .rearrange("i c r n -> i c (r n)"),
+                out=staged[first:STAGE_END:SETS, :, :, :].rearrange("i c r n -> i c (r n)"),
                 in_=scales_of[branch]
-                .bitcast(I32)[rounds[0] * ROUND_GROUPS : (rounds[-1] + 1) * ROUND_GROUPS]
+                .bitcast(I32)[half * GROUPS // 2 : (half + 1) * GROUPS // 2]
                 .rearrange("(c j) (q r) n -> (j q) c (r n)", j=ROUND_GROUPS, r=QUADRANT_ROWS),
             )
 
@@ -127,12 +132,12 @@ def tile_feedforward_pa_k_kernel(
                     in_=staged[rows, :, :, :].rearrange("p c r n -> p r c n"),
                 )
 
-        def spread_scales(which, quadrants):
+        def spread_scales(branch, half, quadrants):
             for quadrant in quadrants:
-                first = STAGE_FIRST + SETS * quadrant + which
+                first = STAGE_FIRST + SETS * quadrant + sets.index((branch, half))
                 live = slice(QUADRANT * quadrant, QUADRANT * quadrant + ROUND_GROUPS * QUADRANT_ROWS)
                 nc.sync.dma_start(
-                    out=planes[live, SET_STEPS * which : SET_STEPS * (which + 1), :]
+                    out=planes[branch][live, SET_ROUNDS * half : SET_ROUNDS * (half + 1), :]
                     .rearrange("p c n -> p (c n)")
                     .bitcast(I32),
                     in_=regrouped[first : STAGE_END : SETS * QUADRANTS, :, :, :].rearrange(
@@ -175,14 +180,13 @@ def tile_feedforward_pa_k_kernel(
         def load_step(index):
             for unit in units_before(index):
                 load_x(unit)
-            which, place = divmod(index, SET_STEPS)
-            if which > 0 and place == 0:
-                spread_scales(which, lower_quadrants)
+            for branch, half in sets_before(index):
+                spread_scales(branch, half, lower_quadrants)
             branch, rnd = steps[index]
             words = w_pool.tile(
                 [P, ROUND_GROUPS, F], U32, name="w_words", tag="w_words", align_bytes=64
             )
-            count = LOAD_GROUPS[which]
+            count = 1 if index >= len(steps) - 5 else 2 if index >= len(steps) - 7 else ROUND_GROUPS
             for i in range(0, ROUND_GROUPS, count):
                 first = rnd * ROUND_GROUPS + i
                 nc.sync.dma_start(
@@ -244,7 +248,6 @@ def tile_feedforward_pa_k_kernel(
             )
 
         def multiply(branch, rnd):
-            column = plane_column[(branch, rnd)]
             for pair in range(0, ROUND_GROUPS, 2):
                 for tt in range(TOKEN_TILES):
                     unit = TOKEN_TILES * rnd + tt
@@ -255,7 +258,7 @@ def tile_feedforward_pa_k_kernel(
                             lhsT=x_codes[unit][:, local, :].bitcast(FP8X4),
                             lhsT_scale=x_scales[unit][:, local, :],
                             rhs=w_words[(branch, rnd)][:, local, :].bitcast(FP8X4),
-                            rhs_scale=planes[QUADRANT_ROWS * local : P, column, :],
+                            rhs_scale=planes[branch][QUADRANT_ROWS * local : P, rnd, :],
                             start=(group == 0),
                             stop=(group == GROUPS - 1),
                         )
@@ -311,20 +314,19 @@ def tile_feedforward_pa_k_kernel(
                 )
 
         on_scalar, on_vector = nc.scalar.copy, nc.vector.tensor_copy
-        for which in range(SETS):
-            if which == SETS - 1:
-                load_x(0)
-            for branch in branches:
-                stage_scales(which, branch)
+        load_x(0)
+        for branch, half in sets:
+            stage_scales(branch, half)
         load_x(1)
         load_lora()
         load_x(2)
         load_x(3)
         load_step(0)
         regroup_scales()
-        for which in range(SETS):
-            spread_scales(which, upper_quadrants)
-        spread_scales(0, lower_quadrants)
+        for half in range(2):
+            for branch in branches:
+                spread_scales(branch, half, upper_quadrants)
+        spread_scales("w1", 0, lower_quadrants)
         load_step(1)
 
         sort_x(0, on_scalar)

@@ -101,7 +101,7 @@ def tile_feedforward_pa_k_kernel(
         regrouped = keep.tile([P, QUADRANT_ROWS, SET_ROUNDS, F // 4], I32, name="regrouped")
         planes = {}
         for branch in branches:
-            planes[branch] = keep.tile([P, ROUNDS, F], U8, name="planes_" + branch, align_bytes=64)
+            planes[branch] = keep.tile([P, ROUNDS, F], U8, name="planes_" + branch, align_bytes=256)
             nc.vector.memset(planes[branch][:].bitcast(I32), 0)
         a2_words = keep.tile([P, R], U32, name="a2_words", align_bytes=64)
         a2_plane = keep.tile([P, R], U8, name="a2_plane", align_bytes=64)
@@ -184,7 +184,7 @@ def tile_feedforward_pa_k_kernel(
                 spread_scales(branch, half, lower_quadrants)
             branch, rnd = steps[index]
             words = w_pool.tile(
-                [P, ROUND_GROUPS, F], U32, name="w_words", tag="w_words", align_bytes=64
+                [P, ROUND_GROUPS, F], U32, name="w_words", tag="w_words", align_bytes=256
             )
             count = 1 if index >= len(steps) - 5 else 2 if index >= len(steps) - 7 else ROUND_GROUPS
             for i in range(0, ROUND_GROUPS, count):
@@ -236,10 +236,10 @@ def tile_feedforward_pa_k_kernel(
 
         def quantise_x(unit):
             x_codes[unit] = codes_pool.tile(
-                [P, ROUND_GROUPS, P], U32, name="x_codes", tag="x_codes", align_bytes=64
+                [P, ROUND_GROUPS, P], U32, name="x_codes", tag="x_codes", align_bytes=256
             )
             x_scales[unit] = codes_pool.tile(
-                [P, ROUND_GROUPS, P], U8, name="x_scales", tag="x_scales", align_bytes=64
+                [P, ROUND_GROUPS, P], U8, name="x_scales", tag="x_scales", align_bytes=256
             )
             nc.vector.quantize_mx(
                 out=x_codes[unit][:].rearrange("p g s -> p (g s)").bitcast(FP8X4),

@@ -97,13 +97,13 @@ def tile_feedforward_pa_k_kernel(
         table_out = keep.tile([P, 1], F32, name="table_out")
         nc.vector.memset(table_in[:], 0.0)
         nc.scalar.activation(out=table_out[:], in_=table_in[:], func=SILU)
-        staged = keep.tile([P, SET_ROUNDS, QUADRANT_ROWS, F // 4], I32, name="staged")
-        regrouped = keep.tile([P, QUADRANT_ROWS, SET_ROUNDS, F // 4], I32, name="regrouped")
+        staged = keep.tile([P, SET_ROUNDS, QUADRANT_ROWS, F // 4], I32, name="staged", align_bytes=256)
+        regrouped = keep.tile([P, QUADRANT_ROWS, SET_ROUNDS, F // 4], I32, name="regrouped", align_bytes=256)
         planes = {}
         for branch in branches:
             planes[branch] = keep.tile([P, ROUNDS, F], U8, name="planes_" + branch, align_bytes=256)
             nc.vector.memset(planes[branch][:].bitcast(I32), 0)
-        a2_words = keep.tile([P, R], U32, name="a2_words", align_bytes=64)
+        a2_words = keep.tile([P, R], U32, name="a2_words", align_bytes=256)
         a2_plane = keep.tile([P, R], U8, name="a2_plane", align_bytes=64)
         nc.vector.memset(a2_plane[:].bitcast(I32), 0)
         identity_f32 = keep.tile([P, P], F32, name="identity_f32")
@@ -154,7 +154,7 @@ def tile_feedforward_pa_k_kernel(
 
         def load_x(unit):
             rnd, tt = divmod(unit, TOKEN_TILES)
-            x_raw[unit] = x_pool.tile([P, ROUND_GROUPS, K_PASS], BF16, name="x_raw", tag="x_raw")
+            x_raw[unit] = x_pool.tile([P, ROUND_GROUPS, K_PASS], BF16, name="x_raw", tag="x_raw", align_bytes=256)
             source = x[tt].rearrange("s (g k) -> s g k", k=K_PASS)[
                 :, rnd * ROUND_GROUPS : (rnd + 1) * ROUND_GROUPS, :
             ]
@@ -167,7 +167,7 @@ def tile_feedforward_pa_k_kernel(
         def load_lora():
             for branch in branches:
                 xa, lora_b = lora_inputs[branch]
-                lora_in[branch] = keep.tile([P, LORA_BLOCKS, R], BF16, name="lora_in_" + branch)
+                lora_in[branch] = keep.tile([P, LORA_BLOCKS, R], BF16, name="lora_in_" + branch, align_bytes=256)
                 nc.sync.dma_start(
                     out=lora_in[branch][:, 0:TOKEN_TILES, :],
                     in_=xa.rearrange("b (q i) r -> (b q) i r", i=TOKEN_TILES),
@@ -381,7 +381,7 @@ def tile_feedforward_pa_k_kernel(
             g_grouped[tt] = keep.tile([P, P, PACK], BF16, name="g_grouped_%d" % tt, align_bytes=64)
             nc.scalar.copy(out=g_grouped[tt][:], in_=g_turned[tt][:].rearrange("p t s -> p s t"))
         for tt in range(TOKEN_TILES):
-            g = keep.tile([P, F], F32, name="g_%d" % tt)
+            g = keep.tile([P, F], F32, name="g_%d" % tt, align_bytes=256)
             nc.vector.tensor_add(
                 out=g[:].rearrange("s (p t) -> s p t", t=PACK),
                 in0=gated_sum[tt][:].rearrange("s t p -> s p t"),
@@ -406,6 +406,6 @@ def tile_feedforward_pa_k_kernel(
                 start=True,
                 stop=True,
             )
-            ga2 = keep.tile([P, R], F32, name="ga2_%d" % tt)
+            ga2 = keep.tile([P, R], F32, name="ga2_%d" % tt, align_bytes=256)
             nc.scalar.copy(out=ga2[:], in_=ga2_psum[:])
             nc.scalar.dma_start(out=out_1[tt], in_=ga2[:])

@@ -132,11 +132,11 @@ def tile_feedforward_pa_k_kernel(
                     in_=staged[rows, :, :, :].rearrange("p c r n -> p r c n"),
                 )
 
-        def spread_scales(branch, half, quadrants):
+        def spread_scales(branch, half, quadrants, queue):
             for quadrant in quadrants:
                 first = STAGE_FIRST + SETS * quadrant + sets.index((branch, half))
                 live = slice(QUADRANT * quadrant, QUADRANT * quadrant + ROUND_GROUPS * QUADRANT_ROWS)
-                nc.sync.dma_start(
+                queue.dma_start(
                     out=planes[branch][live, SET_ROUNDS * half : SET_ROUNDS * (half + 1), :]
                     .rearrange("p c n -> p (c n)")
                     .bitcast(I32),
@@ -180,8 +180,6 @@ def tile_feedforward_pa_k_kernel(
         def load_step(index):
             for unit in units_before(index):
                 load_x(unit)
-            for branch, half in sets_before(index):
-                spread_scales(branch, half, lower_quadrants)
             branch, rnd = steps[index]
             words = w_pool.tile(
                 [P, ROUND_GROUPS, F], U32, name="w_words", tag="w_words", align_bytes=256
@@ -323,10 +321,10 @@ def tile_feedforward_pa_k_kernel(
         load_x(3)
         load_step(0)
         regroup_scales()
-        for half in range(2):
-            for branch in branches:
-                spread_scales(branch, half, upper_quadrants)
-        spread_scales("w1", 0, lower_quadrants)
+        spread_scales("w1", 0, upper_quadrants, nc.sync)
+        spread_scales("w1", 0, lower_quadrants, nc.sync)
+        for branch, half in (("w3", 0), ("w1", 1), ("w3", 1)):
+            spread_scales(branch, half, range(QUADRANTS), nc.gpsimd)
         load_step(1)
 
         sort_x(0, on_scalar)

@@ -12,7 +12,7 @@ FP8X4 = mybir.dt.float8_e4m3fn_x4
 SILU = mybir.ActivationFunctionType.Silu
 
 P = 128
-TOKEN_TILES = 2
+TILES = 2
 D = 16384
 F = 512
 R = 128
@@ -22,87 +22,56 @@ K_PASS = P * PACK
 GROUPS = D // K_PASS
 QUADRANT = 32
 QUADRANTS = P // QUADRANT
-QUADRANT_ROWS = 4
-ROUND_GROUPS = 4
-ROUNDS = GROUPS // ROUND_GROUPS
-UNITS = TOKEN_TILES * ROUNDS
-BANK_GROUPS = 2
+ROWS = 4
+ROUND = 4
+ROUNDS = GROUPS // ROUND
+HALF = ROUNDS // 2
 LAG = 2
 HEAD_ROUNDS = 2
-SETS = 4
-SET_ROUNDS = ROUNDS // 2
 STAGE_FIRST = 32
 STAGE_END = 96
-LORA_BLOCKS = TOKEN_TILES + F // P
+STAGE_STEP = 4
+LORA_BLOCKS = TILES + F // P
 
-FLOPS = 2 * TOKEN_TILES * P * (2 * D * F + 2 * R * F + F * R)
+FLOPS = 2 * TILES * P * (2 * D * F + 2 * R * F + F * R)
 
 
 def tile_feedforward_pa_k_kernel(
-    tc,
-    x,
-    w1_words,
-    w1_scales,
-    w3_words,
-    w3_scales,
-    xa1,
-    xa3,
-    lora_B1,
-    lora_B3,
-    lora_A2_words,
-    lora_A2_scales,
-    out_0,
-    out_1,
+    tc, x, w1_words, w1_scales, w3_words, w3_scales, xa1, xa3, lora_B1, lora_B3, lora_A2_words, lora_A2_scales, out_0, out_1
 ):
     nc = tc.nc
-    branches = ("w1", "w3")
-    words_of = {"w1": w1_words, "w3": w3_words}
-    scales_of = {"w1": w1_scales, "w3": w3_scales}
-    lora_inputs = {"w1": (xa1, lora_B1), "w3": (xa3, lora_B3)}
+    words_in = (w1_words, w3_words)
+    scales_in = (w1_scales, w3_scales)
+    lora_inputs = ((xa1, lora_B1), (xa3, lora_B3))
+    steps = [(0, r) for r in range(LAG)]
+    for r in range(LAG, ROUNDS + LAG):
+        steps += [(0, r)] * (r < ROUNDS) + [(1, r - LAG)]
+    last = len(steps) - 1
 
-    steps = []
-    for rnd in range(ROUNDS + LAG):
-        if rnd < ROUNDS:
-            steps.append(("w1", rnd))
-        if rnd >= LAG:
-            steps.append(("w3", rnd - LAG))
-    sets = [(branch, half) for branch in branches for half in range(2)]
-
-    def units_before(index):
+    def round_before(index):
         following = steps[index + 1 : index + 2]
-        rounds = [rnd for branch, rnd in following if branch == "w1" and rnd >= HEAD_ROUNDS]
-        return [TOKEN_TILES * rnd + tt for rnd in rounds for tt in range(TOKEN_TILES)]
-
-    def sets_before(index):
-        ahead = steps[index : index + 2] if units_before(index) else []
-        return [(branch, rnd // SET_ROUNDS) for branch, rnd in ahead if rnd % SET_ROUNDS == 0]
+        return [r for w, r in following if w == 0 and r >= HEAD_ROUNDS]
 
     with ExitStack() as ctx:
         keep = ctx.enter_context(tc.tile_pool(name="keep", bufs=1))
-        x_pool = ctx.enter_context(tc.tile_pool(name="x_pool", bufs=6))
+        x_pool = ctx.enter_context(tc.tile_pool(name="x_pool", bufs=3))
         sorted_pool = ctx.enter_context(tc.tile_pool(name="sorted_pool", bufs=3))
         grouped_pool = ctx.enter_context(tc.tile_pool(name="grouped_pool", bufs=3))
-        codes_pool = ctx.enter_context(tc.tile_pool(name="codes_pool", bufs=UNITS))
+        codes_pool = ctx.enter_context(tc.tile_pool(name="codes_pool", bufs=TILES * ROUNDS))
         w_pool = ctx.enter_context(tc.tile_pool(name="w_pool", bufs=7))
         turn_psum = ctx.enter_context(tc.psum_pool(name="turn_psum", bufs=4))
         acc_psum = ctx.enter_context(tc.psum_pool(name="acc_psum", bufs=1))
         ctx.enter_context(tc.manual_schedule())
 
-        x_raw, x_sorted, x_grouped, x_codes, x_scales = {}, {}, {}, {}, {}
-        w_words = {}
-        lora_in, lora_turned, lora_term = {}, {}, {}
-        gate, gated_lora, gated_sum, g_turned, g_grouped = {}, {}, {}, {}, {}
-
         table_in = keep.tile([P, 1], F32, name="table_in")
         table_out = keep.tile([P, 1], F32, name="table_out")
         nc.vector.memset(table_in[:], 0.0)
         nc.scalar.activation(out=table_out[:], in_=table_in[:], func=SILU)
-        staged = keep.tile([P, SET_ROUNDS, QUADRANT_ROWS, F // 4], I32, name="staged", align_bytes=256)
-        regrouped = keep.tile([P, QUADRANT_ROWS, SET_ROUNDS, F // 4], I32, name="regrouped", align_bytes=256)
-        planes = {}
-        for branch in branches:
-            planes[branch] = keep.tile([P, ROUNDS, F], U8, name="planes_" + branch, align_bytes=256)
-            nc.vector.memset(planes[branch][:].bitcast(I32), 0)
+        staged = keep.tile([P, ROWS, ROUNDS, F // 4], I32, name="staged", align_bytes=2048)
+        planes = []
+        for w in range(2):
+            planes.append(keep.tile([P, ROUNDS, F], U8, name="planes_%d" % w, align_bytes=2048))
+            nc.vector.memset(planes[w][:].bitcast(I32), 0)
         a2_words = keep.tile([P, R], U32, name="a2_words", align_bytes=256)
         a2_plane = keep.tile([P, R], U8, name="a2_plane", align_bytes=64)
         nc.vector.memset(a2_plane[:].bitcast(I32), 0)
@@ -110,289 +79,244 @@ def tile_feedforward_pa_k_kernel(
         make_identity(nc, identity_f32[:])
         identity_bf16 = keep.tile([P, P], BF16, name="identity_bf16")
         make_identity(nc, identity_bf16[:])
-        acc = {}
-        for branch in branches:
-            for tt in range(TOKEN_TILES):
-                acc[(branch, tt)] = acc_psum.tile([P, F], F32, name="acc_%s_%d" % (branch, tt))
+        acc = [[acc_psum.tile([P, F], F32, name="acc_%d_%d" % (w, t)) for t in range(TILES)] for w in range(2)]
 
-        def stage_scales(branch, half):
-            first = STAGE_FIRST + sets.index((branch, half))
-            nc.sync.dma_start(
-                out=staged[first:STAGE_END:SETS, :, :, :].rearrange("i c r n -> i c (r n)"),
-                in_=scales_of[branch]
-                .bitcast(I32)[half * GROUPS // 2 : (half + 1) * GROUPS // 2]
-                .rearrange("(c j) (q r) n -> (j q) c (r n)", j=ROUND_GROUPS, r=QUADRANT_ROWS),
-            )
+        x_raw, x_sorted, x_grouped, x_codes, x_scales, words = {}, {}, {}, {}, {}, {}
+        lora_in, lora_turned, lora_term, gate, gated_lora = {}, {}, {}, {}, {}
 
-        def regroup_scales():
-            for first in range(STAGE_FIRST, STAGE_END, QUADRANT):
-                rows = slice(first, first + QUADRANT)
-                nc.vector.tensor_copy(
-                    out=regrouped[rows, :, :, :],
-                    in_=staged[rows, :, :, :].rearrange("p c r n -> p r c n"),
-                )
+        def stage(w):
+            rows = scales_in[w].bitcast(I32).rearrange("(c j) (q r) n -> r (j q) c n", j=ROUND, r=ROWS)
+            for r in range(ROWS):
+                nc.sync.dma_start(out=staged[STAGE_FIRST + w : STAGE_END : STAGE_STEP, r, :, :], in_=rows[r])
 
-        def spread_scales(branch, half, quadrants, queue):
-            for quadrant in quadrants:
-                first = STAGE_FIRST + SETS * quadrant + sets.index((branch, half))
-                live = slice(QUADRANT * quadrant, QUADRANT * quadrant + ROUND_GROUPS * QUADRANT_ROWS)
-                queue.dma_start(
-                    out=planes[branch][live, SET_ROUNDS * half : SET_ROUNDS * (half + 1), :]
+        def spread(w, quadrants, rounds):
+            for q in quadrants:
+                first = STAGE_FIRST + w + STAGE_STEP * q
+                nc.sync.dma_start(
+                    out=planes[w][QUADRANT * q : QUADRANT * q + ROUND * ROWS, rounds, :]
                     .rearrange("p c n -> p (c n)")
                     .bitcast(I32),
-                    in_=regrouped[first : STAGE_END : SETS * QUADRANTS, :, :, :].rearrange(
+                    in_=staged[first : STAGE_END : STAGE_STEP * QUADRANTS, :, rounds, :].rearrange(
                         "j r c n -> j r (c n)"
                     ),
                 )
 
-        lower_quadrants = range(QUADRANTS // 2)
-        upper_quadrants = range(QUADRANTS // 2, QUADRANTS)
+        def x_tile(r):
+            x_raw[r] = x_pool.tile([P, TILES, ROUND * K_PASS], BF16, name="x_raw", tag="x_raw", align_bytes=4096)
 
-        def pieces_of(unit):
-            count = BANK_GROUPS if unit == UNITS - 1 else ROUND_GROUPS
-            return [slice(i, i + count) for i in range(0, ROUND_GROUPS, count)]
+        def load_x(r, tiles, groups):
+            cols = slice(groups.start * K_PASS, groups.stop * K_PASS)
+            source = x.rearrange("b s (c k) -> s b c k", k=ROUND * K_PASS)[:, tiles, r, cols]
+            nc.sync.dma_start(out=x_raw[r][:, tiles, cols], in_=source)
 
-        def load_x(unit):
-            rnd, tt = divmod(unit, TOKEN_TILES)
-            x_raw[unit] = x_pool.tile([P, ROUND_GROUPS, K_PASS], BF16, name="x_raw", tag="x_raw", align_bytes=256)
-            source = x[tt].rearrange("s (g k) -> s g k", k=K_PASS)[
-                :, rnd * ROUND_GROUPS : (rnd + 1) * ROUND_GROUPS, :
-            ]
-            for piece in pieces_of(unit):
-                nc.sync.dma_start(
-                    out=x_raw[unit][:, piece, :].rearrange("s g k -> s (g k)"),
-                    in_=source[:, piece, :].rearrange("s g k -> s (g k)"),
-                )
+        def pieces(r, t):
+            count = 2 if (r, t) == (ROUNDS - 1, TILES - 1) else ROUND
+            return [slice(g, g + count) for g in range(0, ROUND, count)]
 
-        def load_lora():
-            for branch in branches:
-                xa, lora_b = lora_inputs[branch]
-                lora_in[branch] = keep.tile([P, LORA_BLOCKS, R], BF16, name="lora_in_" + branch, align_bytes=256)
-                nc.sync.dma_start(
-                    out=lora_in[branch][:, 0:TOKEN_TILES, :],
-                    in_=xa.rearrange("b (q i) r -> (b q) i r", i=TOKEN_TILES),
-                )
-                nc.sync.dma_start(
-                    out=lora_in[branch][:, TOKEN_TILES:, :],
-                    in_=lora_b.rearrange("(p t) r -> p t r", t=PACK),
-                )
+        def load_x_round(r):
+            x_tile(r)
+            if r < ROUNDS - 2:
+                load_x(r, slice(0, TILES), slice(0, ROUND))
+            else:
+                for t in range(TILES):
+                    for piece in pieces(r, t):
+                        load_x(r, slice(t, t + 1), piece)
+
+        def load_lora(w):
+            xa, lora_b = lora_inputs[w]
+            lora_in[w] = keep.tile([P, LORA_BLOCKS, R], BF16, name="lora_in_%d" % w, align_bytes=256)
+            nc.sync.dma_start(out=lora_in[w][:, 0:TILES, :], in_=xa.rearrange("b (q i) r -> (b q) i r", i=TILES))
+            nc.sync.dma_start(out=lora_in[w][:, TILES:, :], in_=lora_b.rearrange("(p t) r -> p t r", t=PACK))
 
         def load_step(index):
-            for unit in units_before(index):
-                load_x(unit)
-            branch, rnd = steps[index]
-            words = w_pool.tile(
-                [P, ROUND_GROUPS, F], U32, name="w_words", tag="w_words", align_bytes=256
-            )
-            count = 1 if index >= len(steps) - 5 else 2 if index >= len(steps) - 7 else ROUND_GROUPS
-            for i in range(0, ROUND_GROUPS, count):
-                first = rnd * ROUND_GROUPS + i
+            for r in round_before(index):
+                load_x_round(r)
+                for w, r2 in steps[index : index + 2]:
+                    if r2 == HALF:
+                        spread(w, range(QUADRANTS // 2), slice(HALF, ROUNDS))
+            w, r = steps[index]
+            words[index] = w_pool.tile([P, ROUND, F], U32, name="words", tag="words", align_bytes=4096)
+            left = len(steps) - index
+            count = 1 if left in (5, 4) else 2 if left <= 7 else ROUND
+            for g in range(0, ROUND, count):
                 nc.sync.dma_start(
-                    out=words[:, i : i + count, :].bitcast(I32),
-                    in_=words_of[branch][first : first + count]
+                    out=words[index][:, g : g + count, :].bitcast(I32),
+                    in_=words_in[w][r * ROUND + g : r * ROUND + g + count]
                     .rearrange("g p n t -> p g (n t)")
                     .bitcast(I32),
                 )
-            w_words[steps[index]] = words
 
         def load_a2():
             nc.sync.dma_start(
-                out=a2_words[:].bitcast(I32),
-                in_=lora_A2_words[0].rearrange("p n t -> p (n t)").bitcast(I32),
+                out=a2_words[:].bitcast(I32), in_=lora_A2_words[0].rearrange("p n t -> p (n t)").bitcast(I32)
             )
-            for r in range(QUADRANT_ROWS):
+            for r in range(ROWS):
                 nc.sync.dma_start(
-                    out=a2_plane[r:P:QUADRANT, :].bitcast(I32),
-                    in_=lora_A2_scales[0].bitcast(I32)[r :: QUADRANT_ROWS, :],
+                    out=a2_plane[r:P:QUADRANT, :].bitcast(I32), in_=lora_A2_scales[0].bitcast(I32)[r::ROWS, :]
                 )
 
-        def sort_x(unit, copy):
-            x_sorted[unit] = sorted_pool.tile(
-                [P, ROUND_GROUPS, 2, P], F32, name="x_sorted", tag="x_sorted"
-            )
-            pairs = x_raw[unit][:].bitcast(F32).rearrange("s g (p u) -> s g u p", u=2)
-            for piece in pieces_of(unit):
-                copy(out=x_sorted[unit][:, piece, :, :], in_=pairs[:, piece, :, :])
+        def sort_x(r, t, copy):
+            x_sorted[(r, t)] = sorted_pool.tile([P, ROUND, 2, P], F32, name="x_sorted", tag="x_sorted")
+            pairs = x_raw[r][:, t, :].bitcast(F32).rearrange("s (g p u) -> s g u p", p=P, u=2)
+            for piece in pieces(r, t):
+                copy(out=x_sorted[(r, t)][:, piece, :, :], in_=pairs[:, piece, :, :])
 
-        def turn_x(unit, copies):
-            grouped = grouped_pool.tile(
-                [P, ROUND_GROUPS, P, PACK], BF16, name="x_grouped", tag="x_grouped", align_bytes=64
-            )
+        def turn_x(r, t, copies):
+            grouped = grouped_pool.tile([P, ROUND, P, PACK], BF16, name="x_grouped", tag="x_grouped", align_bytes=64)
             for bank, copy in enumerate(copies):
-                first = bank * BANK_GROUPS
-                turned = turn_psum.tile([P, BANK_GROUPS, 2, P], F32, name="x_turned", tag="turn")
-                for i in range(BANK_GROUPS):
+                turned = turn_psum.tile([P, 2, 2, P], F32, name="x_turned", tag="turn")
+                for i in range(2):
                     for u in range(2):
                         nc.tensor.transpose(
-                            turned[:, i, u, :], x_sorted[unit][:, first + i, u, :], identity_f32[:]
+                            turned[:, i, u, :], x_sorted[(r, t)][:, 2 * bank + i, u, :], identity_f32[:]
                         )
                 copy(
-                    out=grouped[:].bitcast(F32)[:, first : first + BANK_GROUPS, :, :],
+                    out=grouped[:].bitcast(F32)[:, 2 * bank : 2 * bank + 2, :, :],
                     in_=turned[:].rearrange("p g u s -> p g s u"),
                 )
-            x_grouped[unit] = grouped
+            x_grouped[(r, t)] = grouped
 
-        def quantise_x(unit):
-            x_codes[unit] = codes_pool.tile(
-                [P, ROUND_GROUPS, P], U32, name="x_codes", tag="x_codes", align_bytes=256
-            )
-            x_scales[unit] = codes_pool.tile(
-                [P, ROUND_GROUPS, P], U8, name="x_scales", tag="x_scales", align_bytes=256
-            )
+        def quantise_x(r, t):
+            x_codes[(r, t)] = codes_pool.tile([P, ROUND, P], U32, name="x_codes", tag="x_codes", align_bytes=256)
+            x_scales[(r, t)] = codes_pool.tile([P, ROUND, P], U8, name="x_scales", tag="x_scales", align_bytes=256)
             nc.vector.quantize_mx(
-                out=x_codes[unit][:].rearrange("p g s -> p (g s)").bitcast(FP8X4),
-                scales=x_scales[unit][:].rearrange("p g s -> p (g s)"),
-                in_=x_grouped[unit][:].rearrange("p g s t -> p (g s t)"),
+                out=x_codes[(r, t)][:].rearrange("p g s -> p (g s)").bitcast(FP8X4),
+                scales=x_scales[(r, t)][:].rearrange("p g s -> p (g s)"),
+                in_=x_grouped[(r, t)][:].rearrange("p g s t -> p (g s t)"),
             )
 
-        def multiply(branch, rnd):
-            for pair in range(0, ROUND_GROUPS, 2):
-                for tt in range(TOKEN_TILES):
-                    unit = TOKEN_TILES * rnd + tt
-                    for local in range(pair, pair + 2):
-                        group = rnd * ROUND_GROUPS + local
+        def multiply(index):
+            w, r = steps[index]
+            for pair in range(0, ROUND, 2):
+                for t in range(TILES):
+                    for j in range(pair, pair + 2):
                         nc.tensor.matmul_mx(
-                            out=acc[(branch, tt)][:],
-                            lhsT=x_codes[unit][:, local, :].bitcast(FP8X4),
-                            lhsT_scale=x_scales[unit][:, local, :],
-                            rhs=w_words[(branch, rnd)][:, local, :].bitcast(FP8X4),
-                            rhs_scale=planes[branch][QUADRANT_ROWS * local : P, rnd, :],
-                            start=(group == 0),
-                            stop=(group == GROUPS - 1),
+                            out=acc[w][t][:],
+                            lhsT=x_codes[(r, t)][:, j, :].bitcast(FP8X4),
+                            lhsT_scale=x_scales[(r, t)][:, j, :],
+                            rhs=words[index][:, j, :].bitcast(FP8X4),
+                            rhs_scale=planes[w][ROWS * j : P, r, :],
+                            start=(r == 0 and j == 0),
+                            stop=(r == ROUNDS - 1 and j == ROUND - 1),
                         )
 
         def turn_lora():
-            for branch in branches:
+            for w in range(2):
                 turned = turn_psum.tile([P, LORA_BLOCKS, P], BF16, name="lora_psum", tag="turn")
                 for i in range(LORA_BLOCKS):
-                    nc.tensor.transpose(turned[:, i, :], lora_in[branch][:, i, :], identity_bf16[:])
-                lora_turned[branch] = keep.tile(
-                    [P, LORA_BLOCKS, P], BF16, name="lora_turned_" + branch
-                )
+                    nc.tensor.transpose(turned[:, i, :], lora_in[w][:, i, :], identity_bf16[:])
+                lora_turned[w] = keep.tile([P, LORA_BLOCKS, P], BF16, name="lora_turned_%d" % w)
                 nc.scalar.copy(
-                    out=lora_turned[branch][:, 0:TOKEN_TILES, :].rearrange(
-                        "r b (q i) -> r (b q) i", i=TOKEN_TILES
-                    ),
-                    in_=turned[:, 0:TOKEN_TILES, :].rearrange("r i p -> r p i"),
+                    out=lora_turned[w][:, 0:TILES, :].rearrange("r b (q i) -> r (b q) i", i=TILES),
+                    in_=turned[:, 0:TILES, :].rearrange("r i p -> r p i"),
                 )
-                nc.scalar.copy(
-                    out=lora_turned[branch][:, TOKEN_TILES:, :], in_=turned[:, TOKEN_TILES:, :]
-                )
+                nc.scalar.copy(out=lora_turned[w][:, TILES:, :], in_=turned[:, TILES:, :])
 
         def multiply_lora():
-            for branch in branches:
-                for tt in range(TOKEN_TILES):
+            for w in range(2):
+                for t in range(TILES):
                     product = turn_psum.tile([P, PACK, P], F32, name="lora_product", tag="turn")
                     nc.tensor.matmul(
                         out=product[:].rearrange("s t p -> s (t p)"),
-                        lhsT=lora_turned[branch][:, tt, :],
-                        rhs=lora_turned[branch][:, TOKEN_TILES:, :].rearrange("r t p -> r (t p)"),
+                        lhsT=lora_turned[w][:, t, :],
+                        rhs=lora_turned[w][:, TILES:, :].rearrange("r t p -> r (t p)"),
                         start=True,
                         stop=True,
                     )
-                    lora_term[(branch, tt)] = keep.tile(
-                        [P, PACK, P], F32, name="lora_term_%s_%d" % (branch, tt)
-                    )
-                    nc.scalar.mul(out=lora_term[(branch, tt)][:], in_=product[:], mul=LORA_SCALING)
+                    lora_term[(w, t)] = keep.tile([P, PACK, P], F32, name="lora_term_%d_%d" % (w, t))
+                    nc.scalar.mul(out=lora_term[(w, t)][:], in_=product[:], mul=LORA_SCALING)
 
         def make_gate():
-            for tt in range(TOKEN_TILES):
-                h1 = keep.tile([P, PACK, P], F32, name="h1_%d" % tt)
+            for t in range(TILES):
+                h1 = keep.tile([P, PACK, P], F32, name="h1_%d" % t)
                 nc.vector.tensor_add(
-                    out=h1[:],
-                    in0=acc[("w1", tt)][:].rearrange("s (p t) -> s t p", t=PACK),
-                    in1=lora_term[("w1", tt)][:],
+                    out=h1[:], in0=acc[0][t][:].rearrange("s (p t) -> s t p", t=PACK), in1=lora_term[(0, t)][:]
                 )
-                gate[tt] = keep.tile([P, PACK, P], F32, name="gate_%d" % tt)
-                nc.scalar.activation(out=gate[tt][:], in_=h1[:], func=SILU)
-            for tt in range(TOKEN_TILES):
-                gated_lora[tt] = keep.tile([P, PACK, P], F32, name="gated_lora_%d" % tt)
-                nc.vector.tensor_mul(
-                    out=gated_lora[tt][:], in0=gate[tt][:], in1=lora_term[("w3", tt)][:]
-                )
+                gate[t] = keep.tile([P, PACK, P], F32, name="gate_%d" % t)
+                nc.scalar.activation(out=gate[t][:], in_=h1[:], func=SILU)
+            for t in range(TILES):
+                gated_lora[t] = keep.tile([P, PACK, P], F32, name="gated_lora_%d" % t)
+                nc.vector.tensor_mul(out=gated_lora[t][:], in0=gate[t][:], in1=lora_term[(1, t)][:])
 
         on_scalar, on_vector = nc.scalar.copy, nc.vector.tensor_copy
-        load_x(0)
-        for branch, half in sets:
-            stage_scales(branch, half)
-        load_x(1)
-        load_lora()
-        load_x(2)
-        load_x(3)
+        x_tile(0)
+        load_x(0, slice(0, 1), slice(0, ROUND))
+        stage(0)
+        load_x(0, slice(1, 2), slice(0, ROUND))
+        stage(1)
+        load_lora(0)
+        load_lora(1)
+        load_x_round(1)
         load_step(0)
-        regroup_scales()
-        spread_scales("w1", 0, upper_quadrants, nc.sync)
-        spread_scales("w1", 0, lower_quadrants, nc.sync)
-        for branch, half in (("w3", 0), ("w1", 1), ("w3", 1)):
-            spread_scales(branch, half, range(QUADRANTS), nc.gpsimd)
+        for w in range(2):
+            spread(w, range(QUADRANTS // 2, QUADRANTS), slice(0, ROUNDS))
+        for w in range(2):
+            spread(w, range(QUADRANTS // 2), slice(0, HALF))
         load_step(1)
 
-        sort_x(0, on_scalar)
-        sort_x(1, on_scalar)
-        turn_x(0, (on_scalar, on_scalar))
-        sort_x(2, on_scalar)
-        turn_x(1, (on_scalar, on_scalar))
+        sort_x(0, 0, on_vector)
+        sort_x(0, 1, on_vector)
+        turn_x(0, 0, (on_scalar, on_vector))
+        turn_x(0, 1, (on_scalar, on_vector))
+        quantise_x(0, 0)
         turn_lora()
-        sort_x(3, on_vector)
-        quantise_x(0)
-        quantise_x(1)
-        turn_x(2, (on_scalar, on_vector))
-        turn_x(3, (on_scalar, on_vector))
+        quantise_x(0, 1)
         multiply_lora()
-        quantise_x(2)
-        quantise_x(3)
 
-        for index, (branch, rnd) in enumerate(steps):
-            if index + 2 < len(steps):
+        sort_x(1, 0, on_vector)
+        sort_x(1, 1, on_vector)
+        for t in range(TILES):
+            turn_x(1, t, (on_scalar, on_vector))
+            quantise_x(1, t)
+
+        for index in range(len(steps)):
+            if index + 2 <= last:
                 load_step(index + 2)
-            elif index + 2 == len(steps):
+            elif index + 2 == last + 1:
                 load_a2()
-            for unit in units_before(index):
-                sort_x(unit, on_vector)
-            for unit in units_before(index):
-                turn_x(unit, (on_scalar, on_vector))
-                quantise_x(unit)
-            multiply(branch, rnd)
-            if (branch, rnd) == ("w1", ROUNDS - 1):
+            for r in round_before(index):
+                for t in range(TILES):
+                    sort_x(r, t, on_vector)
+                for t in range(TILES):
+                    turn_x(r, t, (on_scalar, on_vector))
+                    quantise_x(r, t)
+            multiply(index)
+            if steps[index] == (0, ROUNDS - 1):
                 make_gate()
 
-        for tt in range(TOKEN_TILES):
-            gated_sum[tt] = keep.tile([P, PACK, P], F32, name="gated_sum_%d" % tt)
+        gated_sum, g_grouped = {}, {}
+        for t in range(TILES):
+            gated_sum[t] = keep.tile([P, PACK, P], F32, name="gated_sum_%d" % t)
             nc.vector.tensor_mul(
-                out=gated_sum[tt][:],
-                in0=acc[("w3", tt)][:].rearrange("s (p t) -> s t p", t=PACK),
-                in1=gate[tt][:],
+                out=gated_sum[t][:], in0=acc[1][t][:].rearrange("s (p t) -> s t p", t=PACK), in1=gate[t][:]
             )
-        for tt in range(TOKEN_TILES):
-            g_turned[tt] = turn_psum.tile([P, PACK, P], F32, name="g_turned", tag="turn")
-            terms = (gated_lora[tt], gated_sum[tt])
-            for i, term in enumerate(terms):
-                for t in range(PACK):
+        for t in range(TILES):
+            g_turned = turn_psum.tile([P, PACK, P], F32, name="g_turned", tag="turn")
+            for i, term in enumerate((gated_lora[t], gated_sum[t])):
+                for s in range(PACK):
                     nc.tensor.matmul(
-                        out=g_turned[tt][:, t, :],
-                        lhsT=term[:, t, :],
+                        out=g_turned[:, s, :],
+                        lhsT=term[:, s, :],
                         rhs=identity_f32[:],
-                        start=(i == 0 and t == 0),
-                        stop=(i == len(terms) - 1 and t == PACK - 1),
+                        start=(i == 0 and s == 0),
+                        stop=(i == 1 and s == PACK - 1),
                         is_transpose=True,
                     )
-            g_grouped[tt] = keep.tile([P, P, PACK], BF16, name="g_grouped_%d" % tt, align_bytes=64)
-            nc.scalar.copy(out=g_grouped[tt][:], in_=g_turned[tt][:].rearrange("p t s -> p s t"))
-        for tt in range(TOKEN_TILES):
-            g = keep.tile([P, F], F32, name="g_%d" % tt, align_bytes=256)
+            g_grouped[t] = keep.tile([P, P, PACK], BF16, name="g_grouped_%d" % t, align_bytes=64)
+            nc.scalar.copy(out=g_grouped[t][:], in_=g_turned[:].rearrange("p t s -> p s t"))
+        for t in range(TILES):
+            g = keep.tile([P, F], F32, name="g_%d" % t, align_bytes=256)
             nc.vector.tensor_add(
                 out=g[:].rearrange("s (p t) -> s p t", t=PACK),
-                in0=gated_sum[tt][:].rearrange("s t p -> s p t"),
-                in1=gated_lora[tt][:].rearrange("s t p -> s p t"),
+                in0=gated_sum[t][:].rearrange("s t p -> s p t"),
+                in1=gated_lora[t][:].rearrange("s t p -> s p t"),
             )
-            nc.sync.dma_start(out=out_0[tt], in_=g[:])
-        for tt in range(TOKEN_TILES):
-            g_codes = keep.tile([P, P], U32, name="g_codes_%d" % tt, align_bytes=64)
-            g_scales = keep.tile([P, P], U8, name="g_scales_%d" % tt, align_bytes=64)
+            nc.sync.dma_start(out=out_0[t], in_=g[:])
+        for t in range(TILES):
+            g_codes = keep.tile([P, P], U32, name="g_codes_%d" % t, align_bytes=64)
+            g_scales = keep.tile([P, P], U8, name="g_scales_%d" % t, align_bytes=64)
             nc.vector.quantize_mx(
-                out=g_codes[:].bitcast(FP8X4),
-                scales=g_scales[:],
-                in_=g_grouped[tt][:].rearrange("p s t -> p (s t)"),
+                out=g_codes[:].bitcast(FP8X4), scales=g_scales[:], in_=g_grouped[t][:].rearrange("p s t -> p (s t)")
             )
             ga2_psum = turn_psum.tile([P, R], F32, name="ga2_psum", tag="turn")
             nc.tensor.matmul_mx(
@@ -404,6 +328,6 @@ def tile_feedforward_pa_k_kernel(
                 start=True,
                 stop=True,
             )
-            ga2 = keep.tile([P, R], F32, name="ga2_%d" % tt, align_bytes=256)
+            ga2 = keep.tile([P, R], F32, name="ga2_%d" % t, align_bytes=256)
             nc.scalar.copy(out=ga2[:], in_=ga2_psum[:])
-            nc.scalar.dma_start(out=out_1[tt], in_=ga2[:])
+            nc.scalar.dma_start(out=out_1[t], in_=ga2[:])

@@ -243,10 +243,10 @@ def tile_feedforward_pa_k_kernel(
         load_x(0, slice(0, 1), slice(0, ROUND))
         stage(0)
         load_x(0, slice(1, 2), slice(0, ROUND))
-        stage(1)
         load_lora(0)
-        load_lora(1)
         load_x_round(1)
+        stage(1)
+        load_lora(1)
         load_step(0)
         for w in range(2):
             spread(w, range(QUADRANTS // 2, QUADRANTS), slice(0, ROUNDS))

@@ -284,7 +284,7 @@ def tile_feedforward_pa_k_kernel(
             if steps[index] == (0, ROUNDS - 1):
                 make_gate()
 
-        gated_sum, g_grouped = {}, {}
+        gated_sum, g_grouped, products = {}, {}, {}
         for t in range(TILES):
             gated_sum[t] = keep.tile([P, PACK, P], F32, name="gated_sum_%d" % t)
             nc.vector.tensor_mul(
@@ -311,7 +311,7 @@ def tile_feedforward_pa_k_kernel(
                 in0=gated_sum[t][:].rearrange("s t p -> s p t"),
                 in1=gated_lora[t][:].rearrange("s t p -> s p t"),
             )
-            nc.sync.dma_start(out=out_0[t], in_=g[:])
+            nc.scalar.dma_start(out=out_0[t], in_=g[:])
         for t in range(TILES):
             g_codes = keep.tile([P, P], U32, name="g_codes_%d" % t, align_bytes=64)
             g_scales = keep.tile([P, P], U8, name="g_scales_%d" % t, align_bytes=64)
@@ -328,6 +328,8 @@ def tile_feedforward_pa_k_kernel(
                 start=True,
                 stop=True,
             )
+            products[t] = ga2_psum
+        for t in range(TILES):
             ga2 = keep.tile([P, R], F32, name="ga2_%d" % t, align_bytes=256)
-            nc.scalar.copy(out=ga2[:], in_=ga2_psum[:])
-            nc.scalar.dma_start(out=out_1[t], in_=ga2[:])
+            nc.vector.tensor_copy(out=ga2[:], in_=products[t][:])
+            nc.sync.dma_start(out=out_1[t], in_=ga2[:])

@@ -133,11 +133,13 @@ def tile_feedforward_pa_k_kernel(
                 load_x_round(r)
                 for w, r2 in steps[index : index + 2]:
                     if r2 == HALF:
-                        spread(w, range(QUADRANTS // 2), slice(HALF, ROUNDS))
+                        spread(w, range(QUADRANTS // 2), slice(HALF, ROUNDS - 2 * w))
             w, r = steps[index]
+            if (w, r) == (1, ROUNDS - 2):
+                spread(w, range(QUADRANTS // 2), slice(r, ROUNDS))
             words[index] = w_pool.tile([P, ROUND, F], U32, name="words", tag="words", align_bytes=4096)
             left = len(steps) - index
-            count = 1 if left in (5, 4) else 2 if left <= 7 else ROUND
+            count = 1 if left <= 5 else 2 if left <= 7 else ROUND
             for g in range(0, ROUND, count):
                 nc.sync.dma_start(
                     out=words[index][:, g : g + count, :].bitcast(I32),

@@ -53,12 +53,13 @@ def tile_feedforward_pa_k_kernel(
         return [r for w, r in following if w == 0 and r >= HEAD_ROUNDS]
 
     with ExitStack() as ctx:
+        w_low = ctx.enter_context(tc.tile_pool(name="w_low", bufs=4))
+        sorted_pool = ctx.enter_context(tc.tile_pool(name="sorted_pool", bufs=3))
+        codes_pool = ctx.enter_context(tc.tile_pool(name="codes_pool", bufs=12))
+        grouped_pool = ctx.enter_context(tc.tile_pool(name="grouped_pool", bufs=3))
         keep = ctx.enter_context(tc.tile_pool(name="keep", bufs=1))
         x_pool = ctx.enter_context(tc.tile_pool(name="x_pool", bufs=3))
-        sorted_pool = ctx.enter_context(tc.tile_pool(name="sorted_pool", bufs=3))
-        grouped_pool = ctx.enter_context(tc.tile_pool(name="grouped_pool", bufs=3))
-        codes_pool = ctx.enter_context(tc.tile_pool(name="codes_pool", bufs=TILES * ROUNDS))
-        w_pool = ctx.enter_context(tc.tile_pool(name="w_pool", bufs=7))
+        w_high = ctx.enter_context(tc.tile_pool(name="w_high", bufs=4))
         turn_psum = ctx.enter_context(tc.psum_pool(name="turn_psum", bufs=4))
         acc_psum = ctx.enter_context(tc.psum_pool(name="acc_psum", bufs=1))
         ctx.enter_context(tc.manual_schedule())
@@ -137,12 +138,15 @@ def tile_feedforward_pa_k_kernel(
             w, r = steps[index]
             if (w, r) == (1, ROUNDS - 2):
                 spread(w, range(QUADRANTS // 2), slice(r, ROUNDS))
-            words[index] = w_pool.tile([P, ROUND, F], U32, name="words", tag="words", align_bytes=4096)
             left = len(steps) - index
             count = 1 if left <= 5 else 2 if left <= 7 else ROUND
+            pools = (w_low, w_high) if count < ROUND else ((w_low, w_high)[index % 2],)
+            tiles = [pool.tile([P, ROUND, F], U32, name="words", tag="words", align_bytes=4096) for pool in pools]
             for g in range(0, ROUND, count):
+                for j in range(g, g + count):
+                    words[(index, j)] = tiles[g // count % len(tiles)]
                 nc.sync.dma_start(
-                    out=words[index][:, g : g + count, :].bitcast(I32),
+                    out=words[(index, g)][:, g : g + count, :].bitcast(I32),
                     in_=words_in[w][r * ROUND + g : r * ROUND + g + count]
                     .rearrange("g p n t -> p g (n t)")
                     .bitcast(I32),
@@ -196,7 +200,7 @@ def tile_feedforward_pa_k_kernel(
                             out=acc[w][t][:],
                             lhsT=x_codes[(r, t)][:, j, :].bitcast(FP8X4),
                             lhsT_scale=x_scales[(r, t)][:, j, :],
-                            rhs=words[index][:, j, :].bitcast(FP8X4),
+                            rhs=words[(index, j)][:, j, :].bitcast(FP8X4),
                             rhs_scale=planes[w][ROWS * j : P, r, :],
                             start=(r == 0 and j == 0),
                             stop=(r == ROUNDS - 1 and j == ROUND - 1),

@@ -194,7 +194,7 @@ def tile_feedforward_pa_k_kernel(
         def multiply(index):
             w, r = steps[index]
             for pair in range(0, ROUND, 2):
-                for t in range(TILES):
+                for t in ((0, 1), (1, 0))[(pair // 2 + w) % 2]:
                     for j in range(pair, pair + 2):
                         nc.tensor.matmul_mx(
                             out=acc[w][t][:],

@@ -26,8 +26,11 @@ ROWS = 4
 ROUND = 4
 ROUNDS = GROUPS // ROUND
 HALF = ROUNDS // 2
-LAG = 2
-HEAD_ROUNDS = 2
+LONG_ROUNDS = 6
+HEAD_SHEETS = 2
+SINGLE_STEPS = 5
+FINE_STEPS = 7
+LATE_ROUNDS = 2
 STAGE_FIRST = 32
 STAGE_END = 96
 STAGE_STEP = 4
@@ -43,23 +46,28 @@ def tile_feedforward_pa_k_kernel(
     words_in = (w1_words, w3_words)
     scales_in = (w1_scales, w3_scales)
     lora_inputs = ((xa1, lora_B1), (xa3, lora_B3))
-    steps = [(0, r) for r in range(LAG)]
-    for r in range(LAG, ROUNDS + LAG):
-        steps += [(0, r)] * (r < ROUNDS) + [(1, r - LAG)]
+
+    sheets = [[(r, t), (r + 1, t)] for r in range(0, LONG_ROUNDS, 2) for t in range(TILES)]
+    sheets += [[(r, t) for t in range(TILES)] for r in range(LONG_ROUNDS, ROUNDS)]
+    sheet_before = {2 * (s - HEAD_SHEETS) + 1: s for s in range(HEAD_SHEETS, len(sheets))}
+    steps = []
+    ready = sheets[0] + sheets[1]
+    taken = [0, 0]
+    for index in range(2 * ROUNDS):
+        if index - 1 in sheet_before:
+            ready = ready + sheets[sheet_before[index - 1]]
+        w = 0 if all((taken[0], t) in ready for t in range(TILES)) else 1
+        steps.append((w, taken[w]))
+        taken[w] += 1
     last = len(steps) - 1
 
-    def round_before(index):
-        following = steps[index + 1 : index + 2]
-        return [r for w, r in following if w == 0 and r >= HEAD_ROUNDS]
-
     with ExitStack() as ctx:
-        w_low = ctx.enter_context(tc.tile_pool(name="w_low", bufs=4))
+        words_pool = ctx.enter_context(tc.tile_pool(name="words_pool", bufs=8))
         sorted_pool = ctx.enter_context(tc.tile_pool(name="sorted_pool", bufs=3))
         codes_pool = ctx.enter_context(tc.tile_pool(name="codes_pool", bufs=12))
         grouped_pool = ctx.enter_context(tc.tile_pool(name="grouped_pool", bufs=3))
         keep = ctx.enter_context(tc.tile_pool(name="keep", bufs=1))
         x_pool = ctx.enter_context(tc.tile_pool(name="x_pool", bufs=3))
-        w_high = ctx.enter_context(tc.tile_pool(name="w_high", bufs=4))
         turn_psum = ctx.enter_context(tc.psum_pool(name="turn_psum", bufs=4))
         acc_psum = ctx.enter_context(tc.psum_pool(name="acc_psum", bufs=1))
         ctx.enter_context(tc.manual_schedule())
@@ -102,26 +110,28 @@ def tile_feedforward_pa_k_kernel(
                     ),
                 )
 
-        def x_tile(r):
-            x_raw[r] = x_pool.tile([P, TILES, ROUND * K_PASS], BF16, name="x_raw", tag="x_raw", align_bytes=4096)
-
-        def load_x(r, tiles, groups):
-            cols = slice(groups.start * K_PASS, groups.stop * K_PASS)
-            source = x.rearrange("b s (c k) -> s b c k", k=ROUND * K_PASS)[:, tiles, r, cols]
-            nc.sync.dma_start(out=x_raw[r][:, tiles, cols], in_=source)
-
         def pieces(r, t):
             count = 2 if (r, t) == (ROUNDS - 1, TILES - 1) else ROUND
             return [slice(g, g + count) for g in range(0, ROUND, count)]
 
-        def load_x_round(r):
-            x_tile(r)
-            if r < ROUNDS - 2:
-                load_x(r, slice(0, TILES), slice(0, ROUND))
+        def load_sheet(s):
+            sheet = x_pool.tile([P, 2, ROUND * K_PASS], BF16, name="x_sheet", tag="x_sheet", align_bytes=4096)
+            for i, unit in enumerate(sheets[s]):
+                x_raw[unit] = sheet[:, i, :]
+            (r, t), (r2, t2) = sheets[s]
+            if t == t2:
+                nc.sync.dma_start(
+                    out=sheet[:].rearrange("s i k -> s (i k)"),
+                    in_=x[t, :, r * ROUND * K_PASS : (r2 + 1) * ROUND * K_PASS],
+                )
             else:
                 for t in range(TILES):
                     for piece in pieces(r, t):
-                        load_x(r, slice(t, t + 1), piece)
+                        first = r * ROUND * K_PASS
+                        nc.sync.dma_start(
+                            out=sheet[:, t, piece.start * K_PASS : piece.stop * K_PASS],
+                            in_=x[t, :, first + piece.start * K_PASS : first + piece.stop * K_PASS],
+                        )
 
         def load_lora(w):
             xa, lora_b = lora_inputs[w]
@@ -129,22 +139,26 @@ def tile_feedforward_pa_k_kernel(
             nc.sync.dma_start(out=lora_in[w][:, 0:TILES, :], in_=xa.rearrange("b (q i) r -> (b q) i r", i=TILES))
             nc.sync.dma_start(out=lora_in[w][:, TILES:, :], in_=lora_b.rearrange("(p t) r -> p t r", t=PACK))
 
+        lower, upper = range(QUADRANTS // 2), range(QUADRANTS // 2, QUADRANTS)
+
         def load_step(index):
-            for r in round_before(index):
-                load_x_round(r)
-                for w, r2 in steps[index : index + 2]:
-                    if r2 == HALF:
-                        spread(w, range(QUADRANTS // 2), slice(HALF, ROUNDS - 2 * w))
+            if index in sheet_before:
+                load_sheet(sheet_before[index])
+                for w, r in steps[index : index + 2]:
+                    if r == HALF:
+                        spread(w, lower, slice(HALF, ROUNDS - LATE_ROUNDS * w))
             w, r = steps[index]
-            if (w, r) == (1, ROUNDS - 2):
-                spread(w, range(QUADRANTS // 2), slice(r, ROUNDS))
+            if (w, r) == (1, ROUNDS - LATE_ROUNDS):
+                spread(w, lower, slice(r, ROUNDS))
             left = len(steps) - index
-            count = 1 if left <= 5 else 2 if left <= 7 else ROUND
-            pools = (w_low, w_high) if count < ROUND else ((w_low, w_high)[index % 2],)
-            tiles = [pool.tile([P, ROUND, F], U32, name="words", tag="words", align_bytes=4096) for pool in pools]
+            count = 1 if left <= SINGLE_STEPS else 2 if left <= FINE_STEPS else ROUND
+            halves = 1 if count == ROUND else 2
+            tiles = [
+                words_pool.tile([P, ROUND, F], U32, name="words", tag="words", align_bytes=4096) for h in range(halves)
+            ]
             for g in range(0, ROUND, count):
                 for j in range(g, g + count):
-                    words[(index, j)] = tiles[g // count % len(tiles)]
+                    words[(index, j)] = tiles[g // count % halves]
                 nc.sync.dma_start(
                     out=words[(index, g)][:, g : g + count, :].bitcast(I32),
                     in_=words_in[w][r * ROUND + g : r * ROUND + g + count]
@@ -161,15 +175,15 @@ def tile_feedforward_pa_k_kernel(
                     out=a2_plane[r:P:QUADRANT, :].bitcast(I32), in_=lora_A2_scales[0].bitcast(I32)[r::ROWS, :]
                 )
 
-        def sort_x(r, t, copy):
+        def sort_x(r, t):
             x_sorted[(r, t)] = sorted_pool.tile([P, ROUND, 2, P], F32, name="x_sorted", tag="x_sorted")
-            pairs = x_raw[r][:, t, :].bitcast(F32).rearrange("s (g p u) -> s g u p", p=P, u=2)
+            pairs = x_raw[(r, t)].bitcast(F32).rearrange("s (g p u) -> s g u p", p=P, u=2)
             for piece in pieces(r, t):
-                copy(out=x_sorted[(r, t)][:, piece, :, :], in_=pairs[:, piece, :, :])
+                nc.vector.tensor_copy(out=x_sorted[(r, t)][:, piece, :, :], in_=pairs[:, piece, :, :])
 
-        def turn_x(r, t, copies):
+        def turn_x(r, t):
             grouped = grouped_pool.tile([P, ROUND, P, PACK], BF16, name="x_grouped", tag="x_grouped", align_bytes=64)
-            for bank, copy in enumerate(copies):
+            for bank, copy in enumerate((nc.scalar.copy, nc.vector.tensor_copy)):
                 turned = turn_psum.tile([P, 2, 2, P], F32, name="x_turned", tag="turn")
                 for i in range(2):
                     for u in range(2):
@@ -191,10 +205,17 @@ def tile_feedforward_pa_k_kernel(
                 in_=x_grouped[(r, t)][:].rearrange("p g s t -> p (g s t)"),
             )
 
+        def prepare_sheet(s):
+            for unit in sheets[s]:
+                sort_x(*unit)
+            for unit in sheets[s]:
+                turn_x(*unit)
+                quantise_x(*unit)
+
         def multiply(index):
             w, r = steps[index]
             for pair in range(0, ROUND, 2):
-                for t in ((0, 1), (1, 0))[(pair // 2 + w) % 2]:
+                for t in range(TILES):
                     for j in range(pair, pair + 2):
                         nc.tensor.matmul_mx(
                             out=acc[w][t][:],
@@ -244,48 +265,31 @@ def tile_feedforward_pa_k_kernel(
                 gated_lora[t] = keep.tile([P, PACK, P], F32, name="gated_lora_%d" % t)
                 nc.vector.tensor_mul(out=gated_lora[t][:], in0=gate[t][:], in1=lora_term[(1, t)][:])
 
-        on_scalar, on_vector = nc.scalar.copy, nc.vector.tensor_copy
-        x_tile(0)
-        load_x(0, slice(0, 1), slice(0, ROUND))
+        load_sheet(0)
         stage(0)
-        load_x(0, slice(1, 2), slice(0, ROUND))
         load_lora(0)
-        load_x_round(1)
+        load_sheet(1)
         stage(1)
         load_lora(1)
         load_step(0)
         for w in range(2):
-            spread(w, range(QUADRANTS // 2, QUADRANTS), slice(0, ROUNDS))
+            spread(w, upper, slice(0, ROUNDS))
         for w in range(2):
-            spread(w, range(QUADRANTS // 2), slice(0, HALF))
+            spread(w, lower, slice(0, HALF))
         load_step(1)
 
-        sort_x(0, 0, on_vector)
-        sort_x(0, 1, on_vector)
-        turn_x(0, 0, (on_scalar, on_vector))
-        turn_x(0, 1, (on_scalar, on_vector))
-        quantise_x(0, 0)
+        prepare_sheet(0)
+        prepare_sheet(1)
         turn_lora()
-        quantise_x(0, 1)
         multiply_lora()
-
-        sort_x(1, 0, on_vector)
-        sort_x(1, 1, on_vector)
-        for t in range(TILES):
-            turn_x(1, t, (on_scalar, on_vector))
-            quantise_x(1, t)
 
         for index in range(len(steps)):
             if index + 2 <= last:
                 load_step(index + 2)
             elif index + 2 == last + 1:
                 load_a2()
-            for r in round_before(index):
-                for t in range(TILES):
-                    sort_x(r, t, on_vector)
-                for t in range(TILES):
-                    turn_x(r, t, (on_scalar, on_vector))
-                    quantise_x(r, t)
+            if index in sheet_before:
+                prepare_sheet(sheet_before[index])
             multiply(index)
             if steps[index] == (0, ROUNDS - 1):
                 make_gate()

@@ -28,8 +28,8 @@ ROUNDS = GROUPS // ROUND
 HALF = ROUNDS // 2
 LONG_ROUNDS = 6
 HEAD_SHEETS = 2
-SINGLE_STEPS = 5
-FINE_STEPS = 7
+SINGLE_GROUPS = 8
+FINE_GROUPS = 28
 LATE_ROUNDS = 2
 STAGE_FIRST = 32
 STAGE_END = 96
@@ -47,17 +47,24 @@ def tile_feedforward_pa_k_kernel(
     scales_in = (w1_scales, w3_scales)
     lora_inputs = ((xa1, lora_B1), (xa3, lora_B3))
 
-    sheets = [[(r, t), (r + 1, t)] for r in range(0, LONG_ROUNDS, 2) for t in range(TILES)]
-    sheets += [[(r, t) for t in range(TILES)] for r in range(LONG_ROUNDS, ROUNDS)]
+    whole, first_pair, second_pair = (0, ROUND), (0, ROUND // 2), (ROUND // 2, ROUND)
+    sheets = [[(r, t, whole), (r + 1, t, whole)] for r in range(0, LONG_ROUNDS, 2) for t in range(TILES)]
+    sheets += [[(r, t, whole) for t in range(TILES)] for r in range(LONG_ROUNDS, ROUNDS - 1)]
+    sheets += [[(ROUNDS - 1, t, part) for t in range(TILES)] for part in (first_pair, second_pair)]
     sheet_before = {2 * (s - HEAD_SHEETS) + 1: s for s in range(HEAD_SHEETS, len(sheets))}
+    parts = [
+        [(r, whole) for r in range(ROUNDS - 1)] + [(ROUNDS - 1, first_pair), (ROUNDS - 1, second_pair)],
+        [(r, whole) for r in range(ROUNDS)],
+    ]
     steps = []
     ready = sheets[0] + sheets[1]
     taken = [0, 0]
-    for index in range(2 * ROUNDS):
+    for index in range(len(parts[0]) + len(parts[1])):
         if index - 1 in sheet_before:
             ready = ready + sheets[sheet_before[index - 1]]
-        w = 0 if all((taken[0], t) in ready for t in range(TILES)) else 1
-        steps.append((w, taken[w]))
+        waiting = parts[0][taken[0] : taken[0] + 1]
+        w = 0 if any(all((r, t, part) in ready for t in range(TILES)) for r, part in waiting) else 1
+        steps.append((w,) + parts[w][taken[w]])
         taken[w] += 1
     last = len(steps) - 1
 
@@ -110,28 +117,20 @@ def tile_feedforward_pa_k_kernel(
                     ),
                 )
 
-        def pieces(r, t):
-            count = 2 if (r, t) == (ROUNDS - 1, TILES - 1) else ROUND
-            return [slice(g, g + count) for g in range(0, ROUND, count)]
-
         def load_sheet(s):
             sheet = x_pool.tile([P, 2, ROUND * K_PASS], BF16, name="x_sheet", tag="x_sheet", align_bytes=4096)
             for i, unit in enumerate(sheets[s]):
-                x_raw[unit] = sheet[:, i, :]
-            (r, t), (r2, t2) = sheets[s]
+                x_raw[unit] = sheet[:, i, unit[2][0] * K_PASS : unit[2][1] * K_PASS]
+            (r, t, part), (r2, t2, part2) = sheets[s]
             if t == t2:
                 nc.sync.dma_start(
                     out=sheet[:].rearrange("s i k -> s (i k)"),
                     in_=x[t, :, r * ROUND * K_PASS : (r2 + 1) * ROUND * K_PASS],
                 )
             else:
-                for t in range(TILES):
-                    for piece in pieces(r, t):
-                        first = r * ROUND * K_PASS
-                        nc.sync.dma_start(
-                            out=sheet[:, t, piece.start * K_PASS : piece.stop * K_PASS],
-                            in_=x[t, :, first + piece.start * K_PASS : first + piece.stop * K_PASS],
-                        )
+                for unit in sheets[s]:
+                    cols = slice((r * ROUND + part[0]) * K_PASS, (r * ROUND + part[1]) * K_PASS)
+                    nc.sync.dma_start(out=x_raw[unit], in_=x[unit[1], :, cols])
 
         def load_lora(w):
             xa, lora_b = lora_inputs[w]
@@ -144,19 +143,19 @@ def tile_feedforward_pa_k_kernel(
         def load_step(index):
             if index in sheet_before:
                 load_sheet(sheet_before[index])
-                for w, r in steps[index : index + 2]:
-                    if r == HALF:
-                        spread(w, lower, slice(HALF, ROUNDS - LATE_ROUNDS * w))
-            w, r = steps[index]
-            if (w, r) == (1, ROUNDS - LATE_ROUNDS):
-                spread(w, lower, slice(r, ROUNDS))
-            left = len(steps) - index
-            count = 1 if left <= SINGLE_STEPS else 2 if left <= FINE_STEPS else ROUND
-            halves = 1 if count == ROUND else 2
+                if steps[index][0:2] == (1, HALF):
+                    spread(1, lower, slice(HALF, ROUNDS - LATE_ROUNDS))
+            if steps[index][0:2] == (1, ROUNDS - LATE_ROUNDS):
+                spread(1, lower, slice(ROUNDS - LATE_ROUNDS, ROUNDS))
+            w, r, part = steps[index]
+            left = sum(b - a for w2, r2, (a, b) in steps[index:])
+            count = 1 if left <= SINGLE_GROUPS else 2 if left <= FINE_GROUPS else ROUND
+            count = min(count, part[1] - part[0])
+            halves = 1 if count == part[1] - part[0] else 2
             tiles = [
                 words_pool.tile([P, ROUND, F], U32, name="words", tag="words", align_bytes=4096) for h in range(halves)
             ]
-            for g in range(0, ROUND, count):
+            for g in range(part[0], part[1], count):
                 for j in range(g, g + count):
                     words[(index, j)] = tiles[g // count % halves]
                 nc.sync.dma_start(
@@ -175,52 +174,52 @@ def tile_feedforward_pa_k_kernel(
                     out=a2_plane[r:P:QUADRANT, :].bitcast(I32), in_=lora_A2_scales[0].bitcast(I32)[r::ROWS, :]
                 )
 
-        def sort_x(r, t):
-            x_sorted[(r, t)] = sorted_pool.tile([P, ROUND, 2, P], F32, name="x_sorted", tag="x_sorted")
-            pairs = x_raw[(r, t)].bitcast(F32).rearrange("s (g p u) -> s g u p", p=P, u=2)
-            for piece in pieces(r, t):
-                nc.vector.tensor_copy(out=x_sorted[(r, t)][:, piece, :, :], in_=pairs[:, piece, :, :])
+        def sort_x(unit):
+            x_sorted[unit] = sorted_pool.tile([P, ROUND, 2, P], F32, name="x_sorted", tag="x_sorted")
+            pairs = x_raw[unit].bitcast(F32).rearrange("s (g p u) -> s g u p", p=P, u=2)
+            nc.vector.tensor_copy(out=x_sorted[unit][:, unit[2][0] : unit[2][1], :, :], in_=pairs)
 
-        def turn_x(r, t):
+        def turn_x(unit):
+            r, t, part = unit
             grouped = grouped_pool.tile([P, ROUND, P, PACK], BF16, name="x_grouped", tag="x_grouped", align_bytes=64)
-            for bank, copy in enumerate((nc.scalar.copy, nc.vector.tensor_copy)):
+            for g in range(part[0], part[1], 2):
                 turned = turn_psum.tile([P, 2, 2, P], F32, name="x_turned", tag="turn")
                 for i in range(2):
                     for u in range(2):
-                        nc.tensor.transpose(
-                            turned[:, i, u, :], x_sorted[(r, t)][:, 2 * bank + i, u, :], identity_f32[:]
-                        )
-                copy(
-                    out=grouped[:].bitcast(F32)[:, 2 * bank : 2 * bank + 2, :, :],
-                    in_=turned[:].rearrange("p g u s -> p g s u"),
-                )
-            x_grouped[(r, t)] = grouped
+                        nc.tensor.transpose(turned[:, i, u, :], x_sorted[unit][:, g + i, u, :], identity_f32[:])
+                on_vector = t == 1 if part != whole else g > 0
+                copy = nc.vector.tensor_copy if on_vector else nc.scalar.copy
+                copy(out=grouped[:].bitcast(F32)[:, g : g + 2, :, :], in_=turned[:].rearrange("p g u s -> p g s u"))
+            x_grouped[unit] = grouped
 
-        def quantise_x(r, t):
-            x_codes[(r, t)] = codes_pool.tile([P, ROUND, P], U32, name="x_codes", tag="x_codes", align_bytes=256)
-            x_scales[(r, t)] = codes_pool.tile([P, ROUND, P], U8, name="x_scales", tag="x_scales", align_bytes=256)
+        def quantise_x(unit):
+            r, t, (a, b) = unit
+            codes = codes_pool.tile([P, ROUND, P], U32, name="x_codes", tag="x_codes", align_bytes=256)
+            scales = codes_pool.tile([P, ROUND, P], U8, name="x_scales", tag="x_scales", align_bytes=256)
+            for j in range(a, b):
+                x_codes[(r, t, j)], x_scales[(r, t, j)] = codes, scales
             nc.vector.quantize_mx(
-                out=x_codes[(r, t)][:].rearrange("p g s -> p (g s)").bitcast(FP8X4),
-                scales=x_scales[(r, t)][:].rearrange("p g s -> p (g s)"),
-                in_=x_grouped[(r, t)][:].rearrange("p g s t -> p (g s t)"),
+                out=codes[:, a:b, :].rearrange("p g s -> p (g s)").bitcast(FP8X4),
+                scales=scales[:, a:b, :].rearrange("p g s -> p (g s)"),
+                in_=x_grouped[unit][:, a:b, :, :].rearrange("p g s t -> p (g s t)"),
             )
 
         def prepare_sheet(s):
             for unit in sheets[s]:
-                sort_x(*unit)
+                sort_x(unit)
             for unit in sheets[s]:
-                turn_x(*unit)
-                quantise_x(*unit)
+                turn_x(unit)
+                quantise_x(unit)
 
         def multiply(index):
-            w, r = steps[index]
-            for pair in range(0, ROUND, 2):
+            w, r, part = steps[index]
+            for pair in range(part[0], part[1], 2):
                 for t in range(TILES):
                     for j in range(pair, pair + 2):
                         nc.tensor.matmul_mx(
                             out=acc[w][t][:],
-                            lhsT=x_codes[(r, t)][:, j, :].bitcast(FP8X4),
-                            lhsT_scale=x_scales[(r, t)][:, j, :],
+                            lhsT=x_codes[(r, t, j)][:, j, :].bitcast(FP8X4),
+                            lhsT_scale=x_scales[(r, t, j)][:, j, :],
                             rhs=words[(index, j)][:, j, :].bitcast(FP8X4),
                             rhs_scale=planes[w][ROWS * j : P, r, :],
                             start=(r == 0 and j == 0),
@@ -274,8 +273,8 @@ def tile_feedforward_pa_k_kernel(
         load_step(0)
         for w in range(2):
             spread(w, upper, slice(0, ROUNDS))
-        for w in range(2):
-            spread(w, lower, slice(0, HALF))
+        spread(0, lower, slice(0, ROUNDS))
+        spread(1, lower, slice(0, HALF))
         load_step(1)
 
         prepare_sheet(0)
@@ -291,15 +290,18 @@ def tile_feedforward_pa_k_kernel(
             if index in sheet_before:
                 prepare_sheet(sheet_before[index])
             multiply(index)
-            if steps[index] == (0, ROUNDS - 1):
+            if steps[index] == (0, ROUNDS - 1, second_pair):
                 make_gate()
 
         gated_sum, g_grouped, products = {}, {}, {}
         for t in range(TILES):
             gated_sum[t] = keep.tile([P, PACK, P], F32, name="gated_sum_%d" % t)
-            nc.vector.tensor_mul(
-                out=gated_sum[t][:], in0=acc[1][t][:].rearrange("s (p t) -> s t p", t=PACK), in1=gate[t][:]
-            )
+            for half in (slice(0, PACK // 2), slice(PACK // 2, PACK)):
+                nc.vector.tensor_mul(
+                    out=gated_sum[t][:, half, :],
+                    in0=acc[1][t][:].rearrange("s (p t) -> s t p", t=PACK)[:, half, :],
+                    in1=gate[t][:, half, :],
+                )
         for t in range(TILES):
             g_turned = turn_psum.tile([P, PACK, P], F32, name="g_turned", tag="turn")
             for i, term in enumerate((gated_lora[t], gated_sum[t])):

@@ -79,10 +79,6 @@ def tile_feedforward_pa_k_kernel(
         acc_psum = ctx.enter_context(tc.psum_pool(name="acc_psum", bufs=1))
         ctx.enter_context(tc.manual_schedule())
 
-        table_in = keep.tile([P, 1], F32, name="table_in")
-        table_out = keep.tile([P, 1], F32, name="table_out")
-        nc.vector.memset(table_in[:], 0.0)
-        nc.scalar.activation(out=table_out[:], in_=table_in[:], func=SILU)
         staged = keep.tile([P, ROWS, ROUNDS, F // 4], I32, name="staged", align_bytes=2048)
         planes = []
         for w in range(2):

from contextlib import ExitStack

import concourse.mybir as mybir
from concourse.masks import make_identity

F32 = mybir.dt.float32
BF16 = mybir.dt.bfloat16
I32 = mybir.dt.int32
U32 = mybir.dt.uint32
U8 = mybir.dt.uint8
FP8X4 = mybir.dt.float8_e4m3fn_x4
SILU = mybir.ActivationFunctionType.Silu

P = 128
TILES = 2
D = 16384
F = 512
R = 128
LORA_SCALING = 2.0
PACK = 4
K_PASS = P * PACK
GROUPS = D // K_PASS
QUADRANT = 32
QUADRANTS = P // QUADRANT
ROWS = 4
ROUND = 4
ROUNDS = GROUPS // ROUND
HALF = ROUNDS // 2
LONG_ROUNDS = 6
HEAD_SHEETS = 2
SINGLE_GROUPS = 8
FINE_GROUPS = 28
LATE_ROUNDS = 2
STAGE_FIRST = 32
STAGE_END = 96
STAGE_STEP = 4
LORA_BLOCKS = TILES + F // P

FLOPS = 2 * TILES * P * (2 * D * F + 2 * R * F + F * R)


def tile_feedforward_pa_k_kernel(
    tc, x, w1_words, w1_scales, w3_words, w3_scales, xa1, xa3, lora_B1, lora_B3, lora_A2_words, lora_A2_scales, out_0, out_1
):
    nc = tc.nc
    words_in = (w1_words, w3_words)
    scales_in = (w1_scales, w3_scales)
    lora_inputs = ((xa1, lora_B1), (xa3, lora_B3))

    whole, first_pair, second_pair = (0, ROUND), (0, ROUND // 2), (ROUND // 2, ROUND)
    sheets = [[(r, t, whole), (r + 1, t, whole)] for r in range(0, LONG_ROUNDS, 2) for t in range(TILES)]
    sheets += [[(r, t, whole) for t in range(TILES)] for r in range(LONG_ROUNDS, ROUNDS - 1)]
    sheets += [[(ROUNDS - 1, t, part) for t in range(TILES)] for part in (first_pair, second_pair)]
    sheet_before = {2 * (s - HEAD_SHEETS) + 1: s for s in range(HEAD_SHEETS, len(sheets))}
    parts = [
        [(r, whole) for r in range(ROUNDS - 1)] + [(ROUNDS - 1, first_pair), (ROUNDS - 1, second_pair)],
        [(r, whole) for r in range(ROUNDS)],
    ]
    steps = []
    ready = sheets[0] + sheets[1]
    taken = [0, 0]
    for index in range(len(parts[0]) + len(parts[1])):
        if index - 1 in sheet_before:
            ready = ready + sheets[sheet_before[index - 1]]
        waiting = parts[0][taken[0] : taken[0] + 1]
        w = 0 if any(all((r, t, part) in ready for t in range(TILES)) for r, part in waiting) else 1
        steps.append((w,) + parts[w][taken[w]])
        taken[w] += 1
    last = len(steps) - 1

    with ExitStack() as ctx:
        words_pool = ctx.enter_context(tc.tile_pool(name="words_pool", bufs=8))
        sorted_pool = ctx.enter_context(tc.tile_pool(name="sorted_pool", bufs=3))
        codes_pool = ctx.enter_context(tc.tile_pool(name="codes_pool", bufs=12))
        grouped_pool = ctx.enter_context(tc.tile_pool(name="grouped_pool", bufs=3))
        keep = ctx.enter_context(tc.tile_pool(name="keep", bufs=1))
        x_pool = ctx.enter_context(tc.tile_pool(name="x_pool", bufs=3))
        turn_psum = ctx.enter_context(tc.psum_pool(name="turn_psum", bufs=4))
        acc_psum = ctx.enter_context(tc.psum_pool(name="acc_psum", bufs=1))
        ctx.enter_context(tc.manual_schedule())

        staged = keep.tile([P, ROWS, ROUNDS, F // 4], I32, name="staged", align_bytes=2048)
        planes = []
        for w in range(2):
            planes.append(keep.tile([P, ROUNDS, F], U8, name="planes_%d" % w, align_bytes=2048))
            nc.vector.memset(planes[w][:].bitcast(I32), 0)
        a2_words = keep.tile([P, R], U32, name="a2_words", align_bytes=256)
        a2_plane = keep.tile([P, R], U8, name="a2_plane", align_bytes=64)
        nc.vector.memset(a2_plane[:].bitcast(I32), 0)
        identity_f32 = keep.tile([P, P], F32, name="identity_f32")
        make_identity(nc, identity_f32[:])
        identity_bf16 = keep.tile([P, P], BF16, name="identity_bf16")
        make_identity(nc, identity_bf16[:])
        acc = [[acc_psum.tile([P, F], F32, name="acc_%d_%d" % (w, t)) for t in range(TILES)] for w in range(2)]

        x_raw, x_sorted, x_grouped, x_codes, x_scales, words = {}, {}, {}, {}, {}, {}
        lora_in, lora_turned, lora_term, gate, gated_lora = {}, {}, {}, {}, {}

        def stage(w):
            rows = scales_in[w].bitcast(I32).rearrange("(c j) (q r) n -> r (j q) c n", j=ROUND, r=ROWS)
            for r in range(ROWS):
                nc.sync.dma_start(out=staged[STAGE_FIRST + w : STAGE_END : STAGE_STEP, r, :, :], in_=rows[r])

        def spread(w, quadrants, rounds):
            for q in quadrants:
                first = STAGE_FIRST + w + STAGE_STEP * q
                nc.sync.dma_start(
                    out=planes[w][QUADRANT * q : QUADRANT * q + ROUND * ROWS, rounds, :]
                    .rearrange("p c n -> p (c n)")
                    .bitcast(I32),
                    in_=staged[first : STAGE_END : STAGE_STEP * QUADRANTS, :, rounds, :].rearrange(
                        "j r c n -> j r (c n)"
                    ),
                )

        def load_sheet(s):
            sheet = x_pool.tile([P, 2, ROUND * K_PASS], BF16, name="x_sheet", tag="x_sheet", align_bytes=4096)
            for i, unit in enumerate(sheets[s]):
                x_raw[unit] = sheet[:, i, unit[2][0] * K_PASS : unit[2][1] * K_PASS]
            (r, t, part), (r2, t2, part2) = sheets[s]
            if t == t2:
                nc.sync.dma_start(
                    out=sheet[:].rearrange("s i k -> s (i k)"),
                    in_=x[t, :, r * ROUND * K_PASS : (r2 + 1) * ROUND * K_PASS],
                )
            else:
                for unit in sheets[s]:
                    cols = slice((r * ROUND + part[0]) * K_PASS, (r * ROUND + part[1]) * K_PASS)
                    nc.sync.dma_start(out=x_raw[unit], in_=x[unit[1], :, cols])

        def load_lora(w):
            xa, lora_b = lora_inputs[w]
            lora_in[w] = keep.tile([P, LORA_BLOCKS, R], BF16, name="lora_in_%d" % w, align_bytes=256)
            nc.sync.dma_start(out=lora_in[w][:, 0:TILES, :], in_=xa.rearrange("b (q i) r -> (b q) i r", i=TILES))
            nc.sync.dma_start(out=lora_in[w][:, TILES:, :], in_=lora_b.rearrange("(p t) r -> p t r", t=PACK))

        lower, upper = range(QUADRANTS // 2), range(QUADRANTS // 2, QUADRANTS)

        def load_step(index):
            if index in sheet_before:
                load_sheet(sheet_before[index])
                if steps[index][0:2] == (1, HALF):
                    spread(1, lower, slice(HALF, ROUNDS - LATE_ROUNDS))
            if steps[index][0:2] == (1, ROUNDS - LATE_ROUNDS):
                spread(1, lower, slice(ROUNDS - LATE_ROUNDS, ROUNDS))
            w, r, part = steps[index]
            left = sum(b - a for w2, r2, (a, b) in steps[index:])
            count = 1 if left <= SINGLE_GROUPS else 2 if left <= FINE_GROUPS else ROUND
            count = min(count, part[1] - part[0])
            halves = 1 if count == part[1] - part[0] else 2
            tiles = [
                words_pool.tile([P, ROUND, F], U32, name="words", tag="words", align_bytes=4096) for h in range(halves)
            ]
            for g in range(part[0], part[1], count):
                for j in range(g, g + count):
                    words[(index, j)] = tiles[g // count % halves]
                nc.sync.dma_start(
                    out=words[(index, g)][:, g : g + count, :].bitcast(I32),
                    in_=words_in[w][r * ROUND + g : r * ROUND + g + count]
                    .rearrange("g p n t -> p g (n t)")
                    .bitcast(I32),
                )

        def load_a2():
            nc.sync.dma_start(
                out=a2_words[:].bitcast(I32), in_=lora_A2_words[0].rearrange("p n t -> p (n t)").bitcast(I32)
            )
            for r in range(ROWS):
                nc.sync.dma_start(
                    out=a2_plane[r:P:QUADRANT, :].bitcast(I32), in_=lora_A2_scales[0].bitcast(I32)[r::ROWS, :]
                )

        def sort_x(unit):
            x_sorted[unit] = sorted_pool.tile([P, ROUND, 2, P], F32, name="x_sorted", tag="x_sorted")
            pairs = x_raw[unit].bitcast(F32).rearrange("s (g p u) -> s g u p", p=P, u=2)
            nc.vector.tensor_copy(out=x_sorted[unit][:, unit[2][0] : unit[2][1], :, :], in_=pairs)

        def turn_x(unit):
            r, t, part = unit
            grouped = grouped_pool.tile([P, ROUND, P, PACK], BF16, name="x_grouped", tag="x_grouped", align_bytes=64)
            for g in range(part[0], part[1], 2):
                turned = turn_psum.tile([P, 2, 2, P], F32, name="x_turned", tag="turn")
                for i in range(2):
                    for u in range(2):
                        nc.tensor.transpose(turned[:, i, u, :], x_sorted[unit][:, g + i, u, :], identity_f32[:])
                on_vector = t == 1 if part != whole else g > 0
                copy = nc.vector.tensor_copy if on_vector else nc.scalar.copy
                copy(out=grouped[:].bitcast(F32)[:, g : g + 2, :, :], in_=turned[:].rearrange("p g u s -> p g s u"))
            x_grouped[unit] = grouped

        def quantise_x(unit):
            r, t, (a, b) = unit
            codes = codes_pool.tile([P, ROUND, P], U32, name="x_codes", tag="x_codes", align_bytes=256)
            scales = codes_pool.tile([P, ROUND, P], U8, name="x_scales", tag="x_scales", align_bytes=256)
            for j in range(a, b):
                x_codes[(r, t, j)], x_scales[(r, t, j)] = codes, scales
            nc.vector.quantize_mx(
                out=codes[:, a:b, :].rearrange("p g s -> p (g s)").bitcast(FP8X4),
                scales=scales[:, a:b, :].rearrange("p g s -> p (g s)"),
                in_=x_grouped[unit][:, a:b, :, :].rearrange("p g s t -> p (g s t)"),
            )

        def prepare_sheet(s):
            for unit in sheets[s]:
                sort_x(unit)
            for unit in sheets[s]:
                turn_x(unit)
                quantise_x(unit)

        def multiply(index):
            w, r, part = steps[index]
            for pair in range(part[0], part[1], 2):
                for t in range(TILES):
                    for j in range(pair, pair + 2):
                        nc.tensor.matmul_mx(
                            out=acc[w][t][:],
                            lhsT=x_codes[(r, t, j)][:, j, :].bitcast(FP8X4),
                            lhsT_scale=x_scales[(r, t, j)][:, j, :],
                            rhs=words[(index, j)][:, j, :].bitcast(FP8X4),
                            rhs_scale=planes[w][ROWS * j : P, r, :],
                            start=(r == 0 and j == 0),
                            stop=(r == ROUNDS - 1 and j == ROUND - 1),
                        )

        def turn_lora():
            for w in range(2):
                turned = turn_psum.tile([P, LORA_BLOCKS, P], BF16, name="lora_psum", tag="turn")
                for i in range(LORA_BLOCKS):
                    nc.tensor.transpose(turned[:, i, :], lora_in[w][:, i, :], identity_bf16[:])
                lora_turned[w] = keep.tile([P, LORA_BLOCKS, P], BF16, name="lora_turned_%d" % w)
                nc.scalar.copy(
                    out=lora_turned[w][:, 0:TILES, :].rearrange("r b (q i) -> r (b q) i", i=TILES),
                    in_=turned[:, 0:TILES, :].rearrange("r i p -> r p i"),
                )
                nc.scalar.copy(out=lora_turned[w][:, TILES:, :], in_=turned[:, TILES:, :])

        def multiply_lora():
            for w in range(2):
                for t in range(TILES):
                    product = turn_psum.tile([P, PACK, P], F32, name="lora_product", tag="turn")
                    nc.tensor.matmul(
                        out=product[:].rearrange("s t p -> s (t p)"),
                        lhsT=lora_turned[w][:, t, :],
                        rhs=lora_turned[w][:, TILES:, :].rearrange("r t p -> r (t p)"),
                        start=True,
                        stop=True,
                    )
                    lora_term[(w, t)] = keep.tile([P, PACK, P], F32, name="lora_term_%d_%d" % (w, t))
                    nc.scalar.mul(out=lora_term[(w, t)][:], in_=product[:], mul=LORA_SCALING)

        def make_gate():
            for t in range(TILES):
                h1 = keep.tile([P, PACK, P], F32, name="h1_%d" % t)
                nc.vector.tensor_add(
                    out=h1[:], in0=acc[0][t][:].rearrange("s (p t) -> s t p", t=PACK), in1=lora_term[(0, t)][:]
                )
                gate[t] = keep.tile([P, PACK, P], F32, name="gate_%d" % t)
                nc.scalar.activation(out=gate[t][:], in_=h1[:], func=SILU)
            for t in range(TILES):
                gated_lora[t] = keep.tile([P, PACK, P], F32, name="gated_lora_%d" % t)
                nc.vector.tensor_mul(out=gated_lora[t][:], in0=gate[t][:], in1=lora_term[(1, t)][:])

        load_sheet(0)
        stage(0)
        load_lora(0)
        load_sheet(1)
        stage(1)
        load_lora(1)
        load_step(0)
        for w in range(2):
            spread(w, upper, slice(0, ROUNDS))
        spread(0, lower, slice(0, ROUNDS))
        spread(1, lower, slice(0, HALF))
        load_step(1)

        prepare_sheet(0)
        prepare_sheet(1)
        turn_lora()
        multiply_lora()

        for index in range(len(steps)):
            if index + 2 <= last:
                load_step(index + 2)
            elif index + 2 == last + 1:
                load_a2()
            if index in sheet_before:
                prepare_sheet(sheet_before[index])
            multiply(index)
            if steps[index] == (0, ROUNDS - 1, second_pair):
                make_gate()

        gated_sum, g_grouped, products = {}, {}, {}
        for t in range(TILES):
            gated_sum[t] = keep.tile([P, PACK, P], F32, name="gated_sum_%d" % t)
            for half in (slice(0, PACK // 2), slice(PACK // 2, PACK)):
                nc.vector.tensor_mul(
                    out=gated_sum[t][:, half, :],
                    in0=acc[1][t][:].rearrange("s (p t) -> s t p", t=PACK)[:, half, :],
                    in1=gate[t][:, half, :],
                )
        for t in range(TILES):
            g_turned = turn_psum.tile([P, PACK, P], F32, name="g_turned", tag="turn")
            for i, term in enumerate((gated_lora[t], gated_sum[t])):
                for s in range(PACK):
                    nc.tensor.matmul(
                        out=g_turned[:, s, :],
                        lhsT=term[:, s, :],
                        rhs=identity_f32[:],
                        start=(i == 0 and s == 0),
                        stop=(i == 1 and s == PACK - 1),
                        is_transpose=True,
                    )
            g_grouped[t] = keep.tile([P, P, PACK], BF16, name="g_grouped_%d" % t, align_bytes=64)
            nc.scalar.copy(out=g_grouped[t][:], in_=g_turned[:].rearrange("p t s -> p s t"))
        for t in range(TILES):
            g = keep.tile([P, F], F32, name="g_%d" % t, align_bytes=256)
            nc.vector.tensor_add(
                out=g[:].rearrange("s (p t) -> s p t", t=PACK),
                in0=gated_sum[t][:].rearrange("s t p -> s p t"),
                in1=gated_lora[t][:].rearrange("s t p -> s p t"),
            )
            nc.scalar.dma_start(out=out_0[t], in_=g[:])
        for t in range(TILES):
            g_codes = keep.tile([P, P], U32, name="g_codes_%d" % t, align_bytes=64)
            g_scales = keep.tile([P, P], U8, name="g_scales_%d" % t, align_bytes=64)
            nc.vector.quantize_mx(
                out=g_codes[:].bitcast(FP8X4), scales=g_scales[:], in_=g_grouped[t][:].rearrange("p s t -> p (s t)")
            )
            ga2_psum = turn_psum.tile([P, R], F32, name="ga2_psum", tag="turn")
            nc.tensor.matmul_mx(
                out=ga2_psum[:],
                lhsT=g_codes[:].bitcast(FP8X4),
                lhsT_scale=g_scales[:],
                rhs=a2_words[:].bitcast(FP8X4),
                rhs_scale=a2_plane[:],
                start=True,
                stop=True,
            )
            products[t] = ga2_psum
        for t in range(TILES):
            ga2 = keep.tile([P, R], F32, name="ga2_%d" % t, align_bytes=256)
            nc.vector.tensor_copy(out=ga2[:], in_=products[t][:])
            nc.sync.dma_start(out=out_1[t], in_=ga2[:])
